import numpy as np
import ml_dtypes


def mxq(x, axis, fmt="e4m3"):
    dtype, down = {"e4m3": (ml_dtypes.float8_e4m3fn, 7), "e5m2": (ml_dtypes.float8_e5m2, 14)}[fmt]
    v = np.moveaxis(np.asarray(x, np.float32).astype(ml_dtypes.bfloat16).astype(np.float64), axis, -1)
    blocks = v.reshape(v.shape[:-1] + (-1, 32))
    amax = np.abs(blocks).max(-1, keepdims=True)
    byte = np.maximum(np.where(amax > 0, np.frexp(amax)[1] - 1 + 127, 0) - down, 1)
    scale = np.exp2(byte - 127.0)
    codes = (blocks / scale).astype(np.float32).astype(dtype).astype(np.float64)
    return np.moveaxis((codes * scale).reshape(v.shape), -1, axis)


WIDE = False


def mx_kscale(k):
    if not WIDE:
        return np.ones(k)
    levels = np.array([10, -10, 5, -5, 0])
    a = np.random.permutation(np.resize(levels, k // 512 * 4)).reshape(k // 512, 4)
    idx = np.arange(k)
    return np.exp2(a[idx // 512, idx % 128 // 32])


BF16 = ml_dtypes.bfloat16


def bf(x):
    return np.asarray(x, np.float32).astype(BF16)


def f64(x):
    return np.asarray(x).astype(np.float64)


B, I, O, G = 8192, 128, 256, 5
DEGREE = 3
NB = G + DEGREE
GRID_MIN, GRID_MAX = -1.0, 1.0
EPS = 1e-8
BLK = 32


def extended_grid():
    h = (GRID_MAX - GRID_MIN) / G
    return GRID_MIN + h * f64(np.arange(-DEGREE, G + DEGREE + 1))


def bspline_basis(x):
    t = extended_grid()
    G0 = G + 2 * DEGREE
    xe = x[..., None]
    basis = ((xe >= t[:-1]) & (xe < t[1:])).astype(np.float64)
    for k in range(1, DEGREE + 1):
        cnt = G0 - k
        left_den = t[k:k + cnt] - t[:cnt]
        right_den = t[k + 1:k + 1 + cnt] - t[1:1 + cnt]
        left_term = np.where(left_den > EPS, (xe - t[:cnt]) / np.where(left_den > EPS, left_den, 1.0), 0.0)
        right_term = np.where(right_den > EPS, (t[k + 1:k + 1 + cnt] - xe) / np.where(right_den > EPS, right_den, 1.0), 0.0)
        basis = left_term * basis[..., :-1] + right_term * basis[..., 1:]
    return basis


def setup_inputs():
    s = mx_kscale(I * NB)
    e = np.repeat(s[::BLK], BLK)
    hot = (e > np.sqrt(e.max() * e.min())).reshape(I, NB)
    huge = e.max() / e.min()
    park = hot.any(axis=1)
    x = np.random.standard_normal((B, I))
    x = np.where(park[None, :], 1.0 + np.abs(x), x)
    dead = (np.arange(NB) < G)[None, :]
    f = np.where(hot & dead, huge, np.where(hot, 0.0, 1.0))
    return {"x": bf(x),
            "spline_coeffs": bf(np.random.standard_normal((O, I, NB)) * 2.0 / np.sqrt(I) * f[None]),
            "residual_weight": bf(np.random.standard_normal((O, I)) / np.sqrt(I)),
            "residual_bias": bf(np.random.standard_normal(O) * 0.3),
            "scale_base": bf(np.random.uniform(0.5, 1.5, (O, 1)) + 0.3 * np.random.standard_normal((O, I)))}


def reference(x, spline_coeffs, residual_weight, residual_bias, scale_base):
    x = f64(x)
    x_clamped = np.clip(x, GRID_MIN, GRID_MAX)
    basis = bspline_basis(x_clamped)
    spline_out = mxq(basis.reshape(B, I * NB), 1, "e4m3") @ mxq(f64(spline_coeffs).reshape(O, I * NB), 1, "e4m3").T
    residual_out = x @ f64(residual_weight).T + f64(residual_bias)
    scale = np.mean(f64(scale_base), axis=1)
    return spline_out * scale + residual_out

@@ -1,0 +1,201 @@
+import math
+from contextlib import ExitStack
+
+import concourse.mybir as mybir
+from concourse.masks import make_identity
+
+F32 = mybir.dt.float32
+BF16 = mybir.dt.bfloat16
+U32 = mybir.dt.uint32
+U8 = mybir.dt.uint8
+FP8X4 = mybir.dt.float8_e4m3fn_x4
+ALU = mybir.AluOpType
+ACT = mybir.ActivationFunctionType
+
+P = 128
+B, I, O, NBAS = 8192, 128, 256, 8
+NT = B // P
+CH = 8
+F = CH * P
+NCH = NT // CH
+HALF = 512
+ACT_REGROUP = (1, 3)
+FLOPS = 2 * B * I * NBAS * O + 2 * B * I * O
+
+
+def tile_bsplinebasis_v2_t_kernel(tc, x, spline_coeffs, residual_weight, residual_bias, scale_base, out):
+    nc = tc.nc
+    r6 = 1.0 / math.sqrt(6.0)
+    with ExitStack() as ctx:
+        const = ctx.enter_context(tc.tile_pool(name="const", bufs=1))
+        setup = ctx.enter_context(tc.tile_pool(name="setup", bufs=1))
+        ew = ctx.enter_context(tc.tile_pool(name="ew", bufs=2))
+        be = ctx.enter_context(tc.tile_pool(name="be", bufs=2))
+        psum = ctx.enter_context(tc.psum_pool(name="psum", bufs=2))
+
+        ident_b = const.tile([P, P], BF16)
+        make_identity(nc, ident_b[:])
+        ident_f = const.tile([P, P], F32)
+        make_identity(nc, ident_f[:])
+
+        x_sb = const.tile([P, NT, I], BF16)
+        xT = const.tile([P, NT, P], BF16)
+        x_v = x.rearrange("(p n) i -> p n i", n=NT)
+        out_v = out.rearrange("(p n) o -> p n o", n=NT)
+        for c in range(NCH):
+            nc.sync.dma_start(out=x_sb[:, c * CH:(c + 1) * CH, :], in_=x_v[:, c * CH:(c + 1) * CH, :])
+
+        c_sb = setup.tile([P, 2, I * NBAS], BF16)
+        nc.scalar.dma_start(out=c_sb[:], in_=spline_coeffs.rearrange("(h p) i j -> p h (i j)", p=P))
+        rw_sb = setup.tile([P, 2, I], BF16)
+        nc.scalar.dma_start(out=rw_sb[:], in_=residual_weight.rearrange("(h p) i -> p h i", p=P))
+        sb_sb = setup.tile([P, 2, I], BF16)
+        nc.scalar.dma_start(out=sb_sb[:], in_=scale_base.rearrange("(h p) i -> p h i", p=P))
+        b_sb = setup.tile([P, P], BF16)
+        nc.vector.memset(b_sb[:], 0.0)
+        nc.scalar.dma_start(out=b_sb[0:2, :], in_=residual_bias.rearrange("(h p) -> h p", p=P))
+
+        cpl = setup.tile([P, 2, NBAS, I], BF16)
+        for h in range(2):
+            for j in range(NBAS):
+                nc.vector.tensor_copy(
+                    out=cpl[:, h, j, :].rearrange("p (c a m e) -> p c a m e", c=2, a=4, m=4, e=4),
+                    in_=c_sb[:, h, :].rearrange("p (c m a e j) -> p j c a m e", c=2, m=4, a=4, e=4, j=NBAS)[:, j],
+                )
+        cgr = setup.tile([P, 2, 4 * O], BF16, align_bytes=64)
+        ccodes = const.tile([P, 2, O], U32, align_bytes=64)
+        cscales = const.tile([P, 2, O], U8, align_bytes=64)
+        for h in range(2):
+            tpc = psum.tile([P, NBAS, P], BF16, tag="tp")
+            for j in range(NBAS):
+                nc.tensor.transpose(tpc[:, j, :], cpl[:, h, j, :], ident_b[:])
+            nc.vector.tensor_copy(
+                out=cgr[:, :, h * 512:(h + 1) * 512].rearrange("p g (w t) -> p g w t", t=4),
+                in_=tpc[:].rearrange("p (g t) w -> p g w t", t=4),
+            )
+        for g in range(2):
+            nc.vector.quantize_mx(out=ccodes[:, g, :].bitcast(FP8X4), scales=cscales[:, g, :], in_=cgr[:, g, :])
+
+        rwp = setup.tile([P, 2, I], BF16)
+        nc.vector.tensor_copy(
+            out=rwp[:].rearrange("p h (c a m e) -> p (h c) a m e", c=2, a=4, m=4, e=4),
+            in_=rw_sb[:].rearrange("p h (c m a e) -> p (h c) a m e", c=2, m=4, a=4, e=4),
+        )
+        tpr = psum.tile([P, 3, P], BF16, tag="tp")
+        for h in range(2):
+            nc.tensor.transpose(tpr[:, h, :], rwp[:, h, :], ident_b[:])
+        nc.tensor.transpose(tpr[:, 2, :], b_sb[:], ident_b[:])
+        rwT = const.tile([P, 2, P], BF16)
+        nc.vector.tensor_copy(out=rwT[:], in_=tpr[:, 0:2, :])
+        bias = const.tile([P, 2], F32)
+        nc.vector.tensor_copy(out=bias[:], in_=tpr[:, 2, 0:2])
+        ssum = setup.tile([P, 2], F32)
+        nc.vector.tensor_reduce(out=ssum[:], in_=sb_sb[:], axis=mybir.AxisListType.X, op=ALU.add)
+        scale = const.tile([P, 2], F32)
+        nc.vector.tensor_scalar(out=scale[:], in0=ssum[:], scalar1=1.0 / I, scalar2=None, op0=ALU.mult)
+
+        for c in range(NCH):
+            n0 = c * CH
+            xp = ew.tile([P, CH, I], BF16)
+            nc.vector.tensor_copy(
+                out=xp[:].rearrange("p n (c a m e) -> p (n c) a m e", c=2, a=4, m=4, e=4),
+                in_=x_sb[:, n0:n0 + CH, :].rearrange("p n (c m a e) -> p (n c) a m e", c=2, m=4, a=4, e=4),
+            )
+            tpx = psum.tile([P, CH, P], BF16, tag="tp")
+            for n in range(CH):
+                nc.tensor.transpose(tpx[:, n, :], xp[:, n, :], ident_b[:])
+            nc.scalar.copy(out=xT[:, n0:n0 + CH, :], in_=tpx[:])
+            xTc = xT[:, n0:n0 + CH, :].rearrange("p n w -> p (n w)")
+
+            u = ew.tile([P, F], BF16)
+            nc.vector.tensor_scalar(out=u[:], in0=xTc, scalar1=-1.0, scalar2=1.0, op0=ALU.max, op1=ALU.min)
+            a1 = ew.tile([P, F], F32)
+            nc.scalar.activation(out=a1[:], in_=u[:], func=ACT.Abs, bias=0.5, scale=2.5)
+            b1 = ew.tile([P, F], F32)
+            nc.scalar.activation(out=b1[:], in_=u[:], func=ACT.Abs, bias=-0.5, scale=2.5)
+            e = ew.tile([P, F], F32)
+            nc.scalar.activation(out=e[:], in_=a1[:], func=ACT.Abs, bias=-2.0, scale=1.0)
+            nc.scalar.activation(out=e[:], in_=e[:], func=ACT.Abs, bias=-1.0, scale=1.0)
+            d = ew.tile([P, F], F32)
+            nc.scalar.activation(out=d[:], in_=e[:], func=ACT.Identity, bias=1.0, scale=-1.0)
+            sqd = ew.tile([P, F], F32)
+            nc.scalar.activation(out=sqd[:], in_=d[:], func=ACT.Square, bias=0.0, scale=r6)
+            sqe = ew.tile([P, F], F32)
+            nc.scalar.activation(out=sqe[:], in_=e[:], func=ACT.Square, bias=0.0, scale=r6)
+
+            x3 = ew.tile([P, F], BF16)
+            nc.vector.tensor_tensor(out=x3[:], in0=sqd[:], in1=d[:], op=ALU.mult)
+            y3 = ew.tile([P, F], BF16)
+            nc.vector.tensor_tensor(out=y3[:], in0=sqe[:], in1=e[:], op=ALU.mult)
+            nc.vector.scalar_tensor_tensor(out=sqd[:], in0=sqd[:], scalar=1.0 / 6.0, in1=e[:], op0=ALU.subtract, op1=ALU.mult)
+            nc.vector.scalar_tensor_tensor(out=sqe[:], in0=sqe[:], scalar=1.0 / 6.0, in1=d[:], op0=ALU.subtract, op1=ALU.mult)
+            xi = ew.tile([P, F], BF16)
+            nc.vector.tensor_scalar(out=xi[:], in0=sqe[:], scalar1=3.0, scalar2=2.0 / 3.0, op0=ALU.mult, op1=ALU.add)
+            yi = ew.tile([P, F], BF16)
+            nc.vector.tensor_scalar(out=yi[:], in0=sqd[:], scalar1=3.0, scalar2=2.0 / 3.0, op0=ALU.mult, op1=ALU.add)
+
+            planes = ew.tile([P, NBAS, F], BF16)
+            vs = []
+            rzs = []
+            for t in range(4):
+                src = b1 if t % 2 == 0 else a1
+                v = ew.tile([P, F], BF16, tag="v%d" % t)
+                sgn = -1.0 if t in (0, 3) else 1.0
+                off = 7.0 / 6.0 if t in (0, 3) else -5.0 / 6.0
+                nc.scalar.activation(out=v[:], in_=src[:], func=ACT.Identity, bias=off, scale=sgn)
+                vs.append(v)
+            for t in range(4):
+                nc.vector.tensor_tensor(out=vs[t][:], in0=vs[t][:], in1=(yi if t % 2 == 0 else xi)[:], op=ALU.min)
+            for t in range(4):
+                rz = ew.tile([P, F], BF16, tag="rz%d" % t, bufs=1)
+                nc.vector.tensor_scalar(out=rz[:], in0=u[:], scalar1=0.4 * (t + 1) - 1.0, scalar2=0.0, op0=ALU.subtract, op1=ALU.max)
+                rzs.append(rz)
+            for t in range(4):
+                nc.vector.tensor_tensor(out=vs[t][:], in0=vs[t][:], in1=(y3 if t % 2 == 0 else x3)[:], op=ALU.max)
+            for t in range(4):
+                nc.vector.tensor_tensor(out=planes[:, t + 4, :], in0=vs[t][:], in1=rzs[t][:], op=ALU.min)
+            for t in range(4):
+                nc.vector.tensor_tensor(out=planes[:, t, :], in0=vs[t][:], in1=planes[:, t + 4, :], op=ALU.subtract)
+
+            for hf in range(F // HALF):
+                cols = slice(hf * HALF, (hf + 1) * HALF)
+                nh = n0 + hf * (HALF // P)
+                gr = be.tile([P, 2, 4 * HALF], BF16, align_bytes=64)
+                bcodes = be.tile([P, 2, HALF], U32, align_bytes=64)
+                bscales = be.tile([P, 2, HALF], U8, align_bytes=64)
+                for g in range(2):
+                    dst = gr[:, g, :].rearrange("p (c i t) -> p c t i", i=4, t=4)
+                    srcp = planes[:, 4 * g:4 * g + 4, cols].rearrange("p t (c i) -> p c t i", i=4)
+                    if (2 * hf + g) in ACT_REGROUP:
+                        nc.scalar.copy(out=dst, in_=srcp)
+                    else:
+                        nc.vector.tensor_copy(out=dst, in_=srcp)
+                for g in range(2):
+                    nc.vector.quantize_mx(out=bcodes[:, g, :].bitcast(FP8X4), scales=bscales[:, g, :], in_=gr[:, g, :])
+                t1s = []
+                for h in range(2):
+                    mx = psum.tile([P, HALF], F32, tag="mx")
+                    for g in range(2):
+                        nc.tensor.matmul_mx(
+                            out=mx[:],
+                            lhsT=ccodes[:, g, h * P:(h + 1) * P].bitcast(FP8X4),
+                            lhsT_scale=cscales[:, g, h * P:(h + 1) * P],
+                            rhs=bcodes[:, g, :].bitcast(FP8X4),
+                            rhs_scale=bscales[:, g, :],
+                            start=(g == 0),
+                            stop=(g == 1),
+                        )
+                    t1 = be.tile([P, HALF], F32, tag="t1_%d" % h)
+                    nc.scalar.activation(out=t1[:], in_=mx[:], func=ACT.Identity, bias=bias[:, h:h + 1], scale=scale[:, h:h + 1])
+                    t1s.append(t1)
+                osb = be.tile([P, 4, O], F32)
+                for k in range(2):
+                    ot = psum.tile([P, 2, O], F32, tag="ot", bufs=4)
+                    for q in range(2):
+                        n = 2 * k + q
+                        for h in range(2):
+                            dsto = ot[:, q, h * P:(h + 1) * P]
+                            nc.tensor.matmul(out=dsto, lhsT=xT[:, nh + n, :], rhs=rwT[:, h, :], start=True, stop=False)
+                            nc.tensor.matmul(out=dsto, lhsT=t1s[h][:, n * P:(n + 1) * P], rhs=ident_f[:], is_transpose=True, start=False, stop=True)
+                    nc.scalar.copy(out=osb[:, 2 * k:2 * k + 2, :], in_=ot[:])
+                nc.sync.dma_start(out=out_v[:, nh:nh + 4, :], in_=osb[:])

@@ -15,12 +15,19 @@ ACT = mybir.ActivationFunctionType
 P = 128
 B, I, O, NBAS = 8192, 128, 256, 8
 NT = B // P
-CH = 8
-F = CH * P
-NCH = NT // CH
-HALF = 512
-ACT_REGROUP = (1, 3)
+SIZES = [8] * 8
+NCH = len(SIZES)
+STARTS = [sum(SIZES[:c]) for c in range(NCH)]
+FMAX = max(SIZES) * P
+RT = 4
+TS = (3, 0, 1, 2)
+L_ON_V = ()
+D_ON_V = ()
+HI_ON_V = ()
+LO_ON_ACT = ()
+MANUAL = True
 FLOPS = 2 * B * I * NBAS * O + 2 * B * I * O
+assert sum(SIZES) == NT
 
 
 def tile_bsplinebasis_v2_t_kernel(tc, x, spline_coeffs, residual_weight, residual_bias, scale_base, out):
@@ -31,19 +38,21 @@ def tile_bsplinebasis_v2_t_kernel(tc, x, spline_coeffs, residual_weight, residua
         setup = ctx.enter_context(tc.tile_pool(name="setup", bufs=1))
         ew = ctx.enter_context(tc.tile_pool(name="ew", bufs=2))
         be = ctx.enter_context(tc.tile_pool(name="be", bufs=2))
-        psum = ctx.enter_context(tc.psum_pool(name="psum", bufs=2))
-
-        ident_b = const.tile([P, P], BF16)
-        make_identity(nc, ident_b[:])
-        ident_f = const.tile([P, P], F32)
-        make_identity(nc, ident_f[:])
+        psum = ctx.enter_context(tc.psum_pool(name="psum", bufs=1))
+        if MANUAL:
+            ctx.enter_context(tc.manual_schedule())
 
         x_sb = const.tile([P, NT, I], BF16)
         xT = const.tile([P, NT, P], BF16)
         x_v = x.rearrange("(p n) i -> p n i", n=NT)
         out_v = out.rearrange("(p n) o -> p n o", n=NT)
         for c in range(NCH):
-            nc.sync.dma_start(out=x_sb[:, c * CH:(c + 1) * CH, :], in_=x_v[:, c * CH:(c + 1) * CH, :])
+            nc.sync.dma_start(out=x_sb[:, STARTS[c]:STARTS[c] + SIZES[c], :], in_=x_v[:, STARTS[c]:STARTS[c] + SIZES[c], :])
+
+        ident_b = const.tile([P, P], BF16)
+        make_identity(nc, ident_b[:])
+        ident_f = const.tile([P, P], F32)
+        make_identity(nc, ident_f[:])
 
         c_sb = setup.tile([P, 2, I * NBAS], BF16)
         nc.scalar.dma_start(out=c_sb[:], in_=spline_coeffs.rearrange("(h p) i j -> p h (i j)", p=P))
@@ -52,129 +61,197 @@ def tile_bsplinebasis_v2_t_kernel(tc, x, spline_coeffs, residual_weight, residua
         sb_sb = setup.tile([P, 2, I], BF16)
         nc.scalar.dma_start(out=sb_sb[:], in_=scale_base.rearrange("(h p) i -> p h i", p=P))
         b_sb = setup.tile([P, P], BF16)
-        nc.vector.memset(b_sb[:], 0.0)
+        nc.gpsimd.memset(b_sb[:], 0.0)
         nc.scalar.dma_start(out=b_sb[0:2, :], in_=residual_bias.rearrange("(h p) -> h p", p=P))
 
         cpl = setup.tile([P, 2, NBAS, I], BF16)
         for h in range(2):
-            for j in range(NBAS):
-                nc.vector.tensor_copy(
-                    out=cpl[:, h, j, :].rearrange("p (c a m e) -> p c a m e", c=2, a=4, m=4, e=4),
+            for q in range(NBAS):
+                j = 4 * (q // 4) + TS[q % 4]
+                nc.gpsimd.tensor_copy(
+                    out=cpl[:, h, q, :].rearrange("p (c a m e) -> p c a m e", c=2, a=4, m=4, e=4),
                     in_=c_sb[:, h, :].rearrange("p (c m a e j) -> p j c a m e", c=2, m=4, a=4, e=4, j=NBAS)[:, j],
                 )
         cgr = setup.tile([P, 2, 4 * O], BF16, align_bytes=64)
         ccodes = const.tile([P, 2, O], U32, align_bytes=64)
         cscales = const.tile([P, 2, O], U8, align_bytes=64)
-        for h in range(2):
-            tpc = psum.tile([P, NBAS, P], BF16, tag="tp")
-            for j in range(NBAS):
-                nc.tensor.transpose(tpc[:, j, :], cpl[:, h, j, :], ident_b[:])
-            nc.vector.tensor_copy(
-                out=cgr[:, :, h * 512:(h + 1) * 512].rearrange("p g (w t) -> p g w t", t=4),
-                in_=tpc[:].rearrange("p (g t) w -> p g w t", t=4),
-            )
-        for g in range(2):
-            nc.vector.quantize_mx(out=ccodes[:, g, :].bitcast(FP8X4), scales=cscales[:, g, :], in_=cgr[:, g, :])
-
-        rwp = setup.tile([P, 2, I], BF16)
-        nc.vector.tensor_copy(
-            out=rwp[:].rearrange("p h (c a m e) -> p (h c) a m e", c=2, a=4, m=4, e=4),
-            in_=rw_sb[:].rearrange("p h (c m a e) -> p (h c) a m e", c=2, m=4, a=4, e=4),
-        )
-        tpr = psum.tile([P, 3, P], BF16, tag="tp")
-        for h in range(2):
-            nc.tensor.transpose(tpr[:, h, :], rwp[:, h, :], ident_b[:])
-        nc.tensor.transpose(tpr[:, 2, :], b_sb[:], ident_b[:])
         rwT = const.tile([P, 2, P], BF16)
-        nc.vector.tensor_copy(out=rwT[:], in_=tpr[:, 0:2, :])
         bias = const.tile([P, 2], F32)
-        nc.vector.tensor_copy(out=bias[:], in_=tpr[:, 2, 0:2])
-        ssum = setup.tile([P, 2], F32)
-        nc.vector.tensor_reduce(out=ssum[:], in_=sb_sb[:], axis=mybir.AxisListType.X, op=ALU.add)
         scale = const.tile([P, 2], F32)
-        nc.vector.tensor_scalar(out=scale[:], in0=ssum[:], scalar1=1.0 / I, scalar2=None, op0=ALU.mult)
 
-        for c in range(NCH):
-            n0 = c * CH
-            xp = ew.tile([P, CH, I], BF16)
+        def weights():
+            rwp = setup.tile([P, 2, I], BF16)
+            nc.vector.tensor_copy(
+                out=rwp[:].rearrange("p h (c a m e) -> p (h c) a m e", c=2, a=4, m=4, e=4),
+                in_=rw_sb[:].rearrange("p h (c m a e) -> p (h c) a m e", c=2, m=4, a=4, e=4),
+            )
+            tpr = psum.tile([P, 3, P], BF16, tag="mx", bufs=3)
+            for h in range(2):
+                nc.tensor.transpose(tpr[:, h, :], rwp[:, h, :], ident_b[:])
+            nc.tensor.transpose(tpr[:, 2, :], b_sb[:], ident_b[:])
+            nc.vector.tensor_copy(out=rwT[:], in_=tpr[:, 0:2, :])
+            nc.vector.tensor_copy(out=bias[:], in_=tpr[:, 2, 0:2])
+            ssum = setup.tile([P, 2], F32)
+            nc.vector.tensor_reduce(out=ssum[:], in_=sb_sb[:], axis=mybir.AxisListType.X, op=ALU.add)
+            nc.vector.tensor_scalar(out=scale[:], in0=ssum[:], scalar1=1.0 / I, scalar2=None, op0=ALU.mult)
+            for h in range(2):
+                tpc = psum.tile([P, NBAS, P], BF16, tag="mx", bufs=3)
+                for q in range(NBAS):
+                    nc.tensor.transpose(tpc[:, q, :], cpl[:, h, q, :], ident_b[:])
+                nc.vector.tensor_copy(
+                    out=cgr[:, :, h * 512:(h + 1) * 512].rearrange("p g (w s) -> p g w s", s=4),
+                    in_=tpc[:].rearrange("p (g s) w -> p g w s", s=4),
+                )
+            nc.vector.quantize_mx(
+                out=ccodes[:].rearrange("p g o -> p (g o)").bitcast(FP8X4),
+                scales=cscales[:].rearrange("p g o -> p (g o)"),
+                in_=cgr[:].rearrange("p g k -> p (g k)"),
+            )
+
+        T = [dict() for c in range(NCH)]
+
+        def ok(c):
+            return 0 <= c < NCH
+
+        def rounds(c):
+            return [(r0, min(RT, SIZES[c] - r0)) for r0 in range(0, SIZES[c], RT)]
+
+        def s_xp(c):
+            if not ok(c):
+                return
+            s, n0 = SIZES[c], STARTS[c]
+            xp = ew.tile([P, s, I], BF16, tag="xp")
             nc.vector.tensor_copy(
                 out=xp[:].rearrange("p n (c a m e) -> p (n c) a m e", c=2, a=4, m=4, e=4),
-                in_=x_sb[:, n0:n0 + CH, :].rearrange("p n (c m a e) -> p (n c) a m e", c=2, m=4, a=4, e=4),
+                in_=x_sb[:, n0:n0 + s, :].rearrange("p n (c m a e) -> p (n c) a m e", c=2, m=4, a=4, e=4),
             )
-            tpx = psum.tile([P, CH, P], BF16, tag="tp")
-            for n in range(CH):
+            tpx = psum.tile([P, s, P], BF16, tag="tp")
+            for n in range(s):
                 nc.tensor.transpose(tpx[:, n, :], xp[:, n, :], ident_b[:])
-            nc.scalar.copy(out=xT[:, n0:n0 + CH, :], in_=tpx[:])
-            xTc = xT[:, n0:n0 + CH, :].rearrange("p n w -> p (n w)")
+            T[c]["tpx"] = tpx
 
-            u = ew.tile([P, F], BF16)
-            nc.vector.tensor_scalar(out=u[:], in0=xTc, scalar1=-1.0, scalar2=1.0, op0=ALU.max, op1=ALU.min)
-            a1 = ew.tile([P, F], F32)
-            nc.scalar.activation(out=a1[:], in_=u[:], func=ACT.Abs, bias=0.5, scale=2.5)
-            b1 = ew.tile([P, F], F32)
-            nc.scalar.activation(out=b1[:], in_=u[:], func=ACT.Abs, bias=-0.5, scale=2.5)
-            e = ew.tile([P, F], F32)
-            nc.scalar.activation(out=e[:], in_=a1[:], func=ACT.Abs, bias=-2.0, scale=1.0)
-            nc.scalar.activation(out=e[:], in_=e[:], func=ACT.Abs, bias=-1.0, scale=1.0)
-            d = ew.tile([P, F], F32)
-            nc.scalar.activation(out=d[:], in_=e[:], func=ACT.Identity, bias=1.0, scale=-1.0)
-            sqd = ew.tile([P, F], F32)
-            nc.scalar.activation(out=sqd[:], in_=d[:], func=ACT.Square, bias=0.0, scale=r6)
-            sqe = ew.tile([P, F], F32)
-            nc.scalar.activation(out=sqe[:], in_=e[:], func=ACT.Square, bias=0.0, scale=r6)
+        def s_evx(c):
+            if not ok(c):
+                return
+            s, n0 = SIZES[c], STARTS[c]
+            nc.scalar.copy(out=xT[:, n0:n0 + s, :], in_=T[c]["tpx"][:])
 
-            x3 = ew.tile([P, F], BF16)
-            nc.vector.tensor_tensor(out=x3[:], in0=sqd[:], in1=d[:], op=ALU.mult)
-            y3 = ew.tile([P, F], BF16)
-            nc.vector.tensor_tensor(out=y3[:], in0=sqe[:], in1=e[:], op=ALU.mult)
-            nc.vector.scalar_tensor_tensor(out=sqd[:], in0=sqd[:], scalar=1.0 / 6.0, in1=e[:], op0=ALU.subtract, op1=ALU.mult)
-            nc.vector.scalar_tensor_tensor(out=sqe[:], in0=sqe[:], scalar=1.0 / 6.0, in1=d[:], op0=ALU.subtract, op1=ALU.mult)
-            xi = ew.tile([P, F], BF16)
-            nc.vector.tensor_scalar(out=xi[:], in0=sqe[:], scalar1=3.0, scalar2=2.0 / 3.0, op0=ALU.mult, op1=ALU.add)
-            yi = ew.tile([P, F], BF16)
-            nc.vector.tensor_scalar(out=yi[:], in0=sqd[:], scalar1=3.0, scalar2=2.0 / 3.0, op0=ALU.mult, op1=ALU.add)
+        def s_u(c):
+            if not ok(c):
+                return
+            s, n0 = SIZES[c], STARTS[c]
+            u = ew.tile([P, s * P], BF16, tag="u", bufs=3)
+            nc.vector.tensor_scalar(out=u[:], in0=xT[:, n0:n0 + s, :].rearrange("p n w -> p (n w)"), scalar1=-1.0, scalar2=1.0, op0=ALU.max, op1=ALU.min)
+            T[c]["u"] = u
 
-            planes = ew.tile([P, NBAS, F], BF16)
-            vs = []
-            rzs = []
-            for t in range(4):
-                src = b1 if t % 2 == 0 else a1
-                v = ew.tile([P, F], BF16, tag="v%d" % t)
-                sgn = -1.0 if t in (0, 3) else 1.0
-                off = 7.0 / 6.0 if t in (0, 3) else -5.0 / 6.0
-                nc.scalar.activation(out=v[:], in_=src[:], func=ACT.Identity, bias=off, scale=sgn)
-                vs.append(v)
-            for t in range(4):
-                nc.vector.tensor_tensor(out=vs[t][:], in0=vs[t][:], in1=(yi if t % 2 == 0 else xi)[:], op=ALU.min)
-            for t in range(4):
-                rz = ew.tile([P, F], BF16, tag="rz%d" % t, bufs=1)
-                nc.vector.tensor_scalar(out=rz[:], in0=u[:], scalar1=0.4 * (t + 1) - 1.0, scalar2=0.0, op0=ALU.subtract, op1=ALU.max)
-                rzs.append(rz)
-            for t in range(4):
-                nc.vector.tensor_tensor(out=vs[t][:], in0=vs[t][:], in1=(y3 if t % 2 == 0 else x3)[:], op=ALU.max)
-            for t in range(4):
-                nc.vector.tensor_tensor(out=planes[:, t + 4, :], in0=vs[t][:], in1=rzs[t][:], op=ALU.min)
-            for t in range(4):
-                nc.vector.tensor_tensor(out=planes[:, t, :], in0=vs[t][:], in1=planes[:, t + 4, :], op=ALU.subtract)
+        def s_front(c):
+            if not ok(c):
+                return
+            f = SIZES[c] * P
+            u = T[c]["u"]
+            ab = ew.tile([P, 2, f], F32, tag="ab")
+            de = ew.tile([P, 2, f], F32, tag="de")
+            sq = ew.tile([P, 2, f], F32, tag="sq")
+            nc.scalar.activation(out=ab[:, 0, :], in_=u[:], func=ACT.Abs, bias=0.5, scale=2.5)
+            nc.scalar.activation(out=de[:, 1, :], in_=ab[:, 0, :], func=ACT.Abs, bias=-2.0, scale=1.0)
+            nc.scalar.activation(out=de[:, 1, :], in_=de[:, 1, :], func=ACT.Abs, bias=-1.0, scale=1.0)
+            if c in D_ON_V:
+                nc.vector.tensor_scalar(out=de[:, 0, :], in0=de[:, 1, :], scalar1=-1.0, scalar2=1.0, op0=ALU.mult, op1=ALU.add)
+                nc.scalar.activation(out=ab[:, 1, :], in_=u[:], func=ACT.Abs, bias=-0.5, scale=2.5)
+            else:
+                nc.scalar.activation(out=de[:, 0, :], in_=de[:, 1, :], func=ACT.Identity, bias=1.0, scale=-1.0)
+            nc.scalar.activation(out=sq[:], in_=de[:], func=ACT.Square, bias=0.0, scale=r6)
+            if c not in D_ON_V:
+                nc.scalar.activation(out=ab[:, 1, :], in_=u[:], func=ACT.Abs, bias=-0.5, scale=2.5)
+            T[c]["ab"], T[c]["de"], T[c]["sq"] = ab, de, sq
 
-            for hf in range(F // HALF):
-                cols = slice(hf * HALF, (hf + 1) * HALF)
-                nh = n0 + hf * (HALF // P)
-                gr = be.tile([P, 2, 4 * HALF], BF16, align_bytes=64)
-                bcodes = be.tile([P, 2, HALF], U32, align_bytes=64)
-                bscales = be.tile([P, 2, HALF], U8, align_bytes=64)
-                for g in range(2):
-                    dst = gr[:, g, :].rearrange("p (c i t) -> p c t i", i=4, t=4)
-                    srcp = planes[:, 4 * g:4 * g + 4, cols].rearrange("p t (c i) -> p c t i", i=4)
-                    if (2 * hf + g) in ACT_REGROUP:
-                        nc.scalar.copy(out=dst, in_=srcp)
-                    else:
-                        nc.vector.tensor_copy(out=dst, in_=srcp)
-                for g in range(2):
-                    nc.vector.quantize_mx(out=bcodes[:, g, :].bitcast(FP8X4), scales=bscales[:, g, :], in_=gr[:, g, :])
-                t1s = []
+        def s_env(c):
+            if not ok(c):
+                return
+            f = SIZES[c] * P
+            ab = T[c]["ab"]
+            v = ew.tile([P, 4, f], BF16, tag="v")
+            if c in L_ON_V:
+                nc.vector.tensor_scalar(out=v[:, 0:2, :], in0=ab[:], scalar1=-1.0, scalar2=7.0 / 6.0, op0=ALU.mult, op1=ALU.add)
+                nc.vector.tensor_scalar(out=v[:, 2:4, :], in0=ab[:], scalar1=1.0, scalar2=-5.0 / 6.0, op0=ALU.mult, op1=ALU.add)
+            else:
+                nc.scalar.activation(out=v[:, 0:2, :], in_=ab[:], func=ACT.Identity, bias=7.0 / 6.0, scale=-1.0)
+                nc.scalar.activation(out=v[:, 2:4, :], in_=ab[:], func=ACT.Identity, bias=-5.0 / 6.0, scale=1.0)
+            T[c]["v"] = v
+
+        def s_poly(c):
+            if not ok(c):
+                return
+            f = SIZES[c] * P
+            ab, de, sq = T[c]["ab"], T[c]["de"], T[c]["sq"]
+            ring = ew.tile([P, 2, f], BF16, tag="ring", bufs=1)
+            nc.vector.tensor_tensor(out=ring[:], in0=sq[:], in1=de[:], op=ALU.mult)
+            for k in range(2):
+                nc.vector.scalar_tensor_tensor(out=ab[:, k, :], in0=sq[:, 1 - k, :], scalar=1.0 / 6.0, in1=de[:, k, :], op0=ALU.subtract, op1=ALU.mult)
+            T[c]["ring"] = ring
+
+        def s_inner(c):
+            if not ok(c):
+                return
+            f = SIZES[c] * P
+            inner = ew.tile([P, 2, f], BF16, tag="inner", bufs=1)
+            nc.vector.tensor_scalar(out=inner[:], in0=T[c]["ab"][:], scalar1=3.0, scalar2=2.0 / 3.0, op0=ALU.mult, op1=ALU.add)
+            rz = ew.tile([P, 4, f], BF16, tag="rz", bufs=1)
+            for s in range(4):
+                nc.vector.tensor_scalar(out=rz[:, s, :], in0=T[c]["u"][:], scalar1=0.4 * (TS[s] + 1) - 1.0, scalar2=0.0, op0=ALU.subtract, op1=ALU.max)
+            T[c]["inner"], T[c]["rz"] = inner, rz
+
+        def s_sel(c):
+            if not ok(c):
+                return
+            f = SIZES[c] * P
+            v = T[c]["v"]
+            v4 = v[:].rearrange("p (r k) f -> p r (k f)", r=2)
+            nc.vector.tensor_tensor(out=v4, in0=v4, in1=T[c]["inner"][:].rearrange("p k f -> p (k f)").unsqueeze(1).to_broadcast([P, 2, 2 * f]), op=ALU.min)
+            nc.vector.tensor_tensor(out=v4, in0=v4, in1=T[c]["ring"][:].rearrange("p k f -> p (k f)").unsqueeze(1).to_broadcast([P, 2, 2 * f]), op=ALU.max)
+            planes = ew.tile([P, 2, 4, f], BF16, tag="planes", bufs=1)
+            nc.vector.tensor_tensor(out=planes[:, 1], in0=v[:], in1=T[c]["rz"][:], op=ALU.min)
+            T[c]["planes"] = planes
+            T[c]["gr"] = []
+            for r0, rs in rounds(c):
+                gr = be.tile([P, 2, 4 * rs * P], BF16, tag="gr", align_bytes=64)
+                T[c]["gr"].append(gr)
+
+        def s_lo(c):
+            if not ok(c):
+                return
+            planes = T[c]["planes"]
+            nc.vector.tensor_tensor(out=planes[:, 0], in0=T[c]["v"][:], in1=planes[:, 1], op=ALU.subtract)
+
+        def s_rg(c, g, eng):
+            if not ok(c):
+                return
+            on_act = (c not in HI_ON_V) if g == 1 else (c in LO_ON_ACT)
+            if on_act != (eng == "act"):
+                return
+            for ri, (r0, rs) in enumerate(rounds(c)):
+                dst = T[c]["gr"][ri][:, g, :].rearrange("p (c i s) -> p c s i", i=4, s=4)
+                srcp = T[c]["planes"][:, g, :, r0 * P:(r0 + rs) * P].rearrange("p s (c i) -> p c s i", i=4)
+                if on_act:
+                    nc.scalar.copy(out=dst, in_=srcp)
+                else:
+                    nc.vector.tensor_copy(out=dst, in_=srcp)
+
+        def s_q(c):
+            if not ok(c):
+                return
+            T[c]["mx"] = []
+            for ri, (r0, rs) in enumerate(rounds(c)):
+                n = rs * P
+                bcodes = be.tile([P, 2, n], U32, tag="bcodes", align_bytes=64)
+                bscales = be.tile([P, 2, n], U8, tag="bscales", align_bytes=64)
+                nc.vector.quantize_mx(
+                    out=bcodes[:].rearrange("p g w -> p (g w)").bitcast(FP8X4),
+                    scales=bscales[:].rearrange("p g w -> p (g w)"),
+                    in_=T[c]["gr"][ri][:].rearrange("p g k -> p (g k)"),
+                )
                 for h in range(2):
-                    mx = psum.tile([P, HALF], F32, tag="mx")
+                    mx = psum.tile([P, n], F32, tag="mx", bufs=3)
                     for g in range(2):
                         nc.tensor.matmul_mx(
                             out=mx[:],
@@ -185,17 +262,56 @@ def tile_bsplinebasis_v2_t_kernel(tc, x, spline_coeffs, residual_weight, residua
                             start=(g == 0),
                             stop=(g == 1),
                         )
-                    t1 = be.tile([P, HALF], F32, tag="t1_%d" % h)
-                    nc.scalar.activation(out=t1[:], in_=mx[:], func=ACT.Identity, bias=bias[:, h:h + 1], scale=scale[:, h:h + 1])
+                    T[c]["mx"].append(mx)
+
+        def s_t1(c):
+            if not ok(c):
+                return
+            T[c]["ot"] = []
+            for ri, (r0, rs) in enumerate(rounds(c)):
+                t1s = []
+                for h in range(2):
+                    t1 = be.tile([P, rs * P], F32, tag="t1_%d" % h)
+                    nc.scalar.activation(out=t1[:], in_=T[c]["mx"][2 * ri + h][:], func=ACT.Identity, bias=bias[:, h:h + 1], scale=scale[:, h:h + 1])
                     t1s.append(t1)
-                osb = be.tile([P, 4, O], F32)
-                for k in range(2):
-                    ot = psum.tile([P, 2, O], F32, tag="ot", bufs=4)
-                    for q in range(2):
-                        n = 2 * k + q
+                for k0 in range(0, rs, 2):
+                    kn = min(2, rs - k0)
+                    ot = psum.tile([P, kn, O], F32, tag="ot", bufs=4)
+                    for q in range(kn):
+                        n = k0 + q
                         for h in range(2):
                             dsto = ot[:, q, h * P:(h + 1) * P]
-                            nc.tensor.matmul(out=dsto, lhsT=xT[:, nh + n, :], rhs=rwT[:, h, :], start=True, stop=False)
+                            nc.tensor.matmul(out=dsto, lhsT=xT[:, STARTS[c] + r0 + n, :], rhs=rwT[:, h, :], start=True, stop=False)
                             nc.tensor.matmul(out=dsto, lhsT=t1s[h][:, n * P:(n + 1) * P], rhs=ident_f[:], is_transpose=True, start=False, stop=True)
-                    nc.scalar.copy(out=osb[:, 2 * k:2 * k + 2, :], in_=ot[:])
-                nc.sync.dma_start(out=out_v[:, nh:nh + 4, :], in_=osb[:])
+                    T[c]["ot"].append((ri, k0, kn, ot))
+
+        def s_ev(c):
+            if not ok(c):
+                return
+            rr = rounds(c)
+            osbs = [be.tile([P, rs, O], F32, tag="osb", name="osb") for r0, rs in rr]
+            for ri, k0, kn, ot in T[c]["ot"]:
+                nc.scalar.copy(out=osbs[ri][:, k0:k0 + kn, :], in_=ot[:])
+            for ri, (r0, rs) in enumerate(rr):
+                nh = STARTS[c] + r0
+                nc.sync.dma_start(out=out_v[:, nh:nh + rs, :], in_=osbs[ri][:])
+
+        for k in range(-3, NCH + 2):
+            s_poly(k)
+            s_front(k + 1)
+            s_q(k - 1)
+            s_xp(k + 3)
+            s_u(k + 2)
+            if k == -1:
+                weights()
+            s_inner(k)
+            s_t1(k - 1)
+            s_env(k + 1)
+            s_sel(k)
+            s_ev(k - 1)
+            s_lo(k)
+            s_rg(k, 1, "act")
+            s_rg(k, 1, "v")
+            s_rg(k, 0, "v")
+            s_rg(k, 0, "act")
+            s_evx(k + 3)

@@ -15,19 +15,18 @@ ACT = mybir.ActivationFunctionType
 P = 128
 B, I, O, NBAS = 8192, 128, 256, 8
 NT = B // P
-SIZES = [8] * 8
-NCH = len(SIZES)
-STARTS = [sum(SIZES[:c]) for c in range(NCH)]
-FMAX = max(SIZES) * P
-RT = 4
+GROUPS = [[1, 1], [2, 2]] + [[4, 4]] * 7 + [[1, 1]]
+UNITS = [s for grp in GROUPS for s in grp]
+NU = len(UNITS)
+STARTS = [sum(UNITS[:i]) for i in range(NU)]
+NG = len(GROUPS)
+GFIRST = [sum(len(grp) for grp in GROUPS[:k]) for k in range(NG)]
 TS = (3, 0, 1, 2)
-L_ON_V = ()
-D_ON_V = ()
-HI_ON_V = ()
-LO_ON_ACT = ()
-MANUAL = True
+SLOT = (1, 2, 3, 0)
+RG_V = ((9, 0), (9, 1))
+W_AT = 0
 FLOPS = 2 * B * I * NBAS * O + 2 * B * I * O
-assert sum(SIZES) == NT
+assert sum(UNITS) == NT
 
 
 def tile_bsplinebasis_v2_t_kernel(tc, x, spline_coeffs, residual_weight, residual_bias, scale_base, out):
@@ -36,18 +35,19 @@ def tile_bsplinebasis_v2_t_kernel(tc, x, spline_coeffs, residual_weight, residua
     with ExitStack() as ctx:
         const = ctx.enter_context(tc.tile_pool(name="const", bufs=1))
         setup = ctx.enter_context(tc.tile_pool(name="setup", bufs=1))
-        ew = ctx.enter_context(tc.tile_pool(name="ew", bufs=2))
+        ew = ctx.enter_context(tc.tile_pool(name="ew", bufs=4))
         be = ctx.enter_context(tc.tile_pool(name="be", bufs=2))
         psum = ctx.enter_context(tc.psum_pool(name="psum", bufs=1))
-        if MANUAL:
-            ctx.enter_context(tc.manual_schedule())
+        ctx.enter_context(tc.manual_schedule())
 
         x_sb = const.tile([P, NT, I], BF16)
         xT = const.tile([P, NT, P], BF16)
         x_v = x.rearrange("(p n) i -> p n i", n=NT)
         out_v = out.rearrange("(p n) o -> p n o", n=NT)
-        for c in range(NCH):
-            nc.sync.dma_start(out=x_sb[:, STARTS[c]:STARTS[c] + SIZES[c], :], in_=x_v[:, STARTS[c]:STARTS[c] + SIZES[c], :])
+        for k in range(NG):
+            a = STARTS[GFIRST[k]]
+            b = a + sum(GROUPS[k])
+            nc.sync.dma_start(out=x_sb[:, a:b, :], in_=x_v[:, a:b, :])
 
         ident_b = const.tile([P, P], BF16)
         make_identity(nc, ident_b[:])
@@ -64,14 +64,6 @@ def tile_bsplinebasis_v2_t_kernel(tc, x, spline_coeffs, residual_weight, residua
         nc.gpsimd.memset(b_sb[:], 0.0)
         nc.scalar.dma_start(out=b_sb[0:2, :], in_=residual_bias.rearrange("(h p) -> h p", p=P))
 
-        cpl = setup.tile([P, 2, NBAS, I], BF16)
-        for h in range(2):
-            for q in range(NBAS):
-                j = 4 * (q // 4) + TS[q % 4]
-                nc.gpsimd.tensor_copy(
-                    out=cpl[:, h, q, :].rearrange("p (c a m e) -> p c a m e", c=2, a=4, m=4, e=4),
-                    in_=c_sb[:, h, :].rearrange("p (c m a e j) -> p j c a m e", c=2, m=4, a=4, e=4, j=NBAS)[:, j],
-                )
         cgr = setup.tile([P, 2, 4 * O], BF16, align_bytes=64)
         ccodes = const.tile([P, 2, O], U32, align_bytes=64)
         cscales = const.tile([P, 2, O], U8, align_bytes=64)
@@ -80,6 +72,11 @@ def tile_bsplinebasis_v2_t_kernel(tc, x, spline_coeffs, residual_weight, residua
         scale = const.tile([P, 2], F32)
 
         def weights():
+            cpm = setup.tile([P, 2, I * NBAS], BF16)
+            nc.vector.tensor_copy(
+                out=cpm[:].rearrange("p h (c a m k) -> p (h c) a m k", c=2, a=4, m=4, k=32),
+                in_=c_sb[:].rearrange("p h (c m a k) -> p (h c) a m k", c=2, m=4, a=4, k=32),
+            )
             rwp = setup.tile([P, 2, I], BF16)
             nc.vector.tensor_copy(
                 out=rwp[:].rearrange("p h (c a m e) -> p (h c) a m e", c=2, a=4, m=4, e=4),
@@ -97,7 +94,8 @@ def tile_bsplinebasis_v2_t_kernel(tc, x, spline_coeffs, residual_weight, residua
             for h in range(2):
                 tpc = psum.tile([P, NBAS, P], BF16, tag="mx", bufs=3)
                 for q in range(NBAS):
-                    nc.tensor.transpose(tpc[:, q, :], cpl[:, h, q, :], ident_b[:])
+                    j = 4 * (q // 4) + TS[q % 4]
+                    nc.tensor.transpose(tpc[:, q, :], cpm[:, h, :].rearrange("p (r j) -> p j r", j=NBAS)[:, j], ident_b[:])
                 nc.vector.tensor_copy(
                     out=cgr[:, :, h * 512:(h + 1) * 512].rearrange("p g (w s) -> p g w s", s=4),
                     in_=tpc[:].rearrange("p (g s) w -> p g w s", s=4),
@@ -108,210 +106,239 @@ def tile_bsplinebasis_v2_t_kernel(tc, x, spline_coeffs, residual_weight, residua
                 in_=cgr[:].rearrange("p g k -> p (g k)"),
             )
 
-        T = [dict() for c in range(NCH)]
+        T = [dict() for i in range(NU)]
 
-        def ok(c):
-            return 0 <= c < NCH
+        def units(k):
+            if 0 <= k < NG:
+                return list(range(GFIRST[k], GFIRST[k] + len(GROUPS[k])))
+            return []
 
-        def rounds(c):
-            return [(r0, min(RT, SIZES[c] - r0)) for r0 in range(0, SIZES[c], RT)]
+        def each(k, *ops):
+            for op in ops:
+                for i in units(k):
+                    op(i)
 
-        def s_xp(c):
-            if not ok(c):
-                return
-            s, n0 = SIZES[c], STARTS[c]
-            xp = ew.tile([P, s, I], BF16, tag="xp")
+        def one(k, j, op):
+            us = units(k)
+            if j < len(us):
+                op(us[j])
+
+        def xp_(i):
+            s, n0 = UNITS[i], STARTS[i]
+            xp = ew.tile([P, s, I], BF16, tag="xp", bufs=2)
             nc.vector.tensor_copy(
                 out=xp[:].rearrange("p n (c a m e) -> p (n c) a m e", c=2, a=4, m=4, e=4),
                 in_=x_sb[:, n0:n0 + s, :].rearrange("p n (c m a e) -> p (n c) a m e", c=2, m=4, a=4, e=4),
             )
-            tpx = psum.tile([P, s, P], BF16, tag="tp")
-            for n in range(s):
-                nc.tensor.transpose(tpx[:, n, :], xp[:, n, :], ident_b[:])
-            T[c]["tpx"] = tpx
+            T[i]["xp"] = xp
 
-        def s_evx(c):
-            if not ok(c):
+        def tx_(k):
+            us = units(k)
+            if not us:
                 return
-            s, n0 = SIZES[c], STARTS[c]
-            nc.scalar.copy(out=xT[:, n0:n0 + s, :], in_=T[c]["tpx"][:])
+            tot = sum(GROUPS[k])
+            tpx = psum.tile([P, tot, P], BF16, tag="tp")
+            o0 = 0
+            for i in us:
+                for n in range(UNITS[i]):
+                    nc.tensor.transpose(tpx[:, o0 + n, :], T[i]["xp"][:, n, :], ident_b[:])
+                o0 += UNITS[i]
+            T[us[0]]["tpx"] = tpx
 
-        def s_u(c):
-            if not ok(c):
+        def evx_(k):
+            us = units(k)
+            if not us:
                 return
-            s, n0 = SIZES[c], STARTS[c]
-            u = ew.tile([P, s * P], BF16, tag="u", bufs=3)
+            a = STARTS[us[0]]
+            nc.scalar.copy(out=xT[:, a:a + sum(GROUPS[k]), :], in_=T[us[0]]["tpx"][:])
+
+        def u_(i):
+            s, n0 = UNITS[i], STARTS[i]
+            u = ew.tile([P, s * P], BF16, tag="u", bufs=6)
             nc.vector.tensor_scalar(out=u[:], in0=xT[:, n0:n0 + s, :].rearrange("p n w -> p (n w)"), scalar1=-1.0, scalar2=1.0, op0=ALU.max, op1=ALU.min)
-            T[c]["u"] = u
+            T[i]["u"] = u
 
-        def s_front(c):
-            if not ok(c):
-                return
-            f = SIZES[c] * P
-            u = T[c]["u"]
-            ab = ew.tile([P, 2, f], F32, tag="ab")
+        def a1_(i):
+            f = UNITS[i] * P
             de = ew.tile([P, 2, f], F32, tag="de")
+            nc.scalar.activation(out=de[:, 1, :], in_=T[i]["u"][:], func=ACT.Abs, bias=0.5, scale=2.5)
+            T[i]["de"] = de
+
+        def a2_(i):
+            e = T[i]["de"][:, 1, :]
+            nc.scalar.activation(out=e, in_=e, func=ACT.Abs, bias=-2.0, scale=1.0)
+
+        def a3_(i):
+            e = T[i]["de"][:, 1, :]
+            nc.scalar.activation(out=e, in_=e, func=ACT.Abs, bias=-1.0, scale=1.0)
+
+        def sqd_(i):
+            f = UNITS[i] * P
             sq = ew.tile([P, 2, f], F32, tag="sq")
-            nc.scalar.activation(out=ab[:, 0, :], in_=u[:], func=ACT.Abs, bias=0.5, scale=2.5)
-            nc.scalar.activation(out=de[:, 1, :], in_=ab[:, 0, :], func=ACT.Abs, bias=-2.0, scale=1.0)
-            nc.scalar.activation(out=de[:, 1, :], in_=de[:, 1, :], func=ACT.Abs, bias=-1.0, scale=1.0)
-            if c in D_ON_V:
-                nc.vector.tensor_scalar(out=de[:, 0, :], in0=de[:, 1, :], scalar1=-1.0, scalar2=1.0, op0=ALU.mult, op1=ALU.add)
-                nc.scalar.activation(out=ab[:, 1, :], in_=u[:], func=ACT.Abs, bias=-0.5, scale=2.5)
-            else:
-                nc.scalar.activation(out=de[:, 0, :], in_=de[:, 1, :], func=ACT.Identity, bias=1.0, scale=-1.0)
-            nc.scalar.activation(out=sq[:], in_=de[:], func=ACT.Square, bias=0.0, scale=r6)
-            if c not in D_ON_V:
-                nc.scalar.activation(out=ab[:, 1, :], in_=u[:], func=ACT.Abs, bias=-0.5, scale=2.5)
-            T[c]["ab"], T[c]["de"], T[c]["sq"] = ab, de, sq
+            nc.scalar.activation(out=sq[:, 0, :], in_=T[i]["de"][:, 1, :], func=ACT.Square, bias=r6, scale=-r6)
+            T[i]["sq"] = sq
 
-        def s_env(c):
-            if not ok(c):
-                return
-            f = SIZES[c] * P
-            ab = T[c]["ab"]
-            v = ew.tile([P, 4, f], BF16, tag="v")
-            if c in L_ON_V:
-                nc.vector.tensor_scalar(out=v[:, 0:2, :], in0=ab[:], scalar1=-1.0, scalar2=7.0 / 6.0, op0=ALU.mult, op1=ALU.add)
-                nc.vector.tensor_scalar(out=v[:, 2:4, :], in0=ab[:], scalar1=1.0, scalar2=-5.0 / 6.0, op0=ALU.mult, op1=ALU.add)
-            else:
-                nc.scalar.activation(out=v[:, 0:2, :], in_=ab[:], func=ACT.Identity, bias=7.0 / 6.0, scale=-1.0)
-                nc.scalar.activation(out=v[:, 2:4, :], in_=ab[:], func=ACT.Identity, bias=-5.0 / 6.0, scale=1.0)
-            T[c]["v"] = v
+        def sqe_(i):
+            nc.scalar.activation(out=T[i]["sq"][:, 1, :], in_=T[i]["de"][:, 1, :], func=ACT.Square, bias=0.0, scale=r6)
 
-        def s_poly(c):
-            if not ok(c):
-                return
-            f = SIZES[c] * P
-            ab, de, sq = T[c]["ab"], T[c]["de"], T[c]["sq"]
-            ring = ew.tile([P, 2, f], BF16, tag="ring", bufs=1)
-            nc.vector.tensor_tensor(out=ring[:], in0=sq[:], in1=de[:], op=ALU.mult)
-            for k in range(2):
-                nc.vector.scalar_tensor_tensor(out=ab[:, k, :], in0=sq[:, 1 - k, :], scalar=1.0 / 6.0, in1=de[:, k, :], op0=ALU.subtract, op1=ALU.mult)
-            T[c]["ring"] = ring
+        def da_(i):
+            de = T[i]["de"]
+            nc.scalar.activation(out=de[:, 0, :], in_=de[:, 1, :], func=ACT.Identity, bias=1.0, scale=-1.0)
 
-        def s_inner(c):
-            if not ok(c):
-                return
-            f = SIZES[c] * P
-            inner = ew.tile([P, 2, f], BF16, tag="inner", bufs=1)
-            nc.vector.tensor_scalar(out=inner[:], in0=T[c]["ab"][:], scalar1=3.0, scalar2=2.0 / 3.0, op0=ALU.mult, op1=ALU.add)
-            rz = ew.tile([P, 4, f], BF16, tag="rz", bufs=1)
+        def ia_(i):
+            f = UNITS[i] * P
+            inner = ew.tile([P, 2, f], BF16, tag="inner", bufs=2)
+            nc.scalar.activation(out=inner[:], in_=T[i]["w"][:], func=ACT.Identity, bias=2.0 / 3.0, scale=3.0)
+            T[i]["inner"] = inner
+
+        def d_(i):
+            de = T[i]["de"]
+            nc.vector.tensor_scalar(out=de[:, 0, :], in0=de[:, 1, :], scalar1=-1.0, scalar2=1.0, op0=ALU.mult, op1=ALU.add)
+
+        def ring_(i):
+            f = UNITS[i] * P
+            ring = ew.tile([P, 2, f], BF16, tag="ring", bufs=2)
+            nc.vector.tensor_tensor(out=ring[:], in0=T[i]["sq"][:], in1=T[i]["de"][:], op=ALU.mult)
+            T[i]["ring"] = ring
+
+        def w0_(i):
+            f = UNITS[i] * P
+            w = ew.tile([P, 2, f], F32, tag="w", bufs=2)
+            nc.vector.scalar_tensor_tensor(out=w[:, 0, :], in0=T[i]["sq"][:, 1, :], scalar=1.0 / 6.0, in1=T[i]["de"][:, 0, :], op0=ALU.subtract, op1=ALU.mult)
+            T[i]["w"] = w
+
+        def w1_(i):
+            nc.vector.scalar_tensor_tensor(out=T[i]["w"][:, 1, :], in0=T[i]["sq"][:, 0, :], scalar=1.0 / 6.0, in1=T[i]["de"][:, 1, :], op0=ALU.subtract, op1=ALU.mult)
+
+        def inner_(i):
+            f = UNITS[i] * P
+            inner = ew.tile([P, 2, f], BF16, tag="inner", bufs=2)
+            nc.vector.tensor_scalar(out=inner[:], in0=T[i]["w"][:], scalar1=3.0, scalar2=2.0 / 3.0, op0=ALU.mult, op1=ALU.add)
+            T[i]["inner"] = inner
+
+        def gam_(i):
+            f = UNITS[i] * P
+            gam = ew.tile([P, 4, f], BF16, tag="gam", bufs=2)
             for s in range(4):
-                nc.vector.tensor_scalar(out=rz[:, s, :], in0=T[c]["u"][:], scalar1=0.4 * (TS[s] + 1) - 1.0, scalar2=0.0, op0=ALU.subtract, op1=ALU.max)
-            T[c]["inner"], T[c]["rz"] = inner, rz
+                nc.vector.tensor_scalar(out=gam[:, s, :], in0=T[i]["u"][:], scalar1=0.4 * (TS[s] + 1) - 1.0, scalar2=None, op0=ALU.is_gt)
+            T[i]["gam"] = gam
 
-        def s_sel(c):
-            if not ok(c):
-                return
-            f = SIZES[c] * P
-            v = T[c]["v"]
-            v4 = v[:].rearrange("p (r k) f -> p r (k f)", r=2)
-            nc.vector.tensor_tensor(out=v4, in0=v4, in1=T[c]["inner"][:].rearrange("p k f -> p (k f)").unsqueeze(1).to_broadcast([P, 2, 2 * f]), op=ALU.min)
-            nc.vector.tensor_tensor(out=v4, in0=v4, in1=T[c]["ring"][:].rearrange("p k f -> p (k f)").unsqueeze(1).to_broadcast([P, 2, 2 * f]), op=ALU.max)
-            planes = ew.tile([P, 2, 4, f], BF16, tag="planes", bufs=1)
-            nc.vector.tensor_tensor(out=planes[:, 1], in0=v[:], in1=T[c]["rz"][:], op=ALU.min)
-            T[c]["planes"] = planes
-            T[c]["gr"] = []
-            for r0, rs in rounds(c):
-                gr = be.tile([P, 2, 4 * rs * P], BF16, tag="gr", align_bytes=64)
-                T[c]["gr"].append(gr)
+        def beta_(i):
+            f = UNITS[i] * P
+            gam = T[i]["gam"]
+            beta = ew.tile([P, 2, f], BF16, tag="beta", bufs=2)
+            for k in range(2):
+                nc.vector.tensor_tensor(out=beta[:, k, :], in0=gam[:, SLOT[k], :], in1=gam[:, SLOT[k + 2], :], op=ALU.subtract)
+            T[i]["beta"] = beta
 
-        def s_lo(c):
-            if not ok(c):
-                return
-            planes = T[c]["planes"]
-            nc.vector.tensor_tensor(out=planes[:, 0], in0=T[c]["v"][:], in1=planes[:, 1], op=ALU.subtract)
+        def p1_(i):
+            f = UNITS[i] * P
+            v = ew.tile([P, 4, f], BF16, tag="v", bufs=2)
+            nc.vector.tensor_tensor(out=v[:, 0:2, :], in0=T[i]["beta"][:], in1=T[i]["inner"][:], op=ALU.mult)
+            T[i]["v"] = v
 
-        def s_rg(c, g, eng):
-            if not ok(c):
-                return
-            on_act = (c not in HI_ON_V) if g == 1 else (c in LO_ON_ACT)
-            if on_act != (eng == "act"):
-                return
-            for ri, (r0, rs) in enumerate(rounds(c)):
-                dst = T[c]["gr"][ri][:, g, :].rearrange("p (c i s) -> p c s i", i=4, s=4)
-                srcp = T[c]["planes"][:, g, :, r0 * P:(r0 + rs) * P].rearrange("p s (c i) -> p c s i", i=4)
-                if on_act:
-                    nc.scalar.copy(out=dst, in_=srcp)
-                else:
-                    nc.vector.tensor_copy(out=dst, in_=srcp)
+        def p0_(i):
+            v = T[i]["v"]
+            nc.vector.tensor_tensor(out=v[:, 2:4, :], in0=T[i]["inner"][:], in1=v[:, 0:2, :], op=ALU.subtract)
 
-        def s_q(c):
-            if not ok(c):
-                return
-            T[c]["mx"] = []
-            for ri, (r0, rs) in enumerate(rounds(c)):
-                n = rs * P
-                bcodes = be.tile([P, 2, n], U32, tag="bcodes", align_bytes=64)
-                bscales = be.tile([P, 2, n], U8, tag="bscales", align_bytes=64)
-                nc.vector.quantize_mx(
-                    out=bcodes[:].rearrange("p g w -> p (g w)").bitcast(FP8X4),
-                    scales=bscales[:].rearrange("p g w -> p (g w)"),
-                    in_=T[c]["gr"][ri][:].rearrange("p g k -> p (g k)"),
-                )
-                for h in range(2):
-                    mx = psum.tile([P, n], F32, tag="mx", bufs=3)
-                    for g in range(2):
-                        nc.tensor.matmul_mx(
-                            out=mx[:],
-                            lhsT=ccodes[:, g, h * P:(h + 1) * P].bitcast(FP8X4),
-                            lhsT_scale=cscales[:, g, h * P:(h + 1) * P],
-                            rhs=bcodes[:, g, :].bitcast(FP8X4),
-                            rhs_scale=bscales[:, g, :],
-                            start=(g == 0),
-                            stop=(g == 1),
-                        )
-                    T[c]["mx"].append(mx)
+        def max_(i):
+            f = UNITS[i] * P
+            v4 = T[i]["v"][:].rearrange("p (r k) f -> p r (k f)", r=2)
+            nc.vector.tensor_tensor(out=v4, in0=v4, in1=T[i]["ring"][:].rearrange("p k f -> p (k f)").unsqueeze(1).to_broadcast([P, 2, 2 * f]), op=ALU.max)
 
-        def s_t1(c):
-            if not ok(c):
-                return
-            T[c]["ot"] = []
-            for ri, (r0, rs) in enumerate(rounds(c)):
-                t1s = []
-                for h in range(2):
-                    t1 = be.tile([P, rs * P], F32, tag="t1_%d" % h)
-                    nc.scalar.activation(out=t1[:], in_=T[c]["mx"][2 * ri + h][:], func=ACT.Identity, bias=bias[:, h:h + 1], scale=scale[:, h:h + 1])
-                    t1s.append(t1)
-                for k0 in range(0, rs, 2):
-                    kn = min(2, rs - k0)
-                    ot = psum.tile([P, kn, O], F32, tag="ot", bufs=4)
-                    for q in range(kn):
-                        n = k0 + q
-                        for h in range(2):
-                            dsto = ot[:, q, h * P:(h + 1) * P]
-                            nc.tensor.matmul(out=dsto, lhsT=xT[:, STARTS[c] + r0 + n, :], rhs=rwT[:, h, :], start=True, stop=False)
-                            nc.tensor.matmul(out=dsto, lhsT=t1s[h][:, n * P:(n + 1) * P], rhs=ident_f[:], is_transpose=True, start=False, stop=True)
-                    T[c]["ot"].append((ri, k0, kn, ot))
+        def hi_(i):
+            f = UNITS[i] * P
+            planes = ew.tile([P, 2, 4, f], BF16, tag="planes", bufs=4)
+            nc.vector.tensor_tensor(out=planes[:, 1], in0=T[i]["v"][:], in1=T[i]["gam"][:], op=ALU.mult)
+            T[i]["planes"] = planes
+            gr = be.tile([P, 2, 4 * f], BF16, tag="gr", bufs=4, align_bytes=64)
+            T[i]["gr"] = gr
 
-        def s_ev(c):
-            if not ok(c):
-                return
-            rr = rounds(c)
-            osbs = [be.tile([P, rs, O], F32, tag="osb", name="osb") for r0, rs in rr]
-            for ri, k0, kn, ot in T[c]["ot"]:
-                nc.scalar.copy(out=osbs[ri][:, k0:k0 + kn, :], in_=ot[:])
-            for ri, (r0, rs) in enumerate(rr):
-                nh = STARTS[c] + r0
-                nc.sync.dma_start(out=out_v[:, nh:nh + rs, :], in_=osbs[ri][:])
+        def lo_(i):
+            planes = T[i]["planes"]
+            nc.vector.tensor_tensor(out=planes[:, 0], in0=T[i]["v"][:], in1=planes[:, 1], op=ALU.subtract)
 
-        for k in range(-3, NCH + 2):
-            s_poly(k)
-            s_front(k + 1)
-            s_q(k - 1)
-            s_xp(k + 3)
-            s_u(k + 2)
-            if k == -1:
+        def rg(i, g, eng):
+            dst = T[i]["gr"][:, g, :].rearrange("p (c i s) -> p c s i", i=4, s=4)
+            srcp = T[i]["planes"][:, g].rearrange("p s (c i) -> p c s i", i=4)
+            if eng == "act":
+                nc.scalar.copy(out=dst, in_=srcp)
+            else:
+                nc.vector.tensor_copy(out=dst, in_=srcp)
+
+        def rgs(k, eng):
+            for i in units(k):
+                for g in (1, 0):
+                    if ((k, g) in RG_V) == (eng == "v"):
+                        rg(i, g, eng)
+
+        def q_(i):
+            n = UNITS[i] * P
+            bcodes = be.tile([P, 2, n], U32, tag="bcodes", align_bytes=64)
+            bscales = be.tile([P, 2, n], U8, tag="bscales", align_bytes=64)
+            nc.vector.quantize_mx(
+                out=bcodes[:].rearrange("p g w -> p (g w)").bitcast(FP8X4),
+                scales=bscales[:].rearrange("p g w -> p (g w)"),
+                in_=T[i]["gr"][:].rearrange("p g k -> p (g k)"),
+            )
+            T[i]["mx"] = []
+            for h in range(2):
+                mx = psum.tile([P, n], F32, tag="mx", bufs=3)
+                for g in range(2):
+                    nc.tensor.matmul_mx(
+                        out=mx[:],
+                        lhsT=ccodes[:, g, h * P:(h + 1) * P].bitcast(FP8X4),
+                        lhsT_scale=cscales[:, g, h * P:(h + 1) * P],
+                        rhs=bcodes[:, g, :].bitcast(FP8X4),
+                        rhs_scale=bscales[:, g, :],
+                        start=(g == 0),
+                        stop=(g == 1),
+                    )
+                T[i]["mx"].append(mx)
+
+        def t1_(i):
+            s = UNITS[i]
+            t1s = []
+            for h in range(2):
+                t1 = be.tile([P, s * P], F32, tag="t1_%d" % h)
+                nc.scalar.activation(out=t1[:], in_=T[i]["mx"][h][:], func=ACT.Identity, bias=bias[:, h:h + 1], scale=scale[:, h:h + 1])
+                t1s.append(t1)
+            T[i]["ot"] = []
+            for k0 in range(0, s, 2):
+                kn = min(2, s - k0)
+                ot = psum.tile([P, kn, O], F32, tag="ot", bufs=4)
+                for q in range(kn):
+                    n = k0 + q
+                    for h in range(2):
+                        dsto = ot[:, q, h * P:(h + 1) * P]
+                        nc.tensor.matmul(out=dsto, lhsT=xT[:, STARTS[i] + n, :], rhs=rwT[:, h, :], start=True, stop=False)
+                        nc.tensor.matmul(out=dsto, lhsT=t1s[h][:, n * P:(n + 1) * P], rhs=ident_f[:], is_transpose=True, start=False, stop=True)
+                T[i]["ot"].append((k0, kn, ot))
+
+        def ev_(i):
+            s = UNITS[i]
+            osb = be.tile([P, s, O], F32, tag="osb", bufs=3)
+            for k0, kn, ot in T[i]["ot"]:
+                nc.scalar.copy(out=osb[:, k0:k0 + kn, :], in_=ot[:])
+            nc.sync.dma_start(out=out_v[:, STARTS[i]:STARTS[i] + s, :], in_=osb[:])
+
+        for k in range(-3, NG + 2):
+            each(k + 3, xp_)
+            tx_(k + 3)
+            rgs(k - 1, "act")
+            each(k, ring_, w0_, w1_)
+            each(k + 1, a1_, a2_, a3_)
+            rgs(k - 1, "v")
+            one(k - 1, 0, q_)
+            each(k, inner_, gam_)
+            one(k - 1, 0, t1_)
+            one(k - 1, 1, q_)
+            each(k + 1, sqd_, sqe_, da_)
+            each(k, beta_, p1_, p0_, max_)
+            one(k - 1, 1, t1_)
+            evx_(k + 3)
+            each(k, hi_, lo_)
+            each(k - 1, ev_)
+            each(k + 2, u_)
+            if k == W_AT:
                 weights()
-            s_inner(k)
-            s_t1(k - 1)
-            s_env(k + 1)
-            s_sel(k)
-            s_ev(k - 1)
-            s_lo(k)
-            s_rg(k, 1, "act")
-            s_rg(k, 1, "v")
-            s_rg(k, 0, "v")
-            s_rg(k, 0, "act")
-            s_evx(k + 3)

@@ -15,18 +15,15 @@ ACT = mybir.ActivationFunctionType
 P = 128
 B, I, O, NBAS = 8192, 128, 256, 8
 NT = B // P
-GROUPS = [[1, 1], [2, 2]] + [[4, 4]] * 7 + [[1, 1]]
-UNITS = [s for grp in GROUPS for s in grp]
-NU = len(UNITS)
-STARTS = [sum(UNITS[:i]) for i in range(NU)]
+GROUPS = [[1, 1], [2, 2]] + [[4, 4]] * 6 + [[2, 2], [2, 2], [1, 1]]
 NG = len(GROUPS)
-GFIRST = [sum(len(grp) for grp in GROUPS[:k]) for k in range(NG)]
+GSTART = [sum(sum(grp) for grp in GROUPS[:k]) for k in range(NG)]
 TS = (3, 0, 1, 2)
 SLOT = (1, 2, 3, 0)
-RG_V = ((9, 0), (9, 1))
+RG_V = ((10, 0), (10, 1), (9, 0), (9, 1))
 W_AT = 0
 FLOPS = 2 * B * I * NBAS * O + 2 * B * I * O
-assert sum(UNITS) == NT
+assert sum(sum(grp) for grp in GROUPS) == NT
 
 
 def tile_bsplinebasis_v2_t_kernel(tc, x, spline_coeffs, residual_weight, residual_bias, scale_base, out):
@@ -35,7 +32,7 @@ def tile_bsplinebasis_v2_t_kernel(tc, x, spline_coeffs, residual_weight, residua
     with ExitStack() as ctx:
         const = ctx.enter_context(tc.tile_pool(name="const", bufs=1))
         setup = ctx.enter_context(tc.tile_pool(name="setup", bufs=1))
-        ew = ctx.enter_context(tc.tile_pool(name="ew", bufs=4))
+        ew = ctx.enter_context(tc.tile_pool(name="ew", bufs=2))
         be = ctx.enter_context(tc.tile_pool(name="be", bufs=2))
         psum = ctx.enter_context(tc.psum_pool(name="psum", bufs=1))
         ctx.enter_context(tc.manual_schedule())
@@ -45,7 +42,7 @@ def tile_bsplinebasis_v2_t_kernel(tc, x, spline_coeffs, residual_weight, residua
         x_v = x.rearrange("(p n) i -> p n i", n=NT)
         out_v = out.rearrange("(p n) o -> p n o", n=NT)
         for k in range(NG):
-            a = STARTS[GFIRST[k]]
+            a = GSTART[k]
             b = a + sum(GROUPS[k])
             nc.sync.dma_start(out=x_sb[:, a:b, :], in_=x_v[:, a:b, :])
 
@@ -82,7 +79,7 @@ def tile_bsplinebasis_v2_t_kernel(tc, x, spline_coeffs, residual_weight, residua
                 out=rwp[:].rearrange("p h (c a m e) -> p (h c) a m e", c=2, a=4, m=4, e=4),
                 in_=rw_sb[:].rearrange("p h (c m a e) -> p (h c) a m e", c=2, m=4, a=4, e=4),
             )
-            tpr = psum.tile([P, 3, P], BF16, tag="mx", bufs=3)
+            tpr = psum.tile([P, 3, P], BF16, tag="mx", bufs=4)
             for h in range(2):
                 nc.tensor.transpose(tpr[:, h, :], rwp[:, h, :], ident_b[:])
             nc.tensor.transpose(tpr[:, 2, :], b_sb[:], ident_b[:])
@@ -92,7 +89,7 @@ def tile_bsplinebasis_v2_t_kernel(tc, x, spline_coeffs, residual_weight, residua
             nc.vector.tensor_reduce(out=ssum[:], in_=sb_sb[:], axis=mybir.AxisListType.X, op=ALU.add)
             nc.vector.tensor_scalar(out=scale[:], in0=ssum[:], scalar1=1.0 / I, scalar2=None, op0=ALU.mult)
             for h in range(2):
-                tpc = psum.tile([P, NBAS, P], BF16, tag="mx", bufs=3)
+                tpc = psum.tile([P, NBAS, P], BF16, tag="mx", bufs=4)
                 for q in range(NBAS):
                     j = 4 * (q // 4) + TS[q % 4]
                     nc.tensor.transpose(tpc[:, q, :], cpm[:, h, :].rearrange("p (r j) -> p j r", j=NBAS)[:, j], ident_b[:])
@@ -106,184 +103,167 @@ def tile_bsplinebasis_v2_t_kernel(tc, x, spline_coeffs, residual_weight, residua
                 in_=cgr[:].rearrange("p g k -> p (g k)"),
             )
 
-        T = [dict() for i in range(NU)]
+        T = [dict() for k in range(NG)]
 
-        def units(k):
-            if 0 <= k < NG:
-                return list(range(GFIRST[k], GFIRST[k] + len(GROUPS[k])))
-            return []
+        def ok(k):
+            return 0 <= k < NG
 
-        def each(k, *ops):
+        def nun(k):
+            return len(GROUPS[k]) if ok(k) else 0
+
+        def dims(k):
+            return len(GROUPS[k]), GROUPS[k][0] * P
+
+        def grp(k, *ops):
+            if ok(k):
+                for op in ops:
+                    op(k)
+
+        def alt(k, *ops):
             for op in ops:
-                for i in units(k):
-                    op(i)
+                for j in range(nun(k)):
+                    op(k, j)
 
-        def one(k, j, op):
-            us = units(k)
-            if j < len(us):
-                op(us[j])
+        def one(k, j, *ops):
+            if j < nun(k):
+                for op in ops:
+                    op(k, j)
 
-        def xp_(i):
-            s, n0 = UNITS[i], STARTS[i]
-            xp = ew.tile([P, s, I], BF16, tag="xp", bufs=2)
+        def early(k):
+            return (k, 0) in RG_V and (k, 1) in RG_V
+
+        def late(k, j, op):
+            if ok(k - 2) and not early(k - 2):
+                one(k - 2, j, op)
+            if ok(k - 1) and early(k - 1):
+                one(k - 1, j, op)
+
+        def xp_(k):
+            s, n0 = sum(GROUPS[k]), GSTART[k]
+            xp = ew.tile([P, s, I], BF16, tag="xp")
             nc.vector.tensor_copy(
                 out=xp[:].rearrange("p n (c a m e) -> p (n c) a m e", c=2, a=4, m=4, e=4),
                 in_=x_sb[:, n0:n0 + s, :].rearrange("p n (c m a e) -> p (n c) a m e", c=2, m=4, a=4, e=4),
             )
-            T[i]["xp"] = xp
-
-        def tx_(k):
-            us = units(k)
-            if not us:
-                return
-            tot = sum(GROUPS[k])
-            tpx = psum.tile([P, tot, P], BF16, tag="tp")
-            o0 = 0
-            for i in us:
-                for n in range(UNITS[i]):
-                    nc.tensor.transpose(tpx[:, o0 + n, :], T[i]["xp"][:, n, :], ident_b[:])
-                o0 += UNITS[i]
-            T[us[0]]["tpx"] = tpx
+            tpx = psum.tile([P, s, P], BF16, tag="tp")
+            for n in range(s):
+                nc.tensor.transpose(tpx[:, n, :], xp[:, n, :], ident_b[:])
+            T[k]["tpx"] = tpx
 
         def evx_(k):
-            us = units(k)
-            if not us:
-                return
-            a = STARTS[us[0]]
-            nc.scalar.copy(out=xT[:, a:a + sum(GROUPS[k]), :], in_=T[us[0]]["tpx"][:])
+            s, n0 = sum(GROUPS[k]), GSTART[k]
+            nc.scalar.copy(out=xT[:, n0:n0 + s, :], in_=T[k]["tpx"][:])
 
-        def u_(i):
-            s, n0 = UNITS[i], STARTS[i]
-            u = ew.tile([P, s * P], BF16, tag="u", bufs=6)
-            nc.vector.tensor_scalar(out=u[:], in0=xT[:, n0:n0 + s, :].rearrange("p n w -> p (n w)"), scalar1=-1.0, scalar2=1.0, op0=ALU.max, op1=ALU.min)
-            T[i]["u"] = u
+        def u_(k):
+            s, n0 = sum(GROUPS[k]), GSTART[k]
+            nu, f = dims(k)
+            u = ew.tile([P, nu, f], BF16, tag="u", bufs=3)
+            nc.vector.tensor_scalar(out=u[:].rearrange("p a f -> p (a f)"), in0=xT[:, n0:n0 + s, :].rearrange("p n w -> p (n w)"), scalar1=-1.0, scalar2=1.0, op0=ALU.max, op1=ALU.min)
+            T[k]["u"] = u
+            T[k]["de"] = ew.tile([P, nu, 2, f], F32, tag="de", name="de")
 
-        def a1_(i):
-            f = UNITS[i] * P
-            de = ew.tile([P, 2, f], F32, tag="de")
-            nc.scalar.activation(out=de[:, 1, :], in_=T[i]["u"][:], func=ACT.Abs, bias=0.5, scale=2.5)
-            T[i]["de"] = de
+        def a1_(k, j):
+            nc.scalar.activation(out=T[k]["de"][:, j, 1, :], in_=T[k]["u"][:, j, :], func=ACT.Abs, bias=0.5, scale=2.5)
 
-        def a2_(i):
-            e = T[i]["de"][:, 1, :]
+        def a2_(k, j):
+            e = T[k]["de"][:, j, 1, :]
             nc.scalar.activation(out=e, in_=e, func=ACT.Abs, bias=-2.0, scale=1.0)
 
-        def a3_(i):
-            e = T[i]["de"][:, 1, :]
+        def a3_(k, j):
+            e = T[k]["de"][:, j, 1, :]
             nc.scalar.activation(out=e, in_=e, func=ACT.Abs, bias=-1.0, scale=1.0)
 
-        def sqd_(i):
-            f = UNITS[i] * P
-            sq = ew.tile([P, 2, f], F32, tag="sq")
-            nc.scalar.activation(out=sq[:, 0, :], in_=T[i]["de"][:, 1, :], func=ACT.Square, bias=r6, scale=-r6)
-            T[i]["sq"] = sq
+        def da_(k):
+            de = T[k]["de"]
+            nc.scalar.activation(out=de[:, :, 0, :], in_=de[:, :, 1, :], func=ACT.Identity, bias=1.0, scale=-1.0)
 
-        def sqe_(i):
-            nc.scalar.activation(out=T[i]["sq"][:, 1, :], in_=T[i]["de"][:, 1, :], func=ACT.Square, bias=0.0, scale=r6)
+        def sq_(k):
+            nu, f = dims(k)
+            sq = ew.tile([P, nu, 2, f], F32, tag="sq")
+            nc.scalar.activation(out=sq[:], in_=T[k]["de"][:], func=ACT.Square, bias=0.0, scale=r6)
+            T[k]["sq"] = sq
 
-        def da_(i):
-            de = T[i]["de"]
-            nc.scalar.activation(out=de[:, 0, :], in_=de[:, 1, :], func=ACT.Identity, bias=1.0, scale=-1.0)
+        def ring_(k):
+            nu, f = dims(k)
+            ring = ew.tile([P, nu, 2, f], BF16, tag="ring", bufs=1)
+            nc.vector.tensor_tensor(out=ring[:], in0=T[k]["sq"][:], in1=T[k]["de"][:], op=ALU.mult)
+            T[k]["ring"] = ring
 
-        def ia_(i):
-            f = UNITS[i] * P
-            inner = ew.tile([P, 2, f], BF16, tag="inner", bufs=2)
-            nc.scalar.activation(out=inner[:], in_=T[i]["w"][:], func=ACT.Identity, bias=2.0 / 3.0, scale=3.0)
-            T[i]["inner"] = inner
+        def w_(k):
+            sq = T[k]["sq"]
+            nc.vector.scalar_tensor_tensor(
+                out=sq[:].rearrange("p a k f -> p (a k f)"), in0=T[k]["de"][:].rearrange("p a k f -> p (a k f)"), scalar=2.0,
+                in1=sq[:].rearrange("p a k f -> p (a k f)"), op0=ALU.subtract, op1=ALU.mult,
+            )
 
-        def d_(i):
-            de = T[i]["de"]
-            nc.vector.tensor_scalar(out=de[:, 0, :], in0=de[:, 1, :], scalar1=-1.0, scalar2=1.0, op0=ALU.mult, op1=ALU.add)
+        def inner_(k):
+            nu, f = dims(k)
+            inner = ew.tile([P, nu, 2, f], BF16, tag="inner", bufs=1)
+            nc.vector.tensor_scalar(out=inner[:], in0=T[k]["sq"][:], scalar1=3.0, scalar2=2.0 / 3.0, op0=ALU.mult, op1=ALU.add)
+            T[k]["inner"] = inner
 
-        def ring_(i):
-            f = UNITS[i] * P
-            ring = ew.tile([P, 2, f], BF16, tag="ring", bufs=2)
-            nc.vector.tensor_tensor(out=ring[:], in0=T[i]["sq"][:], in1=T[i]["de"][:], op=ALU.mult)
-            T[i]["ring"] = ring
-
-        def w0_(i):
-            f = UNITS[i] * P
-            w = ew.tile([P, 2, f], F32, tag="w", bufs=2)
-            nc.vector.scalar_tensor_tensor(out=w[:, 0, :], in0=T[i]["sq"][:, 1, :], scalar=1.0 / 6.0, in1=T[i]["de"][:, 0, :], op0=ALU.subtract, op1=ALU.mult)
-            T[i]["w"] = w
-
-        def w1_(i):
-            nc.vector.scalar_tensor_tensor(out=T[i]["w"][:, 1, :], in0=T[i]["sq"][:, 0, :], scalar=1.0 / 6.0, in1=T[i]["de"][:, 1, :], op0=ALU.subtract, op1=ALU.mult)
-
-        def inner_(i):
-            f = UNITS[i] * P
-            inner = ew.tile([P, 2, f], BF16, tag="inner", bufs=2)
-            nc.vector.tensor_scalar(out=inner[:], in0=T[i]["w"][:], scalar1=3.0, scalar2=2.0 / 3.0, op0=ALU.mult, op1=ALU.add)
-            T[i]["inner"] = inner
-
-        def gam_(i):
-            f = UNITS[i] * P
-            gam = ew.tile([P, 4, f], BF16, tag="gam", bufs=2)
+        def gam_(k):
+            nu, f = dims(k)
+            gam = ew.tile([P, nu, 4, f], BF16, tag="gam", bufs=1)
             for s in range(4):
-                nc.vector.tensor_scalar(out=gam[:, s, :], in0=T[i]["u"][:], scalar1=0.4 * (TS[s] + 1) - 1.0, scalar2=None, op0=ALU.is_gt)
-            T[i]["gam"] = gam
+                nc.vector.tensor_scalar(out=gam[:, :, s, :], in0=T[k]["u"][:], scalar1=0.4 * (TS[s] + 1) - 1.0, scalar2=None, op0=ALU.is_gt)
+            T[k]["gam"] = gam
 
-        def beta_(i):
-            f = UNITS[i] * P
-            gam = T[i]["gam"]
-            beta = ew.tile([P, 2, f], BF16, tag="beta", bufs=2)
-            for k in range(2):
-                nc.vector.tensor_tensor(out=beta[:, k, :], in0=gam[:, SLOT[k], :], in1=gam[:, SLOT[k + 2], :], op=ALU.subtract)
-            T[i]["beta"] = beta
+        def beta_(k):
+            nu, f = dims(k)
+            gam = T[k]["gam"]
+            beta = ew.tile([P, nu, 2, f], BF16, tag="beta", bufs=1)
+            for c in range(2):
+                nc.vector.tensor_tensor(out=beta[:, :, c, :], in0=gam[:, :, SLOT[c], :], in1=gam[:, :, SLOT[c + 2], :], op=ALU.subtract)
+            T[k]["beta"] = beta
+            T[k]["v"] = ew.tile([P, nu, 4, f], BF16, tag="v", bufs=1, name="v")
+            T[k]["planes"] = ew.tile([P, nu, 2, 4, f], BF16, tag="planes", name="planes")
 
-        def p1_(i):
-            f = UNITS[i] * P
-            v = ew.tile([P, 4, f], BF16, tag="v", bufs=2)
-            nc.vector.tensor_tensor(out=v[:, 0:2, :], in0=T[i]["beta"][:], in1=T[i]["inner"][:], op=ALU.mult)
-            T[i]["v"] = v
+        def p1_(k, j):
+            nc.vector.tensor_tensor(out=T[k]["v"][:, j, 0:2, :], in0=T[k]["beta"][:, j], in1=T[k]["inner"][:, j], op=ALU.mult)
 
-        def p0_(i):
-            v = T[i]["v"]
-            nc.vector.tensor_tensor(out=v[:, 2:4, :], in0=T[i]["inner"][:], in1=v[:, 0:2, :], op=ALU.subtract)
+        def p0_(k, j):
+            nc.vector.tensor_tensor(out=T[k]["v"][:, j, 2:4, :], in0=T[k]["inner"][:, j], in1=T[k]["v"][:, j, 0:2, :], op=ALU.subtract)
 
-        def max_(i):
-            f = UNITS[i] * P
-            v4 = T[i]["v"][:].rearrange("p (r k) f -> p r (k f)", r=2)
-            nc.vector.tensor_tensor(out=v4, in0=v4, in1=T[i]["ring"][:].rearrange("p k f -> p (k f)").unsqueeze(1).to_broadcast([P, 2, 2 * f]), op=ALU.max)
+        def max_(k, j):
+            f = GROUPS[k][j] * P
+            v4 = T[k]["v"][:, j].rearrange("p (r k) f -> p r (k f)", r=2)
+            nc.vector.tensor_tensor(out=v4, in0=v4, in1=T[k]["ring"][:, j].rearrange("p k f -> p (k f)").unsqueeze(1).to_broadcast([P, 2, 2 * f]), op=ALU.max)
 
-        def hi_(i):
-            f = UNITS[i] * P
-            planes = ew.tile([P, 2, 4, f], BF16, tag="planes", bufs=4)
-            nc.vector.tensor_tensor(out=planes[:, 1], in0=T[i]["v"][:], in1=T[i]["gam"][:], op=ALU.mult)
-            T[i]["planes"] = planes
-            gr = be.tile([P, 2, 4 * f], BF16, tag="gr", bufs=4, align_bytes=64)
-            T[i]["gr"] = gr
+        def hi_(k, j):
+            nc.vector.tensor_tensor(out=T[k]["planes"][:, j, 1], in0=T[k]["v"][:, j], in1=T[k]["gam"][:, j], op=ALU.mult)
 
-        def lo_(i):
-            planes = T[i]["planes"]
-            nc.vector.tensor_tensor(out=planes[:, 0], in0=T[i]["v"][:], in1=planes[:, 1], op=ALU.subtract)
+        def lo_(k, j):
+            nc.vector.tensor_tensor(out=T[k]["planes"][:, j, 0], in0=T[k]["v"][:, j], in1=T[k]["planes"][:, j, 1], op=ALU.subtract)
 
-        def rg(i, g, eng):
-            dst = T[i]["gr"][:, g, :].rearrange("p (c i s) -> p c s i", i=4, s=4)
-            srcp = T[i]["planes"][:, g].rearrange("p s (c i) -> p c s i", i=4)
-            if eng == "act":
-                nc.scalar.copy(out=dst, in_=srcp)
-            else:
-                nc.vector.tensor_copy(out=dst, in_=srcp)
-
-        def rgs(k, eng):
-            for i in units(k):
+        def rgs(k, eng, js=(0, 1, 2, 3)):
+            for j in range(nun(k)):
+                if j not in js:
+                    continue
+                if eng == "act" or (k, 1) in RG_V:
+                    if ("gr", j) not in T[k]:
+                        T[k][("gr", j)] = be.tile([P, 2, 4 * GROUPS[k][j] * P], BF16, tag="gr", bufs=4, align_bytes=64, name="gr")
                 for g in (1, 0):
                     if ((k, g) in RG_V) == (eng == "v"):
-                        rg(i, g, eng)
+                        dst = T[k][("gr", j)][:, g, :].rearrange("p (c i s) -> p c s i", i=4, s=4)
+                        srcp = T[k]["planes"][:, j, g].rearrange("p s (c i) -> p c s i", i=4)
+                        if eng == "act":
+                            nc.scalar.copy(out=dst, in_=srcp)
+                        else:
+                            nc.vector.tensor_copy(out=dst, in_=srcp)
 
-        def q_(i):
-            n = UNITS[i] * P
-            bcodes = be.tile([P, 2, n], U32, tag="bcodes", align_bytes=64)
-            bscales = be.tile([P, 2, n], U8, tag="bscales", align_bytes=64)
+        def q_(k, j):
+            n = GROUPS[k][j] * P
+            bcodes = be.tile([P, 2, n], U32, tag="bcodes", bufs=4, align_bytes=64)
+            bscales = be.tile([P, 2, n], U8, tag="bscales", bufs=4, align_bytes=64)
             nc.vector.quantize_mx(
                 out=bcodes[:].rearrange("p g w -> p (g w)").bitcast(FP8X4),
                 scales=bscales[:].rearrange("p g w -> p (g w)"),
-                in_=T[i]["gr"][:].rearrange("p g k -> p (g k)"),
+                in_=T[k][("gr", j)][:].rearrange("p g k -> p (g k)"),
             )
-            T[i]["mx"] = []
+            mxs = []
             for h in range(2):
-                mx = psum.tile([P, n], F32, tag="mx", bufs=3)
+                mx = psum.tile([P, n], F32, tag="mx", bufs=4)
                 for g in range(2):
                     nc.tensor.matmul_mx(
                         out=mx[:],
@@ -294,51 +274,59 @@ def tile_bsplinebasis_v2_t_kernel(tc, x, spline_coeffs, residual_weight, residua
                         start=(g == 0),
                         stop=(g == 1),
                     )
-                T[i]["mx"].append(mx)
+                mxs.append(mx)
+            T[k][("mx", j)] = mxs
 
-        def t1_(i):
-            s = UNITS[i]
+        def t1_(k, j):
+            s = GROUPS[k][j]
+            n0 = GSTART[k] + sum(GROUPS[k][:j])
             t1s = []
             for h in range(2):
                 t1 = be.tile([P, s * P], F32, tag="t1_%d" % h)
-                nc.scalar.activation(out=t1[:], in_=T[i]["mx"][h][:], func=ACT.Identity, bias=bias[:, h:h + 1], scale=scale[:, h:h + 1])
+                nc.scalar.activation(out=t1[:], in_=T[k][("mx", j)][h][:], func=ACT.Identity, bias=bias[:, h:h + 1], scale=scale[:, h:h + 1])
                 t1s.append(t1)
-            T[i]["ot"] = []
+            ots = []
             for k0 in range(0, s, 2):
                 kn = min(2, s - k0)
-                ot = psum.tile([P, kn, O], F32, tag="ot", bufs=4)
+                ot = psum.tile([P, kn, O], F32, tag="ot", bufs=3)
                 for q in range(kn):
                     n = k0 + q
                     for h in range(2):
                         dsto = ot[:, q, h * P:(h + 1) * P]
-                        nc.tensor.matmul(out=dsto, lhsT=xT[:, STARTS[i] + n, :], rhs=rwT[:, h, :], start=True, stop=False)
+                        nc.tensor.matmul(out=dsto, lhsT=xT[:, n0 + n, :], rhs=rwT[:, h, :], start=True, stop=False)
                         nc.tensor.matmul(out=dsto, lhsT=t1s[h][:, n * P:(n + 1) * P], rhs=ident_f[:], is_transpose=True, start=False, stop=True)
-                T[i]["ot"].append((k0, kn, ot))
+                ots.append((k0, kn, ot))
+            T[k][("ot", j)] = ots
 
-        def ev_(i):
-            s = UNITS[i]
+        def ev_(k, j):
+            s = GROUPS[k][j]
+            n0 = GSTART[k] + sum(GROUPS[k][:j])
             osb = be.tile([P, s, O], F32, tag="osb", bufs=3)
-            for k0, kn, ot in T[i]["ot"]:
+            for k0, kn, ot in T[k][("ot", j)]:
                 nc.scalar.copy(out=osb[:, k0:k0 + kn, :], in_=ot[:])
-            nc.sync.dma_start(out=out_v[:, STARTS[i]:STARTS[i] + s, :], in_=osb[:])
+            nc.sync.dma_start(out=out_v[:, n0:n0 + s, :], in_=osb[:])
 
-        for k in range(-3, NG + 2):
-            each(k + 3, xp_)
-            tx_(k + 3)
-            rgs(k - 1, "act")
-            each(k, ring_, w0_, w1_)
-            each(k + 1, a1_, a2_, a3_)
-            rgs(k - 1, "v")
-            one(k - 1, 0, q_)
-            each(k, inner_, gam_)
-            one(k - 1, 0, t1_)
-            one(k - 1, 1, q_)
-            each(k + 1, sqd_, sqe_, da_)
-            each(k, beta_, p1_, p0_, max_)
-            one(k - 1, 1, t1_)
-            evx_(k + 3)
-            each(k, hi_, lo_)
-            each(k - 1, ev_)
-            each(k + 2, u_)
+        for k in range(-3, NG + 3):
+            grp(k + 3, xp_)
+            rgs(k - 1, "act", (0,))
+            grp(k, ring_, w_)
+            late(k, 0, t1_)
+            rgs(k - 1, "act", (1,))
+            grp(k, gam_, inner_, beta_)
+            late(k, 0, ev_)
+            late(k, 1, t1_)
+            alt(k + 1, a1_, a2_, a3_)
+            grp(k + 2, u_)
+            late(k, 1, ev_)
+            grp(k + 1, da_)
+            grp(k + 3, evx_)
+            grp(k + 1, sq_)
+            alt(k, p1_, p0_, max_, hi_, lo_)
+            if not early(k - 1):
+                rgs(k - 1, "v")
+                alt(k - 1, q_)
+            if early(k):
+                rgs(k, "v")
+                alt(k, q_)
             if k == W_AT:
                 weights()

@@ -21,7 +21,7 @@ GSTART = [sum(sum(grp) for grp in GROUPS[:k]) for k in range(NG)]
 TS = (3, 0, 1, 2)
 SLOT = (1, 2, 3, 0)
 RG_V = ((10, 0), (10, 1), (9, 0), (9, 1))
-W_AT = 0
+W_AT = 1
 FLOPS = 2 * B * I * NBAS * O + 2 * B * I * O
 assert sum(sum(grp) for grp in GROUPS) == NT
 
@@ -36,6 +36,10 @@ def tile_bsplinebasis_v2_t_kernel(tc, x, spline_coeffs, residual_weight, residua
         be = ctx.enter_context(tc.tile_pool(name="be", bufs=2))
         psum = ctx.enter_context(tc.psum_pool(name="psum", bufs=1))
         ctx.enter_context(tc.manual_schedule())
+
+        warm = const.tile([P, 1], F32)
+        nc.vector.memset(warm[:], 0.0)
+        nc.scalar.activation(out=warm[:], in_=warm[:], func=ACT.Abs, bias=0.0, scale=1.0)
 
         x_sb = const.tile([P, NT, I], BF16)
         xT = const.tile([P, NT, P], BF16)
@@ -68,17 +72,18 @@ def tile_bsplinebasis_v2_t_kernel(tc, x, spline_coeffs, residual_weight, residua
         bias = const.tile([P, 2], F32)
         scale = const.tile([P, 2], F32)
 
+        rwp = setup.tile([P, 2, I], BF16)
+        nc.gpsimd.tensor_copy(
+            out=rwp[:].rearrange("p h (c a m e) -> p (h c) a m e", c=2, a=4, m=4, e=4),
+            in_=rw_sb[:].rearrange("p h (c m a e) -> p (h c) a m e", c=2, m=4, a=4, e=4),
+        )
+        cpm = setup.tile([P, 2, I * NBAS], BF16)
+        nc.gpsimd.tensor_copy(
+            out=cpm[:].rearrange("p h (c a m k) -> p (h c) a m k", c=2, a=4, m=4, k=32),
+            in_=c_sb[:].rearrange("p h (c m a k) -> p (h c) a m k", c=2, m=4, a=4, k=32),
+        )
+
         def weights():
-            cpm = setup.tile([P, 2, I * NBAS], BF16)
-            nc.vector.tensor_copy(
-                out=cpm[:].rearrange("p h (c a m k) -> p (h c) a m k", c=2, a=4, m=4, k=32),
-                in_=c_sb[:].rearrange("p h (c m a k) -> p (h c) a m k", c=2, m=4, a=4, k=32),
-            )
-            rwp = setup.tile([P, 2, I], BF16)
-            nc.vector.tensor_copy(
-                out=rwp[:].rearrange("p h (c a m e) -> p (h c) a m e", c=2, a=4, m=4, e=4),
-                in_=rw_sb[:].rearrange("p h (c m a e) -> p (h c) a m e", c=2, m=4, a=4, e=4),
-            )
             tpr = psum.tile([P, 3, P], BF16, tag="mx", bufs=4)
             for h in range(2):
                 nc.tensor.transpose(tpr[:, h, :], rwp[:, h, :], ident_b[:])
@@ -322,11 +327,11 @@ def tile_bsplinebasis_v2_t_kernel(tc, x, spline_coeffs, residual_weight, residua
             grp(k + 3, evx_)
             grp(k + 1, sq_)
             alt(k, p1_, p0_, max_, hi_, lo_)
+            if k == W_AT:
+                weights()
             if not early(k - 1):
                 rgs(k - 1, "v")
                 alt(k - 1, q_)
             if early(k):
                 rgs(k, "v")
                 alt(k, q_)
-            if k == W_AT:
-                weights()

@@ -21,7 +21,7 @@ GSTART = [sum(sum(grp) for grp in GROUPS[:k]) for k in range(NG)]
 TS = (3, 0, 1, 2)
 SLOT = (1, 2, 3, 0)
 RG_V = ((10, 0), (10, 1), (9, 0), (9, 1))
-W_AT = 1
+W_AT = 0
 FLOPS = 2 * B * I * NBAS * O + 2 * B * I * O
 assert sum(sum(grp) for grp in GROUPS) == NT
 
@@ -72,18 +72,17 @@ def tile_bsplinebasis_v2_t_kernel(tc, x, spline_coeffs, residual_weight, residua
         bias = const.tile([P, 2], F32)
         scale = const.tile([P, 2], F32)
 
-        rwp = setup.tile([P, 2, I], BF16)
-        nc.gpsimd.tensor_copy(
-            out=rwp[:].rearrange("p h (c a m e) -> p (h c) a m e", c=2, a=4, m=4, e=4),
-            in_=rw_sb[:].rearrange("p h (c m a e) -> p (h c) a m e", c=2, m=4, a=4, e=4),
-        )
-        cpm = setup.tile([P, 2, I * NBAS], BF16)
-        nc.gpsimd.tensor_copy(
-            out=cpm[:].rearrange("p h (c a m k) -> p (h c) a m k", c=2, a=4, m=4, k=32),
-            in_=c_sb[:].rearrange("p h (c m a k) -> p (h c) a m k", c=2, m=4, a=4, k=32),
-        )
-
         def weights():
+            cpm = setup.tile([P, 2, I * NBAS], BF16)
+            nc.vector.tensor_copy(
+                out=cpm[:].rearrange("p h (c a m k) -> p (h c) a m k", c=2, a=4, m=4, k=32),
+                in_=c_sb[:].rearrange("p h (c m a k) -> p (h c) a m k", c=2, m=4, a=4, k=32),
+            )
+            rwp = setup.tile([P, 2, I], BF16)
+            nc.vector.tensor_copy(
+                out=rwp[:].rearrange("p h (c a m e) -> p (h c) a m e", c=2, a=4, m=4, e=4),
+                in_=rw_sb[:].rearrange("p h (c m a e) -> p (h c) a m e", c=2, m=4, a=4, e=4),
+            )
             tpr = psum.tile([P, 3, P], BF16, tag="mx", bufs=4)
             for h in range(2):
                 nc.tensor.transpose(tpr[:, h, :], rwp[:, h, :], ident_b[:])
@@ -327,11 +326,11 @@ def tile_bsplinebasis_v2_t_kernel(tc, x, spline_coeffs, residual_weight, residua
             grp(k + 3, evx_)
             grp(k + 1, sq_)
             alt(k, p1_, p0_, max_, hi_, lo_)
-            if k == W_AT:
-                weights()
             if not early(k - 1):
                 rgs(k - 1, "v")
                 alt(k - 1, q_)
             if early(k):
                 rgs(k, "v")
                 alt(k, q_)
+            if k == W_AT:
+                weights()

@@ -18,10 +18,9 @@ NT = B // P
 GROUPS = [[1, 1], [2, 2]] + [[4, 4]] * 6 + [[2, 2], [2, 2], [1, 1]]
 NG = len(GROUPS)
 GSTART = [sum(sum(grp) for grp in GROUPS[:k]) for k in range(NG)]
-TS = (3, 0, 1, 2)
-SLOT = (1, 2, 3, 0)
-RG_V = ((10, 0), (10, 1), (9, 0), (9, 1))
-W_AT = 0
+SHORT = 2
+J_OF_SLOT = (3, 0, 1, 2)
+SLOT_OF_J = (1, 2, 3, 0)
 FLOPS = 2 * B * I * NBAS * O + 2 * B * I * O
 assert sum(sum(grp) for grp in GROUPS) == NT
 
@@ -37,18 +36,14 @@ def tile_bsplinebasis_v2_t_kernel(tc, x, spline_coeffs, residual_weight, residua
         psum = ctx.enter_context(tc.psum_pool(name="psum", bufs=1))
         ctx.enter_context(tc.manual_schedule())
 
-        warm = const.tile([P, 1], F32)
-        nc.vector.memset(warm[:], 0.0)
-        nc.scalar.activation(out=warm[:], in_=warm[:], func=ACT.Abs, bias=0.0, scale=1.0)
-
         x_sb = const.tile([P, NT, I], BF16)
         xT = const.tile([P, NT, P], BF16)
         x_v = x.rearrange("(p n) i -> p n i", n=NT)
         out_v = out.rearrange("(p n) o -> p n o", n=NT)
         for k in range(NG):
-            a = GSTART[k]
-            b = a + sum(GROUPS[k])
-            nc.sync.dma_start(out=x_sb[:, a:b, :], in_=x_v[:, a:b, :])
+            n0 = GSTART[k]
+            n1 = n0 + sum(GROUPS[k])
+            nc.sync.dma_start(out=x_sb[:, n0:n1, :], in_=x_v[:, n0:n1, :])
 
         ident_b = const.tile([P, P], BF16)
         make_identity(nc, ident_b[:])
@@ -72,202 +67,197 @@ def tile_bsplinebasis_v2_t_kernel(tc, x, spline_coeffs, residual_weight, residua
         bias = const.tile([P, 2], F32)
         scale = const.tile([P, 2], F32)
 
-        def weights():
+        wt = dict()
+
+        def weights_transpose():
             cpm = setup.tile([P, 2, I * NBAS], BF16)
             nc.vector.tensor_copy(
-                out=cpm[:].rearrange("p h (c a m k) -> p (h c) a m k", c=2, a=4, m=4, k=32),
-                in_=c_sb[:].rearrange("p h (c m a k) -> p (h c) a m k", c=2, m=4, a=4, k=32),
+                out=cpm[:].rearrange("p h (c a m z) -> p (h c) a m z", c=2, a=4, m=4, z=4 * NBAS),
+                in_=c_sb[:].rearrange("p h (c m a z) -> p (h c) a m z", c=2, m=4, a=4, z=4 * NBAS),
             )
             rwp = setup.tile([P, 2, I], BF16)
             nc.vector.tensor_copy(
-                out=rwp[:].rearrange("p h (c a m e) -> p (h c) a m e", c=2, a=4, m=4, e=4),
-                in_=rw_sb[:].rearrange("p h (c m a e) -> p (h c) a m e", c=2, m=4, a=4, e=4),
+                out=rwp[:].rearrange("p h (c a m l) -> p (h c) a m l", c=2, a=4, m=4, l=4),
+                in_=rw_sb[:].rearrange("p h (c m a l) -> p (h c) a m l", c=2, m=4, a=4, l=4),
             )
             tpr = psum.tile([P, 3, P], BF16, tag="mx", bufs=4)
             for h in range(2):
                 nc.tensor.transpose(tpr[:, h, :], rwp[:, h, :], ident_b[:])
             nc.tensor.transpose(tpr[:, 2, :], b_sb[:], ident_b[:])
-            nc.vector.tensor_copy(out=rwT[:], in_=tpr[:, 0:2, :])
-            nc.vector.tensor_copy(out=bias[:], in_=tpr[:, 2, 0:2])
+            wt["tpr"] = tpr
+            for h in range(2):
+                tpc = psum.tile([P, NBAS, P], BF16, tag="mx", bufs=4)
+                for q in range(NBAS):
+                    j = 4 * (q // 4) + J_OF_SLOT[q % 4]
+                    nc.tensor.transpose(tpc[:, q, :], cpm[:, h, :].rearrange("p (r j) -> p j r", j=NBAS)[:, j], ident_b[:])
+                wt[h] = tpc
+
+        def weights_finish():
+            nc.vector.tensor_copy(out=rwT[:], in_=wt["tpr"][:, 0:2, :])
+            nc.vector.tensor_copy(out=bias[:], in_=wt["tpr"][:, 2, 0:2])
             ssum = setup.tile([P, 2], F32)
             nc.vector.tensor_reduce(out=ssum[:], in_=sb_sb[:], axis=mybir.AxisListType.X, op=ALU.add)
             nc.vector.tensor_scalar(out=scale[:], in0=ssum[:], scalar1=1.0 / I, scalar2=None, op0=ALU.mult)
             for h in range(2):
-                tpc = psum.tile([P, NBAS, P], BF16, tag="mx", bufs=4)
-                for q in range(NBAS):
-                    j = 4 * (q // 4) + TS[q % 4]
-                    nc.tensor.transpose(tpc[:, q, :], cpm[:, h, :].rearrange("p (r j) -> p j r", j=NBAS)[:, j], ident_b[:])
                 nc.vector.tensor_copy(
-                    out=cgr[:, :, h * 512:(h + 1) * 512].rearrange("p g (w s) -> p g w s", s=4),
-                    in_=tpc[:].rearrange("p (g s) w -> p g w s", s=4),
+                    out=cgr[:, :, h * 4 * P:(h + 1) * 4 * P].rearrange("p g (w s) -> p g w s", s=4),
+                    in_=wt[h][:].rearrange("p (g s) w -> p g w s", s=4),
                 )
             nc.vector.quantize_mx(
                 out=ccodes[:].rearrange("p g o -> p (g o)").bitcast(FP8X4),
                 scales=cscales[:].rearrange("p g o -> p (g o)"),
-                in_=cgr[:].rearrange("p g k -> p (g k)"),
+                in_=cgr[:].rearrange("p g w -> p (g w)"),
             )
 
-        T = [dict() for k in range(NG)]
+        tiles = [dict() for k in range(NG)]
 
-        def ok(k):
+        def exists(k):
             return 0 <= k < NG
 
-        def nun(k):
-            return len(GROUPS[k]) if ok(k) else 0
+        def units(k):
+            return len(GROUPS[k]) if exists(k) else 0
 
         def dims(k):
             return len(GROUPS[k]), GROUPS[k][0] * P
 
-        def grp(k, *ops):
-            if ok(k):
-                for op in ops:
-                    op(k)
+        def short(k):
+            return exists(k) and k >= NG - SHORT
 
-        def alt(k, *ops):
-            for op in ops:
-                for j in range(nun(k)):
-                    op(k, j)
 
-        def one(k, j, *ops):
-            if j < nun(k):
-                for op in ops:
-                    op(k, j)
-
-        def early(k):
-            return (k, 0) in RG_V and (k, 1) in RG_V
-
-        def late(k, j, op):
-            if ok(k - 2) and not early(k - 2):
-                one(k - 2, j, op)
-            if ok(k - 1) and early(k - 1):
-                one(k - 1, j, op)
-
-        def xp_(k):
-            s, n0 = sum(GROUPS[k]), GSTART[k]
-            xp = ew.tile([P, s, I], BF16, tag="xp")
+        def transpose_x(k):
+            nt, n0 = sum(GROUPS[k]), GSTART[k]
+            xp = ew.tile([P, nt, I], BF16, tag="xp")
             nc.vector.tensor_copy(
-                out=xp[:].rearrange("p n (c a m e) -> p (n c) a m e", c=2, a=4, m=4, e=4),
-                in_=x_sb[:, n0:n0 + s, :].rearrange("p n (c m a e) -> p (n c) a m e", c=2, m=4, a=4, e=4),
+                out=xp[:].rearrange("p n (c a m l) -> p (n c) a m l", c=2, a=4, m=4, l=4),
+                in_=x_sb[:, n0:n0 + nt, :].rearrange("p n (c m a l) -> p (n c) a m l", c=2, m=4, a=4, l=4),
             )
-            tpx = psum.tile([P, s, P], BF16, tag="tp")
-            for n in range(s):
+            tpx = psum.tile([P, nt, P], BF16, tag="tp")
+            for n in range(nt):
                 nc.tensor.transpose(tpx[:, n, :], xp[:, n, :], ident_b[:])
-            T[k]["tpx"] = tpx
+            tiles[k]["tpx"] = tpx
 
-        def evx_(k):
-            s, n0 = sum(GROUPS[k]), GSTART[k]
-            nc.scalar.copy(out=xT[:, n0:n0 + s, :], in_=T[k]["tpx"][:])
+        def keep_xT(k):
+            nt, n0 = sum(GROUPS[k]), GSTART[k]
+            nc.scalar.copy(out=xT[:, n0:n0 + nt, :], in_=tiles[k]["tpx"][:])
 
-        def u_(k):
-            s, n0 = sum(GROUPS[k]), GSTART[k]
+        def clamp(k):
+            nt, n0 = sum(GROUPS[k]), GSTART[k]
             nu, f = dims(k)
             u = ew.tile([P, nu, f], BF16, tag="u", bufs=3)
-            nc.vector.tensor_scalar(out=u[:].rearrange("p a f -> p (a f)"), in0=xT[:, n0:n0 + s, :].rearrange("p n w -> p (n w)"), scalar1=-1.0, scalar2=1.0, op0=ALU.max, op1=ALU.min)
-            T[k]["u"] = u
-            T[k]["de"] = ew.tile([P, nu, 2, f], F32, tag="de", name="de")
+            nc.vector.tensor_scalar(
+                out=u[:].rearrange("p d f -> p (d f)"), in0=xT[:, n0:n0 + nt, :].rearrange("p n w -> p (n w)"),
+                scalar1=-1.0, scalar2=1.0, op0=ALU.max, op1=ALU.min,
+            )
+            tiles[k]["u"] = u
+            tiles[k]["de"] = ew.tile([P, nu, 2, f], F32, tag="de", name="de")
 
-        def a1_(k, j):
-            nc.scalar.activation(out=T[k]["de"][:, j, 1, :], in_=T[k]["u"][:, j, :], func=ACT.Abs, bias=0.5, scale=2.5)
+        def fold_1(k, un):
+            nc.scalar.activation(out=tiles[k]["de"][:, un, 1, :], in_=tiles[k]["u"][:, un, :], func=ACT.Abs, bias=0.5, scale=2.5)
 
-        def a2_(k, j):
-            e = T[k]["de"][:, j, 1, :]
-            nc.scalar.activation(out=e, in_=e, func=ACT.Abs, bias=-2.0, scale=1.0)
+        def fold_2(k, un):
+            d_odd = tiles[k]["de"][:, un, 1, :]
+            nc.scalar.activation(out=d_odd, in_=d_odd, func=ACT.Abs, bias=-2.0, scale=1.0)
 
-        def a3_(k, j):
-            e = T[k]["de"][:, j, 1, :]
-            nc.scalar.activation(out=e, in_=e, func=ACT.Abs, bias=-1.0, scale=1.0)
+        def fold_3(k, un):
+            d_odd = tiles[k]["de"][:, un, 1, :]
+            nc.scalar.activation(out=d_odd, in_=d_odd, func=ACT.Abs, bias=-1.0, scale=1.0)
 
-        def da_(k):
-            de = T[k]["de"]
+        def other_distance(k):
+            de = tiles[k]["de"]
             nc.scalar.activation(out=de[:, :, 0, :], in_=de[:, :, 1, :], func=ACT.Identity, bias=1.0, scale=-1.0)
 
-        def sq_(k):
+        def squares(k):
             nu, f = dims(k)
             sq = ew.tile([P, nu, 2, f], F32, tag="sq")
-            nc.scalar.activation(out=sq[:], in_=T[k]["de"][:], func=ACT.Square, bias=0.0, scale=r6)
-            T[k]["sq"] = sq
+            nc.scalar.activation(out=sq[:], in_=tiles[k]["de"][:], func=ACT.Square, bias=0.0, scale=r6)
+            tiles[k]["sq"] = sq
 
-        def ring_(k):
+        def ring_piece(k):
             nu, f = dims(k)
             ring = ew.tile([P, nu, 2, f], BF16, tag="ring", bufs=1)
-            nc.vector.tensor_tensor(out=ring[:], in0=T[k]["sq"][:], in1=T[k]["de"][:], op=ALU.mult)
-            T[k]["ring"] = ring
+            nc.vector.tensor_tensor(out=ring[:], in0=tiles[k]["sq"][:], in1=tiles[k]["de"][:], op=ALU.mult)
+            tiles[k]["ring"] = ring
 
-        def w_(k):
-            sq = T[k]["sq"]
+        def inner_cubic(k):
+            sq = tiles[k]["sq"]
             nc.vector.scalar_tensor_tensor(
-                out=sq[:].rearrange("p a k f -> p (a k f)"), in0=T[k]["de"][:].rearrange("p a k f -> p (a k f)"), scalar=2.0,
-                in1=sq[:].rearrange("p a k f -> p (a k f)"), op0=ALU.subtract, op1=ALU.mult,
+                out=sq[:].rearrange("p d y f -> p (d y f)"), in0=tiles[k]["de"][:].rearrange("p d y f -> p (d y f)"), scalar=2.0,
+                in1=sq[:].rearrange("p d y f -> p (d y f)"), op0=ALU.subtract, op1=ALU.mult,
             )
 
-        def inner_(k):
+        def inner_piece(k):
             nu, f = dims(k)
             inner = ew.tile([P, nu, 2, f], BF16, tag="inner", bufs=1)
-            nc.vector.tensor_scalar(out=inner[:], in0=T[k]["sq"][:], scalar1=3.0, scalar2=2.0 / 3.0, op0=ALU.mult, op1=ALU.add)
-            T[k]["inner"] = inner
+            nc.vector.tensor_scalar(out=inner[:], in0=tiles[k]["sq"][:], scalar1=3.0, scalar2=2.0 / 3.0, op0=ALU.mult, op1=ALU.add)
+            tiles[k]["inner"] = inner
 
-        def gam_(k):
+        def knot_masks(k):
             nu, f = dims(k)
             gam = ew.tile([P, nu, 4, f], BF16, tag="gam", bufs=1)
             for s in range(4):
-                nc.vector.tensor_scalar(out=gam[:, :, s, :], in0=T[k]["u"][:], scalar1=0.4 * (TS[s] + 1) - 1.0, scalar2=None, op0=ALU.is_gt)
-            T[k]["gam"] = gam
+                nc.vector.tensor_scalar(
+                    out=gam[:, :, s, :], in0=tiles[k]["u"][:], scalar1=0.4 * (J_OF_SLOT[s] + 1) - 1.0, scalar2=None, op0=ALU.is_gt,
+                )
+            tiles[k]["gam"] = gam
 
-        def beta_(k):
+        def near_masks(k):
             nu, f = dims(k)
-            gam = T[k]["gam"]
+            gam = tiles[k]["gam"]
             beta = ew.tile([P, nu, 2, f], BF16, tag="beta", bufs=1)
-            for c in range(2):
-                nc.vector.tensor_tensor(out=beta[:, :, c, :], in0=gam[:, :, SLOT[c], :], in1=gam[:, :, SLOT[c + 2], :], op=ALU.subtract)
-            T[k]["beta"] = beta
-            T[k]["v"] = ew.tile([P, nu, 4, f], BF16, tag="v", bufs=1, name="v")
-            T[k]["planes"] = ew.tile([P, nu, 2, 4, f], BF16, tag="planes", name="planes")
+            for y in range(2):
+                nc.vector.tensor_tensor(
+                    out=beta[:, :, y, :], in0=gam[:, :, SLOT_OF_J[y], :], in1=gam[:, :, SLOT_OF_J[y + 2], :], op=ALU.subtract,
+                )
+            tiles[k]["beta"] = beta
+            tiles[k]["v"] = ew.tile([P, nu, 4, f], BF16, tag="v", bufs=1, name="v")
+            tiles[k]["planes"] = ew.tile([P, nu, 2, 4, f], BF16, tag="planes", name="planes")
 
-        def p1_(k, j):
-            nc.vector.tensor_tensor(out=T[k]["v"][:, j, 0:2, :], in0=T[k]["beta"][:, j], in1=T[k]["inner"][:, j], op=ALU.mult)
+        def inner_to_01(k, un):
+            nc.vector.tensor_tensor(out=tiles[k]["v"][:, un, 0:2, :], in0=tiles[k]["beta"][:, un], in1=tiles[k]["inner"][:, un], op=ALU.mult)
 
-        def p0_(k, j):
-            nc.vector.tensor_tensor(out=T[k]["v"][:, j, 2:4, :], in0=T[k]["inner"][:, j], in1=T[k]["v"][:, j, 0:2, :], op=ALU.subtract)
+        def inner_to_23(k, un):
+            nc.vector.tensor_tensor(
+                out=tiles[k]["v"][:, un, 2:4, :], in0=tiles[k]["inner"][:, un], in1=tiles[k]["v"][:, un, 0:2, :], op=ALU.subtract,
+            )
 
-        def max_(k, j):
-            f = GROUPS[k][j] * P
-            v4 = T[k]["v"][:, j].rearrange("p (r k) f -> p r (k f)", r=2)
-            nc.vector.tensor_tensor(out=v4, in0=v4, in1=T[k]["ring"][:, j].rearrange("p k f -> p (k f)").unsqueeze(1).to_broadcast([P, 2, 2 * f]), op=ALU.max)
+        def ring_elsewhere(k, un):
+            f = GROUPS[k][un] * P
+            v4 = tiles[k]["v"][:, un].rearrange("p (e y) f -> p e (y f)", e=2)
+            nc.vector.tensor_tensor(
+                out=v4, in0=v4, in1=tiles[k]["ring"][:, un].rearrange("p y f -> p (y f)").unsqueeze(1).to_broadcast([P, 2, 2 * f]), op=ALU.max,
+            )
 
-        def hi_(k, j):
-            nc.vector.tensor_tensor(out=T[k]["planes"][:, j, 1], in0=T[k]["v"][:, j], in1=T[k]["gam"][:, j], op=ALU.mult)
+        def upper_half(k, un):
+            nc.vector.tensor_tensor(out=tiles[k]["planes"][:, un, 1], in0=tiles[k]["v"][:, un], in1=tiles[k]["gam"][:, un], op=ALU.mult)
 
-        def lo_(k, j):
-            nc.vector.tensor_tensor(out=T[k]["planes"][:, j, 0], in0=T[k]["v"][:, j], in1=T[k]["planes"][:, j, 1], op=ALU.subtract)
+        def lower_half(k, un):
+            nc.vector.tensor_tensor(
+                out=tiles[k]["planes"][:, un, 0], in0=tiles[k]["v"][:, un], in1=tiles[k]["planes"][:, un, 1], op=ALU.subtract,
+            )
 
-        def rgs(k, eng, js=(0, 1, 2, 3)):
-            for j in range(nun(k)):
-                if j not in js:
-                    continue
-                if eng == "act" or (k, 1) in RG_V:
-                    if ("gr", j) not in T[k]:
-                        T[k][("gr", j)] = be.tile([P, 2, 4 * GROUPS[k][j] * P], BF16, tag="gr", bufs=4, align_bytes=64, name="gr")
-                for g in (1, 0):
-                    if ((k, g) in RG_V) == (eng == "v"):
-                        dst = T[k][("gr", j)][:, g, :].rearrange("p (c i s) -> p c s i", i=4, s=4)
-                        srcp = T[k]["planes"][:, j, g].rearrange("p s (c i) -> p c s i", i=4)
-                        if eng == "act":
-                            nc.scalar.copy(out=dst, in_=srcp)
-                        else:
-                            nc.vector.tensor_copy(out=dst, in_=srcp)
+        def regroup(k, un):
+            gr = be.tile([P, 2, 4 * GROUPS[k][un] * P], BF16, tag="gr", bufs=4, align_bytes=64)
+            tiles[k][("gr", un)] = gr
+            for g in (1, 0):
+                dst = gr[:, g, :].rearrange("p (q v s) -> p q s v", v=4, s=4)
+                src = tiles[k]["planes"][:, un, g].rearrange("p s (q v) -> p q s v", v=4)
+                if short(k):
+                    nc.vector.tensor_copy(out=dst, in_=src)
+                else:
+                    nc.scalar.copy(out=dst, in_=src)
 
-        def q_(k, j):
-            n = GROUPS[k][j] * P
-            bcodes = be.tile([P, 2, n], U32, tag="bcodes", bufs=4, align_bytes=64)
-            bscales = be.tile([P, 2, n], U8, tag="bscales", bufs=4, align_bytes=64)
+        def quantise_multiply(k, un):
+            f = GROUPS[k][un] * P
+            bcodes = be.tile([P, 2, f], U32, tag="bcodes", bufs=4, align_bytes=64)
+            bscales = be.tile([P, 2, f], U8, tag="bscales", bufs=4, align_bytes=64)
             nc.vector.quantize_mx(
                 out=bcodes[:].rearrange("p g w -> p (g w)").bitcast(FP8X4),
                 scales=bscales[:].rearrange("p g w -> p (g w)"),
-                in_=T[k][("gr", j)][:].rearrange("p g k -> p (g k)"),
+                in_=tiles[k][("gr", un)][:].rearrange("p g w -> p (g w)"),
             )
             mxs = []
             for h in range(2):
-                mx = psum.tile([P, n], F32, tag="mx", bufs=4)
+                mx = psum.tile([P, f], F32, tag="mx", bufs=4)
                 for g in range(2):
                     nc.tensor.matmul_mx(
                         out=mx[:],
@@ -279,58 +269,88 @@ def tile_bsplinebasis_v2_t_kernel(tc, x, spline_coeffs, residual_weight, residua
                         stop=(g == 1),
                     )
                 mxs.append(mx)
-            T[k][("mx", j)] = mxs
+            tiles[k][("mx", un)] = mxs
 
-        def t1_(k, j):
-            s = GROUPS[k][j]
-            n0 = GSTART[k] + sum(GROUPS[k][:j])
+        def scale_add_residual(k, un):
+            nt = GROUPS[k][un]
+            n0 = GSTART[k] + sum(GROUPS[k][:un])
             t1s = []
             for h in range(2):
-                t1 = be.tile([P, s * P], F32, tag="t1_%d" % h)
-                nc.scalar.activation(out=t1[:], in_=T[k][("mx", j)][h][:], func=ACT.Identity, bias=bias[:, h:h + 1], scale=scale[:, h:h + 1])
+                t1 = be.tile([P, nt * P], F32, tag="t1_%d" % h)
+                nc.scalar.activation(
+                    out=t1[:], in_=tiles[k][("mx", un)][h][:], func=ACT.Identity, bias=bias[:, h:h + 1], scale=scale[:, h:h + 1],
+                )
                 t1s.append(t1)
             ots = []
-            for k0 in range(0, s, 2):
-                kn = min(2, s - k0)
-                ot = psum.tile([P, kn, O], F32, tag="ot", bufs=3)
-                for q in range(kn):
-                    n = k0 + q
+            for first in range(0, nt, 2):
+                count = min(2, nt - first)
+                ot = psum.tile([P, count, O], F32, tag="ot", bufs=3)
+                for pos in range(count):
+                    n = first + pos
                     for h in range(2):
-                        dsto = ot[:, q, h * P:(h + 1) * P]
-                        nc.tensor.matmul(out=dsto, lhsT=xT[:, n0 + n, :], rhs=rwT[:, h, :], start=True, stop=False)
-                        nc.tensor.matmul(out=dsto, lhsT=t1s[h][:, n * P:(n + 1) * P], rhs=ident_f[:], is_transpose=True, start=False, stop=True)
-                ots.append((k0, kn, ot))
-            T[k][("ot", j)] = ots
+                        dst = ot[:, pos, h * P:(h + 1) * P]
+                        nc.tensor.matmul(out=dst, lhsT=xT[:, n0 + n, :], rhs=rwT[:, h, :], start=True, stop=False)
+                        nc.tensor.matmul(
+                            out=dst, lhsT=t1s[h][:, n * P:(n + 1) * P], rhs=ident_f[:], is_transpose=True, start=False, stop=True,
+                        )
+                ots.append((first, count, ot))
+            tiles[k][("ot", un)] = ots
 
-        def ev_(k, j):
-            s = GROUPS[k][j]
-            n0 = GSTART[k] + sum(GROUPS[k][:j])
-            osb = be.tile([P, s, O], F32, tag="osb", bufs=3)
-            for k0, kn, ot in T[k][("ot", j)]:
-                nc.scalar.copy(out=osb[:, k0:k0 + kn, :], in_=ot[:])
-            nc.sync.dma_start(out=out_v[:, n0:n0 + s, :], in_=osb[:])
+        def store(k, un):
+            nt = GROUPS[k][un]
+            n0 = GSTART[k] + sum(GROUPS[k][:un])
+            osb = be.tile([P, nt, O], F32, tag="osb", bufs=3)
+            for first, count, ot in tiles[k][("ot", un)]:
+                nc.scalar.copy(out=osb[:, first:first + count, :], in_=ot[:])
+            nc.sync.dma_start(out=out_v[:, n0:n0 + nt, :], in_=osb[:])
+
+
+        def whole(k, *steps):
+            if exists(k):
+                for step in steps:
+                    step(k)
+
+        def unit(k, un, step):
+            if un < units(k):
+                step(k, un)
+
+        def alternating(k, *steps):
+            for step in steps:
+                for un in range(units(k)):
+                    step(k, un)
+
+        def due(k, un, step):
+            if exists(k - 2) and not short(k - 2):
+                unit(k - 2, un, step)
+            if short(k - 1):
+                unit(k - 1, un, step)
+
+        def scalar_regroups(k, un):
+            if exists(k) and not short(k):
+                unit(k, un, regroup)
 
         for k in range(-3, NG + 3):
-            grp(k + 3, xp_)
-            rgs(k - 1, "act", (0,))
-            grp(k, ring_, w_)
-            late(k, 0, t1_)
-            rgs(k - 1, "act", (1,))
-            grp(k, gam_, inner_, beta_)
-            late(k, 0, ev_)
-            late(k, 1, t1_)
-            alt(k + 1, a1_, a2_, a3_)
-            grp(k + 2, u_)
-            late(k, 1, ev_)
-            grp(k + 1, da_)
-            grp(k + 3, evx_)
-            grp(k + 1, sq_)
-            alt(k, p1_, p0_, max_, hi_, lo_)
-            if not early(k - 1):
-                rgs(k - 1, "v")
-                alt(k - 1, q_)
-            if early(k):
-                rgs(k, "v")
-                alt(k, q_)
-            if k == W_AT:
-                weights()
+            whole(k + 3, transpose_x)
+            scalar_regroups(k - 1, 0)
+            whole(k, ring_piece, inner_cubic)
+            due(k, 0, scale_add_residual)
+            scalar_regroups(k - 1, 1)
+            whole(k, knot_masks, inner_piece, near_masks)
+            due(k, 0, store)
+            due(k, 1, scale_add_residual)
+            alternating(k + 1, fold_1, fold_2, fold_3)
+            whole(k + 2, clamp)
+            due(k, 1, store)
+            whole(k + 1, other_distance)
+            whole(k + 3, keep_xT)
+            whole(k + 1, squares)
+            alternating(k, inner_to_01, inner_to_23, ring_elsewhere, upper_half, lower_half)
+            if not short(k - 1):
+                alternating(k - 1, quantise_multiply)
+            if short(k):
+                alternating(k, regroup)
+                alternating(k, quantise_multiply)
+            if k == -1:
+                weights_transpose()
+            if k == 0:
+                weights_finish()

@@ -92,17 +92,19 @@ def tile_bsplinebasis_v2_t_kernel(tc, x, spline_coeffs, residual_weight, residua
                     nc.tensor.transpose(tpc[:, q, :], cpm[:, h, :].rearrange("p (r j) -> p j r", j=NBAS)[:, j], ident_b[:])
                 wt[h] = tpc
 
-        def weights_finish():
-            nc.vector.tensor_copy(out=rwT[:], in_=wt["tpr"][:, 0:2, :])
-            nc.vector.tensor_copy(out=bias[:], in_=wt["tpr"][:, 2, 0:2])
-            ssum = setup.tile([P, 2], F32)
-            nc.vector.tensor_reduce(out=ssum[:], in_=sb_sb[:], axis=mybir.AxisListType.X, op=ALU.add)
-            nc.vector.tensor_scalar(out=scale[:], in0=ssum[:], scalar1=1.0 / I, scalar2=None, op0=ALU.mult)
+        def weights_leave_psum():
+            nc.scalar.copy(out=rwT[:], in_=wt["tpr"][:, 0:2, :])
+            nc.scalar.copy(out=bias[:], in_=wt["tpr"][:, 2, 0:2])
             for h in range(2):
-                nc.vector.tensor_copy(
+                nc.scalar.copy(
                     out=cgr[:, :, h * 4 * P:(h + 1) * 4 * P].rearrange("p g (w s) -> p g w s", s=4),
                     in_=wt[h][:].rearrange("p (g s) w -> p g w s", s=4),
                 )
+
+        def weights_finish():
+            ssum = setup.tile([P, 2], F32)
+            nc.vector.tensor_reduce(out=ssum[:], in_=sb_sb[:], axis=mybir.AxisListType.X, op=ALU.add)
+            nc.vector.tensor_scalar(out=scale[:], in0=ssum[:], scalar1=1.0 / I, scalar2=None, op0=ALU.mult)
             nc.vector.quantize_mx(
                 out=ccodes[:].rearrange("p g o -> p (g o)").bitcast(FP8X4),
                 scales=cscales[:].rearrange("p g o -> p (g o)"),
@@ -345,6 +347,8 @@ def tile_bsplinebasis_v2_t_kernel(tc, x, spline_coeffs, residual_weight, residua
             whole(k + 3, keep_xT)
             whole(k + 1, squares)
             alternating(k, inner_to_01, inner_to_23, ring_elsewhere, upper_half, lower_half)
+            if k == 1:
+                weights_finish()
             if not short(k - 1):
                 alternating(k - 1, quantise_multiply)
             if short(k):
@@ -353,4 +357,4 @@ def tile_bsplinebasis_v2_t_kernel(tc, x, spline_coeffs, residual_weight, residua
             if k == -1:
                 weights_transpose()
             if k == 0:
-                weights_finish()
+                weights_leave_psum()

@@ -21,6 +21,7 @@ GSTART = [sum(sum(grp) for grp in GROUPS[:k]) for k in range(NG)]
 SHORT = 2
 J_OF_SLOT = (3, 0, 1, 2)
 SLOT_OF_J = (1, 2, 3, 0)
+S_HALVES = ((1, 0), (1,))
 FLOPS = 2 * B * I * NBAS * O + 2 * B * I * O
 assert sum(sum(grp) for grp in GROUPS) == NT
 
@@ -198,7 +199,7 @@ def tile_bsplinebasis_v2_t_kernel(tc, x, spline_coeffs, residual_weight, residua
             gam = ew.tile([P, nu, 4, f], BF16, tag="gam", bufs=1)
             for s in range(4):
                 nc.vector.tensor_scalar(
-                    out=gam[:, :, s, :], in0=tiles[k]["u"][:], scalar1=0.4 * (J_OF_SLOT[s] + 1) - 1.0, scalar2=None, op0=ALU.is_gt,
+                    out=gam[:, :, s, :], in0=tiles[k]["u"][:], scalar1=0.4 * (J_OF_SLOT[s] + 1) - 1.0, scalar2=0.5, op0=ALU.is_gt, op1=ALU.subtract,
                 )
             tiles[k]["gam"] = gam
 
@@ -212,7 +213,7 @@ def tile_bsplinebasis_v2_t_kernel(tc, x, spline_coeffs, residual_weight, residua
                 )
             tiles[k]["beta"] = beta
             tiles[k]["v"] = ew.tile([P, nu, 4, f], BF16, tag="v", bufs=1, name="v")
-            tiles[k]["planes"] = ew.tile([P, nu, 2, 4, f], BF16, tag="planes", name="planes")
+            tiles[k]["z"] = ew.tile([P, nu, 4, f], BF16, tag="z", name="z")
 
         def inner_to_01(k, un):
             nc.vector.tensor_tensor(out=tiles[k]["v"][:, un, 0:2, :], in0=tiles[k]["beta"][:, un], in1=tiles[k]["inner"][:, un], op=ALU.mult)
@@ -229,24 +230,21 @@ def tile_bsplinebasis_v2_t_kernel(tc, x, spline_coeffs, residual_weight, residua
                 out=v4, in0=v4, in1=tiles[k]["ring"][:, un].rearrange("p y f -> p (y f)").unsqueeze(1).to_broadcast([P, 2, 2 * f]), op=ALU.max,
             )
 
-        def upper_half(k, un):
-            nc.vector.tensor_tensor(out=tiles[k]["planes"][:, un, 1], in0=tiles[k]["v"][:, un], in1=tiles[k]["gam"][:, un], op=ALU.mult)
+        def signed(k, un):
+            nc.vector.tensor_tensor(out=tiles[k]["z"][:, un], in0=tiles[k]["v"][:, un], in1=tiles[k]["gam"][:, un], op=ALU.mult)
 
-        def lower_half(k, un):
-            nc.vector.tensor_tensor(
-                out=tiles[k]["planes"][:, un, 0], in0=tiles[k]["v"][:, un], in1=tiles[k]["planes"][:, un, 1], op=ALU.subtract,
-            )
-
-        def regroup(k, un):
-            gr = be.tile([P, 2, 4 * GROUPS[k][un] * P], BF16, tag="gr", bufs=4, align_bytes=64)
-            tiles[k][("gr", un)] = gr
-            for g in (1, 0):
+        def regroup(k, un, halves=(1, 0), on_vector=True):
+            if ("gr", un) not in tiles[k]:
+                tiles[k][("gr", un)] = be.tile([P, 2, 4 * GROUPS[k][un] * P], BF16, tag="gr", bufs=4, align_bytes=64, name="gr")
+            gr = tiles[k][("gr", un)]
+            for g in halves:
                 dst = gr[:, g, :].rearrange("p (q v s) -> p q s v", v=4, s=4)
-                src = tiles[k]["planes"][:, un, g].rearrange("p s (q v) -> p q s v", v=4)
-                if short(k):
-                    nc.vector.tensor_copy(out=dst, in_=src)
+                src = tiles[k]["z"][:, un].rearrange("p s (q v) -> p q s v", v=4)
+                sign = 2.0 if g == 1 else -2.0
+                if on_vector:
+                    nc.vector.tensor_scalar(out=dst, in0=src, scalar1=sign, scalar2=0.0, op0=ALU.mult, op1=ALU.max)
                 else:
-                    nc.scalar.copy(out=dst, in_=src)
+                    nc.scalar.activation(out=dst, in_=src, func=ACT.Relu, bias=0.0, scale=sign)
 
         def quantise_multiply(k, un):
             f = GROUPS[k][un] * P
@@ -328,10 +326,16 @@ def tile_bsplinebasis_v2_t_kernel(tc, x, spline_coeffs, residual_weight, residua
                 unit(k - 1, un, step)
 
         def scalar_regroups(k, un):
+            if exists(k) and not short(k) and un < units(k):
+                regroup(k, un, halves=S_HALVES[un], on_vector=False)
+
+        def vector_regroups(k):
             if exists(k) and not short(k):
-                unit(k, un, regroup)
+                for un in range(units(k)):
+                    regroup(k, un, halves=tuple(g for g in (1, 0) if g not in S_HALVES[un]), on_vector=True)
 
         for k in range(-3, NG + 3):
+            vector_regroups(k - 1)
             whole(k + 3, transpose_x)
             scalar_regroups(k - 1, 0)
             whole(k, ring_piece, inner_cubic)
@@ -346,7 +350,7 @@ def tile_bsplinebasis_v2_t_kernel(tc, x, spline_coeffs, residual_weight, residua
             whole(k + 1, other_distance)
             whole(k + 3, keep_xT)
             whole(k + 1, squares)
-            alternating(k, inner_to_01, inner_to_23, ring_elsewhere, upper_half, lower_half)
+            alternating(k, inner_to_01, inner_to_23, ring_elsewhere, signed)
             if k == 1:
                 weights_finish()
             if not short(k - 1):

@@ -28,7 +28,7 @@ assert sum(sum(grp) for grp in GROUPS) == NT
 
 def tile_bsplinebasis_v2_t_kernel(tc, x, spline_coeffs, residual_weight, residual_bias, scale_base, out):
     nc = tc.nc
-    r6 = 1.0 / math.sqrt(6.0)
+    r2 = 1.0 / math.sqrt(2.0)
     with ExitStack() as ctx:
         const = ctx.enter_context(tc.tile_pool(name="const", bufs=1))
         setup = ctx.enter_context(tc.tile_pool(name="setup", bufs=1))
@@ -172,13 +172,16 @@ def tile_bsplinebasis_v2_t_kernel(tc, x, spline_coeffs, residual_weight, residua
         def squares(k):
             nu, f = dims(k)
             sq = ew.tile([P, nu, 2, f], F32, tag="sq")
-            nc.scalar.activation(out=sq[:], in_=tiles[k]["de"][:], func=ACT.Square, bias=0.0, scale=r6)
+            nc.scalar.activation(out=sq[:], in_=tiles[k]["de"][:], func=ACT.Square, bias=0.0, scale=r2)
             tiles[k]["sq"] = sq
 
         def ring_piece(k):
             nu, f = dims(k)
             ring = ew.tile([P, nu, 2, f], BF16, tag="ring", bufs=1)
-            nc.vector.tensor_tensor(out=ring[:], in0=tiles[k]["sq"][:], in1=tiles[k]["de"][:], op=ALU.mult)
+            nc.vector.scalar_tensor_tensor(
+                out=ring[:].rearrange("p d y f -> p (d y f)"), in0=tiles[k]["sq"][:].rearrange("p d y f -> p (d y f)"), scalar=1.0 / 12.0,
+                in1=tiles[k]["de"][:].rearrange("p d y f -> p (d y f)"), op0=ALU.mult, op1=ALU.mult,
+            )
             tiles[k]["ring"] = ring
 
         def inner_cubic(k):
@@ -189,10 +192,16 @@ def tile_bsplinebasis_v2_t_kernel(tc, x, spline_coeffs, residual_weight, residua
             )
 
         def inner_piece(k):
-            nu, f = dims(k)
-            inner = ew.tile([P, nu, 2, f], BF16, tag="inner", bufs=1)
-            nc.vector.tensor_scalar(out=inner[:], in0=tiles[k]["sq"][:], scalar1=3.0, scalar2=2.0 / 3.0, op0=ALU.mult, op1=ALU.add)
-            tiles[k]["inner"] = inner
+            nc.vector.scalar_tensor_tensor(
+                out=tiles[k]["v"][:, :, 2:4, :].rearrange("p d y f -> p d (y f)"), in0=tiles[k]["sq"][:].rearrange("p d y f -> p d (y f)"),
+                scalar=2.0 / 3.0, in1=tiles[k]["beta"][:].rearrange("p d y f -> p d (y f)"), op0=ALU.add, op1=ALU.mult,
+            )
+
+        def inner_negated(k):
+            nc.vector.tensor_scalar(
+                out=tiles[k]["v"][:, :, 0:2, :].rearrange("p d y f -> p d (y f)"), in0=tiles[k]["v"][:, :, 2:4, :].rearrange("p d y f -> p d (y f)"),
+                scalar1=-1.0, scalar2=None, op0=ALU.mult,
+            )
 
         def knot_masks(k):
             nu, f = dims(k)
@@ -209,19 +218,11 @@ def tile_bsplinebasis_v2_t_kernel(tc, x, spline_coeffs, residual_weight, residua
             beta = ew.tile([P, nu, 2, f], BF16, tag="beta", bufs=1)
             for y in range(2):
                 nc.vector.tensor_tensor(
-                    out=beta[:, :, y, :], in0=gam[:, :, SLOT_OF_J[y], :], in1=gam[:, :, SLOT_OF_J[y + 2], :], op=ALU.subtract,
+                    out=beta[:, :, y, :], in0=gam[:, :, SLOT_OF_J[y], :], in1=gam[:, :, SLOT_OF_J[y + 2], :], op=ALU.mult,
                 )
             tiles[k]["beta"] = beta
             tiles[k]["v"] = ew.tile([P, nu, 4, f], BF16, tag="v", bufs=1, name="v")
             tiles[k]["z"] = ew.tile([P, nu, 4, f], BF16, tag="z", name="z")
-
-        def inner_to_01(k, un):
-            nc.vector.tensor_tensor(out=tiles[k]["v"][:, un, 0:2, :], in0=tiles[k]["beta"][:, un], in1=tiles[k]["inner"][:, un], op=ALU.mult)
-
-        def inner_to_23(k, un):
-            nc.vector.tensor_tensor(
-                out=tiles[k]["v"][:, un, 2:4, :], in0=tiles[k]["inner"][:, un], in1=tiles[k]["v"][:, un, 0:2, :], op=ALU.subtract,
-            )
 
         def ring_elsewhere(k, un):
             f = GROUPS[k][un] * P
@@ -240,7 +241,7 @@ def tile_bsplinebasis_v2_t_kernel(tc, x, spline_coeffs, residual_weight, residua
             for g in halves:
                 dst = gr[:, g, :].rearrange("p (q v s) -> p q s v", v=4, s=4)
                 src = tiles[k]["z"][:, un].rearrange("p s (q v) -> p q s v", v=4)
-                sign = 2.0 if g == 1 else -2.0
+                sign = 8.0 if g == 1 else -8.0
                 if on_vector:
                     nc.vector.tensor_scalar(out=dst, in0=src, scalar1=sign, scalar2=0.0, op0=ALU.mult, op1=ALU.max)
                 else:
@@ -337,24 +338,27 @@ def tile_bsplinebasis_v2_t_kernel(tc, x, spline_coeffs, residual_weight, residua
         for k in range(-3, NG + 3):
             vector_regroups(k - 1)
             whole(k + 3, transpose_x)
-            scalar_regroups(k - 1, 0)
-            whole(k, ring_piece, inner_cubic)
             due(k, 0, scale_add_residual)
+            scalar_regroups(k - 1, 0)
             scalar_regroups(k - 1, 1)
-            whole(k, knot_masks, inner_piece, near_masks)
             due(k, 0, store)
             due(k, 1, scale_add_residual)
+            whole(k, ring_piece, inner_cubic, knot_masks, near_masks)
             alternating(k + 1, fold_1, fold_2, fold_3)
             whole(k + 2, clamp)
-            due(k, 1, store)
+            whole(k, inner_piece)
             whole(k + 1, other_distance)
             whole(k + 3, keep_xT)
+            due(k, 1, store)
             whole(k + 1, squares)
-            alternating(k, inner_to_01, inner_to_23, ring_elsewhere, signed)
             if k == 1:
                 weights_finish()
             if not short(k - 1):
-                alternating(k - 1, quantise_multiply)
+                unit(k - 1, 0, quantise_multiply)
+            whole(k, inner_negated)
+            if not short(k - 1):
+                unit(k - 1, 1, quantise_multiply)
+            alternating(k, ring_elsewhere, signed)
             if short(k):
                 alternating(k, regroup)
                 alternating(k, quantise_multiply)

@@ -205,8 +205,8 @@ def tile_bsplinebasis_v2_t_kernel(tc, x, spline_coeffs, residual_weight, residua
 
         def knot_masks(k):
             nu, f = dims(k)
-            gam = ew.tile([P, nu, 4, f], BF16, tag="gam", bufs=1)
-            for s in range(4):
+            gam = ew.tile([P, nu, 4, f], BF16, tag="gam")
+            for s in (SLOT_OF_J[0], SLOT_OF_J[2], SLOT_OF_J[1], SLOT_OF_J[3]):
                 nc.vector.tensor_scalar(
                     out=gam[:, :, s, :], in0=tiles[k]["u"][:], scalar1=0.4 * (J_OF_SLOT[s] + 1) - 1.0, scalar2=0.5, op0=ALU.is_gt, op1=ALU.subtract,
                 )
@@ -336,28 +336,29 @@ def tile_bsplinebasis_v2_t_kernel(tc, x, spline_coeffs, residual_weight, residua
                     regroup(k, un, halves=tuple(g for g in (1, 0) if g not in S_HALVES[un]), on_vector=True)
 
         for k in range(-3, NG + 3):
-            vector_regroups(k - 1)
             whole(k + 3, transpose_x)
+            whole(k, knot_masks)
+            vector_regroups(k - 1)
             due(k, 0, scale_add_residual)
             scalar_regroups(k - 1, 0)
             scalar_regroups(k - 1, 1)
             due(k, 0, store)
             due(k, 1, scale_add_residual)
-            whole(k, ring_piece, inner_cubic, knot_masks, near_masks)
-            alternating(k + 1, fold_1, fold_2, fold_3)
-            whole(k + 2, clamp)
-            whole(k, inner_piece)
-            whole(k + 1, other_distance)
-            whole(k + 3, keep_xT)
-            due(k, 1, store)
-            whole(k + 1, squares)
+            whole(k, ring_piece, near_masks, inner_cubic)
             if k == 1:
                 weights_finish()
             if not short(k - 1):
                 unit(k - 1, 0, quantise_multiply)
+            whole(k, inner_piece)
+            alternating(k + 1, fold_1, fold_2, fold_3)
+            whole(k + 2, clamp)
             whole(k, inner_negated)
             if not short(k - 1):
                 unit(k - 1, 1, quantise_multiply)
+            whole(k + 3, keep_xT)
+            whole(k + 1, other_distance)
+            due(k, 1, store)
+            whole(k + 1, squares)
             alternating(k, ring_elsewhere, signed)
             if short(k):
                 alternating(k, regroup)

@@ -21,7 +21,7 @@ GSTART = [sum(sum(grp) for grp in GROUPS[:k]) for k in range(NG)]
 SHORT = 2
 J_OF_SLOT = (3, 0, 1, 2)
 SLOT_OF_J = (1, 2, 3, 0)
-S_HALVES = ((1, 0), (1,))
+V_PIECES = 1.25
 FLOPS = 2 * B * I * NBAS * O + 2 * B * I * O
 assert sum(sum(grp) for grp in GROUPS) == NT
 
@@ -234,18 +234,29 @@ def tile_bsplinebasis_v2_t_kernel(tc, x, spline_coeffs, residual_weight, residua
         def signed(k, un):
             nc.vector.tensor_tensor(out=tiles[k]["z"][:, un], in0=tiles[k]["v"][:, un], in1=tiles[k]["gam"][:, un], op=ALU.mult)
 
-        def regroup(k, un, halves=(1, 0), on_vector=True):
+        def regroup(k, un, g, c0, c1, on_vector):
             if ("gr", un) not in tiles[k]:
                 tiles[k][("gr", un)] = be.tile([P, 2, 4 * GROUPS[k][un] * P], BF16, tag="gr", bufs=4, align_bytes=64, name="gr")
-            gr = tiles[k][("gr", un)]
-            for g in halves:
-                dst = gr[:, g, :].rearrange("p (q v s) -> p q s v", v=4, s=4)
-                src = tiles[k]["z"][:, un].rearrange("p s (q v) -> p q s v", v=4)
-                sign = 8.0 if g == 1 else -8.0
-                if on_vector:
-                    nc.vector.tensor_scalar(out=dst, in0=src, scalar1=sign, scalar2=0.0, op0=ALU.mult, op1=ALU.max)
-                else:
-                    nc.scalar.activation(out=dst, in_=src, func=ACT.Relu, bias=0.0, scale=sign)
+            dst = tiles[k][("gr", un)][:, g, 4 * c0:4 * c1].rearrange("p (q v s) -> p q s v", v=4, s=4)
+            src = tiles[k]["z"][:, un, :, c0:c1].rearrange("p s (q v) -> p q s v", v=4)
+            sign = 8.0 if g == 1 else -8.0
+            if on_vector:
+                nc.vector.tensor_scalar(out=dst, in0=src, scalar1=sign, scalar2=0.0, op0=ALU.mult, op1=ALU.max)
+            else:
+                nc.scalar.activation(out=dst, in_=src, func=ACT.Relu, bias=0.0, scale=sign)
+
+        def shares(k):
+            f = dims(k)[1]
+            left = 4 * f if short(k) else int(V_PIECES * f)
+            for_scalar, for_vector = [], []
+            for un, g in ((1, 0), (1, 1), (0, 0), (0, 1)):
+                take = min(f, left)
+                left -= take
+                if take < f:
+                    for_scalar.append((un, g, 0, f - take))
+                if take > 0:
+                    for_vector.append((un, g, f - take, f))
+            return list(reversed(for_scalar)), list(reversed(for_vector))
 
         def quantise_multiply(k, un):
             f = GROUPS[k][un] * P
@@ -277,7 +288,7 @@ def tile_bsplinebasis_v2_t_kernel(tc, x, spline_coeffs, residual_weight, residua
             n0 = GSTART[k] + sum(GROUPS[k][:un])
             t1s = []
             for h in range(2):
-                t1 = be.tile([P, nt * P], F32, tag="t1_%d" % h)
+                t1 = be.tile([P, nt * P], F32, tag="t1_%d" % h, bufs=3)
                 nc.scalar.activation(
                     out=t1[:], in_=tiles[k][("mx", un)][h][:], func=ACT.Identity, bias=bias[:, h:h + 1], scale=scale[:, h:h + 1],
                 )
@@ -326,24 +337,45 @@ def tile_bsplinebasis_v2_t_kernel(tc, x, spline_coeffs, residual_weight, residua
             if short(k - 1):
                 unit(k - 1, un, step)
 
+        def due_units(k):
+            found = []
+            if exists(k - 2) and not short(k - 2):
+                found.extend([(k - 2, un) for un in range(units(k - 2))])
+            if short(k - 1):
+                found.extend([(k - 1, un) for un in range(units(k - 1))])
+            return found
+
         def scalar_regroups(k, un):
-            if exists(k) and not short(k) and un < units(k):
-                regroup(k, un, halves=S_HALVES[un], on_vector=False)
+            if exists(k):
+                for piece in shares(k)[0]:
+                    if piece[0] == un:
+                        regroup(k, *piece, on_vector=False)
 
         def vector_regroups(k):
-            if exists(k) and not short(k):
-                for un in range(units(k)):
-                    regroup(k, un, halves=tuple(g for g in (1, 0) if g not in S_HALVES[un]), on_vector=True)
+            if exists(k):
+                for piece in shares(k)[1]:
+                    regroup(k, *piece, on_vector=True)
 
         for k in range(-3, NG + 3):
             whole(k + 3, transpose_x)
             whole(k, knot_masks)
-            vector_regroups(k - 1)
-            due(k, 0, scale_add_residual)
-            scalar_regroups(k - 1, 0)
-            scalar_regroups(k - 1, 1)
-            due(k, 0, store)
-            due(k, 1, scale_add_residual)
+            if not short(k - 1):
+                vector_regroups(k - 1)
+            last_rounds = k >= NG - 1
+            if last_rounds:
+                leaving = due_units(k)
+                for i in range(len(leaving)):
+                    scale_add_residual(*leaving[i])
+                    if i >= 2:
+                        store(*leaving[i - 2])
+                for kk_un in leaving[-2:]:
+                    store(*kk_un)
+            else:
+                due(k, 0, scale_add_residual)
+                scalar_regroups(k - 1, 0)
+                scalar_regroups(k - 1, 1)
+                due(k, 0, store)
+                due(k, 1, scale_add_residual)
             whole(k, ring_piece, near_masks, inner_cubic)
             if k == 1:
                 weights_finish()
@@ -357,11 +389,12 @@ def tile_bsplinebasis_v2_t_kernel(tc, x, spline_coeffs, residual_weight, residua
                 unit(k - 1, 1, quantise_multiply)
             whole(k + 3, keep_xT)
             whole(k + 1, other_distance)
-            due(k, 1, store)
+            if not last_rounds:
+                due(k, 1, store)
             whole(k + 1, squares)
             alternating(k, ring_elsewhere, signed)
             if short(k):
-                alternating(k, regroup)
+                vector_regroups(k)
                 alternating(k, quantise_multiply)
             if k == -1:
                 weights_transpose()

@@ -21,6 +21,7 @@ GSTART = [sum(sum(grp) for grp in GROUPS[:k]) for k in range(NG)]
 SHORT = 2
 J_OF_SLOT = (3, 0, 1, 2)
 SLOT_OF_J = (1, 2, 3, 0)
+KEEP_ON_VECTOR = 4
 V_PIECES = 1.25
 FLOPS = 2 * B * I * NBAS * O + 2 * B * I * O
 assert sum(sum(grp) for grp in GROUPS) == NT
@@ -38,13 +39,21 @@ def tile_bsplinebasis_v2_t_kernel(tc, x, spline_coeffs, residual_weight, residua
         ctx.enter_context(tc.manual_schedule())
 
         x_sb = const.tile([P, NT, I], BF16)
+        xp = const.tile([P, NT, I], BF16)
         xT = const.tile([P, NT, P], BF16)
         x_v = x.rearrange("(p n) i -> p n i", n=NT)
         out_v = out.rearrange("(p n) o -> p n o", n=NT)
-        for k in range(NG):
+        warm = const.tile([P, 1], F32)
+        nc.vector.memset(warm[:], 0.0)
+        nc.scalar.activation(out=warm[:], in_=warm[:], func=ACT.Abs, bias=0.0, scale=1.0)
+
+        def load_x(k):
             n0 = GSTART[k]
             n1 = n0 + sum(GROUPS[k])
             nc.sync.dma_start(out=x_sb[:, n0:n1, :], in_=x_v[:, n0:n1, :])
+
+        load_x(0)
+        load_x(1)
 
         ident_b = const.tile([P, P], BF16)
         make_identity(nc, ident_b[:])
@@ -52,14 +61,16 @@ def tile_bsplinebasis_v2_t_kernel(tc, x, spline_coeffs, residual_weight, residua
         make_identity(nc, ident_f[:])
 
         c_sb = setup.tile([P, 2, I * NBAS], BF16)
-        nc.scalar.dma_start(out=c_sb[:], in_=spline_coeffs.rearrange("(h p) i j -> p h (i j)", p=P))
+        nc.sync.dma_start(out=c_sb[:], in_=spline_coeffs.rearrange("(h p) i j -> p h (i j)", p=P))
         rw_sb = setup.tile([P, 2, I], BF16)
-        nc.scalar.dma_start(out=rw_sb[:], in_=residual_weight.rearrange("(h p) i -> p h i", p=P))
+        nc.sync.dma_start(out=rw_sb[:], in_=residual_weight.rearrange("(h p) i -> p h i", p=P))
         sb_sb = setup.tile([P, 2, I], BF16)
-        nc.scalar.dma_start(out=sb_sb[:], in_=scale_base.rearrange("(h p) i -> p h i", p=P))
+        nc.sync.dma_start(out=sb_sb[:], in_=scale_base.rearrange("(h p) i -> p h i", p=P))
         b_sb = setup.tile([P, P], BF16)
-        nc.gpsimd.memset(b_sb[:], 0.0)
-        nc.scalar.dma_start(out=b_sb[0:2, :], in_=residual_bias.rearrange("(h p) -> h p", p=P))
+        nc.vector.memset(b_sb[:], 0.0)
+        nc.sync.dma_start(out=b_sb[0:2, :], in_=residual_bias.rearrange("(h p) -> h p", p=P))
+        for k in range(2, NG):
+            load_x(k)
 
         cgr = setup.tile([P, 2, 4 * O], BF16, align_bytes=64)
         ccodes = const.tile([P, 2, O], U32, align_bytes=64)
@@ -127,21 +138,26 @@ def tile_bsplinebasis_v2_t_kernel(tc, x, spline_coeffs, residual_weight, residua
             return exists(k) and k >= NG - SHORT
 
 
-        def transpose_x(k):
+        def permute(k):
             nt, n0 = sum(GROUPS[k]), GSTART[k]
-            xp = ew.tile([P, nt, I], BF16, tag="xp")
             nc.vector.tensor_copy(
-                out=xp[:].rearrange("p n (c a m l) -> p (n c) a m l", c=2, a=4, m=4, l=4),
+                out=xp[:, n0:n0 + nt, :].rearrange("p n (c a m l) -> p (n c) a m l", c=2, a=4, m=4, l=4),
                 in_=x_sb[:, n0:n0 + nt, :].rearrange("p n (c m a l) -> p (n c) a m l", c=2, m=4, a=4, l=4),
             )
+
+        def transpose_x(k):
+            nt, n0 = sum(GROUPS[k]), GSTART[k]
             tpx = psum.tile([P, nt, P], BF16, tag="tp")
             for n in range(nt):
-                nc.tensor.transpose(tpx[:, n, :], xp[:, n, :], ident_b[:])
+                nc.tensor.transpose(tpx[:, n, :], xp[:, n0 + n, :], ident_b[:])
             tiles[k]["tpx"] = tpx
 
         def keep_xT(k):
             nt, n0 = sum(GROUPS[k]), GSTART[k]
-            nc.scalar.copy(out=xT[:, n0:n0 + nt, :], in_=tiles[k]["tpx"][:])
+            if k <= KEEP_ON_VECTOR:
+                nc.vector.tensor_copy(out=xT[:, n0:n0 + nt, :], in_=tiles[k]["tpx"][:])
+            else:
+                nc.scalar.copy(out=xT[:, n0:n0 + nt, :], in_=tiles[k]["tpx"][:])
 
         def clamp(k):
             nt, n0 = sum(GROUPS[k]), GSTART[k]
@@ -357,6 +373,8 @@ def tile_bsplinebasis_v2_t_kernel(tc, x, spline_coeffs, residual_weight, residua
                     regroup(k, *piece, on_vector=True)
 
         for k in range(-3, NG + 3):
+            if k < 0:
+                permute(k + 3)
             whole(k + 3, transpose_x)
             whole(k, knot_masks)
             if not short(k - 1):
@@ -398,5 +416,7 @@ def tile_bsplinebasis_v2_t_kernel(tc, x, spline_coeffs, residual_weight, residua
                 alternating(k, quantise_multiply)
             if k == -1:
                 weights_transpose()
+                for later in range(3, NG):
+                    permute(later)
             if k == 0:
                 weights_leave_psum()

@@ -22,7 +22,7 @@ SHORT = 2
 J_OF_SLOT = (3, 0, 1, 2)
 SLOT_OF_J = (1, 2, 3, 0)
 KEEP_ON_VECTOR = 4
-V_PIECES = 1.25
+V_PIECES = 1.0
 FLOPS = 2 * B * I * NBAS * O + 2 * B * I * O
 assert sum(sum(grp) for grp in GROUPS) == NT
 

@@ -261,9 +261,20 @@ def tile_bsplinebasis_v2_t_kernel(tc, x, spline_coeffs, residual_weight, residua
             else:
                 nc.scalar.activation(out=dst, in_=src, func=ACT.Relu, bias=0.0, scale=sign)
 
+        def shrinks(k):
+            return exists(k) and exists(k + 1) and sum(GROUPS[k + 1]) < sum(GROUPS[k])
+
         def shares(k):
             f = dims(k)[1]
-            left = 4 * f if short(k) else int(V_PIECES * f)
+            if short(k):
+                pieces = 4.0
+            elif shrinks(k):
+                pieces = 2.0 * V_PIECES
+            elif shrinks(k - 1):
+                pieces = 0.0
+            else:
+                pieces = V_PIECES
+            left = int(pieces * f)
             for_scalar, for_vector = [], []
             for un, g in ((1, 0), (1, 1), (0, 0), (0, 1)):
                 take = min(f, left)

@@ -15,21 +15,18 @@ ACT = mybir.ActivationFunctionType
 P = 128
 B, I, O, NBAS = 8192, 128, 256, 8
 NT = B // P
-GROUPS = [[1, 1], [2, 2]] + [[4, 4]] * 6 + [[2, 2], [2, 2], [1, 1]]
+GROUPS = [[2], [2, 2]] + [[4, 4]] * 6 + [[2, 2], [2, 2], [2]]
 NG = len(GROUPS)
 GSTART = [sum(sum(grp) for grp in GROUPS[:k]) for k in range(NG)]
-SHORT = 2
 J_OF_SLOT = (3, 0, 1, 2)
 SLOT_OF_J = (1, 2, 3, 0)
-KEEP_ON_VECTOR = 4
-V_PIECES = 1.0
 FLOPS = 2 * B * I * NBAS * O + 2 * B * I * O
 assert sum(sum(grp) for grp in GROUPS) == NT
 
 
 def tile_bsplinebasis_v2_t_kernel(tc, x, spline_coeffs, residual_weight, residual_bias, scale_base, out):
     nc = tc.nc
-    r2 = 1.0 / math.sqrt(2.0)
+    root2 = math.sqrt(2.0)
     with ExitStack() as ctx:
         const = ctx.enter_context(tc.tile_pool(name="const", bufs=1))
         setup = ctx.enter_context(tc.tile_pool(name="setup", bufs=1))
@@ -39,7 +36,7 @@ def tile_bsplinebasis_v2_t_kernel(tc, x, spline_coeffs, residual_weight, residua
         ctx.enter_context(tc.manual_schedule())
 
         x_sb = const.tile([P, NT, I], BF16)
-        xp = const.tile([P, NT, I], BF16)
+        up = const.tile([P, NT, I], BF16)
         xT = const.tile([P, NT, P], BF16)
         x_v = x.rearrange("(p n) i -> p n i", n=NT)
         out_v = out.rearrange("(p n) o -> p n o", n=NT)
@@ -72,231 +69,261 @@ def tile_bsplinebasis_v2_t_kernel(tc, x, spline_coeffs, residual_weight, residua
         for k in range(2, NG):
             load_x(k)
 
+        cpm = setup.tile([P, 2, I, NBAS], BF16)
+        cz = setup.tile([P, 2, 2, 4, I], BF16)
         cgr = setup.tile([P, 2, 4 * O], BF16, align_bytes=64)
         ccodes = const.tile([P, 2, O], U32, align_bytes=64)
         cscales = const.tile([P, 2, O], U8, align_bytes=64)
-        rwT = const.tile([P, 2, P], BF16)
+        rwT = const.tile([P, 2 * P], BF16)
         bias = const.tile([P, 2], F32)
         scale = const.tile([P, 2], F32)
-
         wt = dict()
 
-        def weights_transpose():
-            cpm = setup.tile([P, 2, I * NBAS], BF16)
+        def words(ap):
+            return ap.bitcast(F32)
+
+        def weights_permute():
             nc.vector.tensor_copy(
-                out=cpm[:].rearrange("p h (c a m z) -> p (h c) a m z", c=2, a=4, m=4, z=4 * NBAS),
+                out=cpm[:].rearrange("p h (c a m l) j -> p (h c) a m (l j)", c=2, a=4, m=4, l=4),
                 in_=c_sb[:].rearrange("p h (c m a z) -> p (h c) a m z", c=2, m=4, a=4, z=4 * NBAS),
             )
-            rwp = setup.tile([P, 2, I], BF16)
-            nc.vector.tensor_copy(
-                out=rwp[:].rearrange("p h (c a m l) -> p (h c) a m l", c=2, a=4, m=4, l=4),
-                in_=rw_sb[:].rearrange("p h (c m a l) -> p (h c) a m l", c=2, m=4, a=4, l=4),
-            )
-            tpr = psum.tile([P, 3, P], BF16, tag="mx", bufs=4)
+            for s in range(4):
+                nc.vector.tensor_copy(
+                    out=cz[:, :, :, s, :],
+                    in_=cpm[:].rearrange("p h r (g j) -> p h g j r", g=2)[:, :, :, J_OF_SLOT[s], :],
+                )
+
+        def weights_transpose():
+            tpr = psum.tile([P, 3, P], BF16, tag="ot", bufs=2)
             for h in range(2):
-                nc.tensor.transpose(tpr[:, h, :], rwp[:, h, :], ident_b[:])
+                nc.tensor.transpose(tpr[:, h, :], rw_sb[:, h, :], ident_b[:])
             nc.tensor.transpose(tpr[:, 2, :], b_sb[:], ident_b[:])
             wt["tpr"] = tpr
             for h in range(2):
-                tpc = psum.tile([P, NBAS, P], BF16, tag="mx", bufs=4)
-                for q in range(NBAS):
-                    j = 4 * (q // 4) + J_OF_SLOT[q % 4]
-                    nc.tensor.transpose(tpc[:, q, :], cpm[:, h, :].rearrange("p (r j) -> p j r", j=NBAS)[:, j], ident_b[:])
+                tpc = psum.tile([P, 2, 2, P], F32, tag="mx", bufs=2)
+                for g in range(2):
+                    for e in range(2):
+                        nc.tensor.transpose(
+                            tpc[:, g, e, :], words(cz[:, h, g, 2 * e:2 * e + 2, :].rearrange("p s r -> p (s r)")), ident_f[:],
+                        )
                 wt[h] = tpc
 
         def weights_leave_psum():
-            nc.scalar.copy(out=rwT[:], in_=wt["tpr"][:, 0:2, :])
+            nc.scalar.copy(out=rwT[:].rearrange("p (h o) -> p h o", h=2), in_=wt["tpr"][:, 0:2, :])
             nc.scalar.copy(out=bias[:], in_=wt["tpr"][:, 2, 0:2])
             for h in range(2):
                 nc.scalar.copy(
-                    out=cgr[:, :, h * 4 * P:(h + 1) * 4 * P].rearrange("p g (w s) -> p g w s", s=4),
-                    in_=wt[h][:].rearrange("p (g s) w -> p g w s", s=4),
+                    out=words(cgr[:, :, h * 4 * P:(h + 1) * 4 * P]).rearrange("p g (o e) -> p g o e", e=2),
+                    in_=wt[h][:].rearrange("p g e o -> p g o e"),
                 )
 
         def weights_finish():
             ssum = setup.tile([P, 2], F32)
             nc.vector.tensor_reduce(out=ssum[:], in_=sb_sb[:], axis=mybir.AxisListType.X, op=ALU.add)
-            nc.vector.tensor_scalar(out=scale[:], in0=ssum[:], scalar1=1.0 / I, scalar2=None, op0=ALU.mult)
             nc.vector.quantize_mx(
                 out=ccodes[:].rearrange("p g o -> p (g o)").bitcast(FP8X4),
                 scales=cscales[:].rearrange("p g o -> p (g o)"),
                 in_=cgr[:].rearrange("p g w -> p (g w)"),
             )
+            nc.vector.tensor_scalar(out=scale[:], in0=ssum[:], scalar1=1.0 / I, scalar2=None, op0=ALU.mult)
 
         tiles = [dict() for k in range(NG)]
 
         def exists(k):
             return 0 <= k < NG
 
-        def units(k):
-            return len(GROUPS[k]) if exists(k) else 0
+        def tiles_of(k):
+            return sum(GROUPS[k])
 
-        def dims(k):
-            return len(GROUPS[k]), GROUPS[k][0] * P
-
-        def short(k):
-            return exists(k) and k >= NG - SHORT
+        def unit_tiles(k, un):
+            first = sum(GROUPS[k][:un])
+            return first, first + GROUPS[k][un]
 
 
         def permute(k):
-            nt, n0 = sum(GROUPS[k]), GSTART[k]
+            nt, n0 = tiles_of(k), GSTART[k]
             nc.vector.tensor_copy(
-                out=xp[:, n0:n0 + nt, :].rearrange("p n (c a m l) -> p (n c) a m l", c=2, a=4, m=4, l=4),
+                out=up[:, n0:n0 + nt, :].rearrange("p n (c a m l) -> p (n c) a m l", c=2, a=4, m=4, l=4),
                 in_=x_sb[:, n0:n0 + nt, :].rearrange("p n (c m a l) -> p (n c) a m l", c=2, m=4, a=4, l=4),
             )
 
-        def transpose_x(k):
-            nt, n0 = sum(GROUPS[k]), GSTART[k]
-            tpx = psum.tile([P, nt, P], BF16, tag="tp")
+        def clamp(k):
+            nt, n0 = tiles_of(k), GSTART[k]
+            u = up[:, n0:n0 + nt, :].rearrange("p n i -> p (n i)")
+            nc.vector.tensor_scalar(out=u, in0=u, scalar1=-1.0, scalar2=1.0, op0=ALU.max, op1=ALU.min)
+
+        def transpose_u(k):
+            nt, n0 = tiles_of(k), GSTART[k]
+            tpu = psum.tile([P, nt, P], BF16, tag="z")
             for n in range(nt):
-                nc.tensor.transpose(tpx[:, n, :], xp[:, n0 + n, :], ident_b[:])
+                nc.tensor.transpose(tpu[:, n, :], up[:, n0 + n, :], ident_b[:])
+            tiles[k]["tpu"] = tpu
+
+        def transpose_x(k):
+            nt, n0 = tiles_of(k), GSTART[k]
+            tpx = psum.tile([P, nt, P], BF16, tag="ot", bufs=2)
+            for n in range(nt):
+                nc.tensor.transpose(tpx[:, n, :], x_sb[:, n0 + n, :], ident_b[:])
             tiles[k]["tpx"] = tpx
 
         def keep_xT(k):
-            nt, n0 = sum(GROUPS[k]), GSTART[k]
-            if k <= KEEP_ON_VECTOR:
-                nc.vector.tensor_copy(out=xT[:, n0:n0 + nt, :], in_=tiles[k]["tpx"][:])
-            else:
-                nc.scalar.copy(out=xT[:, n0:n0 + nt, :], in_=tiles[k]["tpx"][:])
+            nt, n0 = tiles_of(k), GSTART[k]
+            nc.scalar.copy(out=xT[:, n0:n0 + nt, :], in_=tiles[k]["tpx"][:])
 
-        def clamp(k):
-            nt, n0 = sum(GROUPS[k]), GSTART[k]
-            nu, f = dims(k)
-            u = ew.tile([P, nu, f], BF16, tag="u", bufs=3)
-            nc.vector.tensor_scalar(
-                out=u[:].rearrange("p d f -> p (d f)"), in0=xT[:, n0:n0 + nt, :].rearrange("p n w -> p (n w)"),
-                scalar1=-1.0, scalar2=1.0, op0=ALU.max, op1=ALU.min,
+        def fold_1(k):
+            nt = tiles_of(k)
+            dh = ew.tile([P, nt * P], F32, tag="dh")
+            nc.scalar.activation(out=dh[:], in_=tiles[k]["tpu"][:].rearrange("p n w -> p (n w)"), func=ACT.Abs, bias=0.5, scale=2.5)
+            tiles[k]["dh"] = dh
+
+        def fold_2(k):
+            dh = tiles[k]["dh"]
+            nc.scalar.activation(out=dh[:], in_=dh[:], func=ACT.Abs, bias=-2.0, scale=1.0)
+
+        def fold_3(k):
+            dh = tiles[k]["dh"]
+            nc.scalar.activation(out=dh[:], in_=dh[:], func=ACT.Abs, bias=-0.5, scale=0.5)
+
+        def square(k, y):
+            nt = tiles_of(k)
+            if "sq" not in tiles[k]:
+                tiles[k]["sq"] = ew.tile([P, 2, nt * P], F32, tag="sq", name="sq")
+                tiles[k]["cub"] = ew.tile([P, 2, nt * P], F32, tag="cub", name="cub")
+            nc.scalar.activation(
+                out=tiles[k]["sq"][:, y, :], in_=tiles[k]["dh"][:], func=ACT.Square,
+                bias=(root2, 0.0)[y], scale=(-2.0 * root2, 2.0 * root2)[y],
             )
-            tiles[k]["u"] = u
-            tiles[k]["de"] = ew.tile([P, nu, 2, f], F32, tag="de", name="de")
 
-        def fold_1(k, un):
-            nc.scalar.activation(out=tiles[k]["de"][:, un, 1, :], in_=tiles[k]["u"][:, un, :], func=ACT.Abs, bias=0.5, scale=2.5)
-
-        def fold_2(k, un):
-            d_odd = tiles[k]["de"][:, un, 1, :]
-            nc.scalar.activation(out=d_odd, in_=d_odd, func=ACT.Abs, bias=-2.0, scale=1.0)
-
-        def fold_3(k, un):
-            d_odd = tiles[k]["de"][:, un, 1, :]
-            nc.scalar.activation(out=d_odd, in_=d_odd, func=ACT.Abs, bias=-1.0, scale=1.0)
-
-        def other_distance(k):
-            de = tiles[k]["de"]
-            nc.scalar.activation(out=de[:, :, 0, :], in_=de[:, :, 1, :], func=ACT.Identity, bias=1.0, scale=-1.0)
-
-        def squares(k):
-            nu, f = dims(k)
-            sq = ew.tile([P, nu, 2, f], F32, tag="sq")
-            nc.scalar.activation(out=sq[:], in_=tiles[k]["de"][:], func=ACT.Square, bias=0.0, scale=r2)
-            tiles[k]["sq"] = sq
-
-        def ring_piece(k):
-            nu, f = dims(k)
-            ring = ew.tile([P, nu, 2, f], BF16, tag="ring", bufs=1)
+        def cube(k, y):
+            dh, sq, cub = tiles[k]["dh"], tiles[k]["sq"], tiles[k]["cub"]
             nc.vector.scalar_tensor_tensor(
-                out=ring[:].rearrange("p d y f -> p (d y f)"), in0=tiles[k]["sq"][:].rearrange("p d y f -> p (d y f)"), scalar=1.0 / 12.0,
-                in1=tiles[k]["de"][:].rearrange("p d y f -> p (d y f)"), op0=ALU.mult, op1=ALU.mult,
-            )
-            tiles[k]["ring"] = ring
-
-        def inner_cubic(k):
-            sq = tiles[k]["sq"]
-            nc.vector.scalar_tensor_tensor(
-                out=sq[:].rearrange("p d y f -> p (d y f)"), in0=tiles[k]["de"][:].rearrange("p d y f -> p (d y f)"), scalar=2.0,
-                in1=sq[:].rearrange("p d y f -> p (d y f)"), op0=ALU.subtract, op1=ALU.mult,
+                out=cub[:, y, :], in0=(dh[:], sq[:, 1, :])[y], scalar=(0.5, -1.0)[y], in1=(sq[:, 0, :], dh[:])[y],
+                op0=(ALU.subtract, ALU.mult)[y], op1=ALU.mult,
             )
 
-        def inner_piece(k):
-            nc.vector.scalar_tensor_tensor(
-                out=tiles[k]["v"][:, :, 2:4, :].rearrange("p d y f -> p d (y f)"), in0=tiles[k]["sq"][:].rearrange("p d y f -> p d (y f)"),
-                scalar=2.0 / 3.0, in1=tiles[k]["beta"][:].rearrange("p d y f -> p d (y f)"), op0=ALU.add, op1=ALU.mult,
-            )
+        def fill_inner(k, q):
+            sq, cub = tiles[k]["sq"], tiles[k]["cub"]
+            t = psum.tile([P, 2, 2, P], F32, tag="t", bufs=2)
+            for pos in range(2):
+                cols = slice((2 * q + pos) * P, (2 * q + pos + 1) * P)
+                for y in range(2):
+                    nc.tensor.matmul(out=t[:, pos, y, :], lhsT=sq[:, y, cols], rhs=ident_f[:], is_transpose=True, start=True, stop=False)
+                    nc.tensor.matmul(out=t[:, pos, y, :], lhsT=cub[:, y, cols], rhs=ident_f[:], is_transpose=True, start=False, stop=True)
+            tiles[k][("t", q)] = t
 
-        def inner_negated(k):
-            nc.vector.tensor_scalar(
-                out=tiles[k]["v"][:, :, 0:2, :].rearrange("p d y f -> p d (y f)"), in0=tiles[k]["v"][:, :, 2:4, :].rearrange("p d y f -> p d (y f)"),
-                scalar1=-1.0, scalar2=None, op0=ALU.mult,
-            )
+        def fill_ring(k, q):
+            cub = tiles[k]["cub"]
+            t = psum.tile([P, 2, 2, P], F32, tag="c")
+            for pos in range(2):
+                cols = slice((2 * q + pos) * P, (2 * q + pos + 1) * P)
+                for y in range(2):
+                    nc.tensor.transpose(t[:, pos, y, :], cub[:, y, cols], ident_f[:])
+            tiles[k][("c", q)] = t
 
-        def knot_masks(k):
-            nu, f = dims(k)
-            gam = ew.tile([P, nu, 4, f], BF16, tag="gam")
+
+        def masks(k):
+            nt, n0 = tiles_of(k), GSTART[k]
+            gam = ew.tile([P, nt, 4, P], BF16, tag="gam")
             for s in (SLOT_OF_J[0], SLOT_OF_J[2], SLOT_OF_J[1], SLOT_OF_J[3]):
                 nc.vector.tensor_scalar(
-                    out=gam[:, :, s, :], in0=tiles[k]["u"][:], scalar1=0.4 * (J_OF_SLOT[s] + 1) - 1.0, scalar2=0.5, op0=ALU.is_gt, op1=ALU.subtract,
+                    out=gam[:, :, s, :], in0=up[:, n0:n0 + nt, :], scalar1=0.4 * (J_OF_SLOT[s] + 1) - 1.0, scalar2=0.5, op0=ALU.is_gt, op1=ALU.subtract,
                 )
             tiles[k]["gam"] = gam
 
         def near_masks(k):
-            nu, f = dims(k)
+            nt = tiles_of(k)
             gam = tiles[k]["gam"]
-            beta = ew.tile([P, nu, 2, f], BF16, tag="beta", bufs=1)
+            beta = ew.tile([P, nt, 2, P], BF16, tag="beta", bufs=1)
             for y in range(2):
                 nc.vector.tensor_tensor(
                     out=beta[:, :, y, :], in0=gam[:, :, SLOT_OF_J[y], :], in1=gam[:, :, SLOT_OF_J[y + 2], :], op=ALU.mult,
                 )
             tiles[k]["beta"] = beta
-            tiles[k]["v"] = ew.tile([P, nu, 4, f], BF16, tag="v", bufs=1, name="v")
-            tiles[k]["z"] = ew.tile([P, nu, 4, f], BF16, tag="z", name="z")
+            tiles[k]["v"] = ew.tile([P, nt, 4, P], BF16, tag="v", name="v")
+            tiles[k]["z"] = ew.tile([P, nt, 4, P], BF16, tag="z", name="z")
+            tiles[k]["ring"] = ew.tile([P, nt, 2, P], BF16, tag="ring", name="ring")
 
-        def ring_elsewhere(k, un):
-            f = GROUPS[k][un] * P
-            v4 = tiles[k]["v"][:, un].rearrange("p (e y) f -> p e (y f)", e=2)
-            nc.vector.tensor_tensor(
-                out=v4, in0=v4, in1=tiles[k]["ring"][:, un].rearrange("p y f -> p (y f)").unsqueeze(1).to_broadcast([P, 2, 2 * f]), op=ALU.max,
+        def inner(k, q):
+            ns = slice(2 * q, 2 * q + 2)
+            nc.vector.scalar_tensor_tensor(
+                out=tiles[k]["v"][:, ns, 0:2, :].rearrange("p n y f -> p n (y f)"), in0=tiles[k][("t", q)][:].rearrange("p n y f -> p n (y f)"),
+                scalar=4.0 / 3.0, in1=tiles[k]["beta"][:, ns].rearrange("p n y f -> p n (y f)"), op0=ALU.subtract, op1=ALU.mult,
             )
 
+        def ring(k, q):
+            ns = slice(2 * q, 2 * q + 2)
+            nc.scalar.activation(
+                out=tiles[k]["ring"][:, ns].rearrange("p n y f -> p (n y f)"), in_=tiles[k][("c", q)][:].rearrange("p n y f -> p (n y f)"),
+                func=ACT.Copy, bias=0.0, scale=-1.0 / 12.0,
+            )
+
+        def inner_negated(k, un):
+            n0, n1 = unit_tiles(k, un)
+            v = tiles[k]["v"]
+            nc.vector.tensor_scalar(
+                out=v[:, n0:n1, 2:4, :].rearrange("p n y f -> p n (y f)"), in0=v[:, n0:n1, 0:2, :].rearrange("p n y f -> p n (y f)"),
+                scalar1=-1.0, scalar2=None, op0=ALU.mult,
+            )
+
+        def ring_elsewhere(k, un):
+            n0, n1 = unit_tiles(k, un)
+            v4 = tiles[k]["v"][:, n0:n1].rearrange("p n (e y) f -> p n e (y f)", e=2)
+            r4 = tiles[k]["ring"][:, n0:n1].rearrange("p n y f -> p n (y f)").unsqueeze(2).to_broadcast([P, n1 - n0, 2, 2 * P])
+            nc.vector.tensor_tensor(out=v4, in0=v4, in1=r4, op=ALU.max)
+
         def signed(k, un):
-            nc.vector.tensor_tensor(out=tiles[k]["z"][:, un], in0=tiles[k]["v"][:, un], in1=tiles[k]["gam"][:, un], op=ALU.mult)
+            n0, n1 = unit_tiles(k, un)
+            nc.vector.tensor_tensor(out=tiles[k]["z"][:, n0:n1], in0=tiles[k]["v"][:, n0:n1], in1=tiles[k]["gam"][:, n0:n1], op=ALU.mult)
 
-        def regroup(k, un, g, c0, c1, on_vector):
-            if ("gr", un) not in tiles[k]:
-                tiles[k][("gr", un)] = be.tile([P, 2, 4 * GROUPS[k][un] * P], BF16, tag="gr", bufs=4, align_bytes=64, name="gr")
-            dst = tiles[k][("gr", un)][:, g, 4 * c0:4 * c1].rearrange("p (q v s) -> p q s v", v=4, s=4)
-            src = tiles[k]["z"][:, un, :, c0:c1].rearrange("p s (q v) -> p q s v", v=4)
-            sign = 8.0 if g == 1 else -8.0
-            if on_vector:
-                nc.vector.tensor_scalar(out=dst, in0=src, scalar1=sign, scalar2=0.0, op0=ALU.mult, op1=ALU.max)
-            else:
-                nc.scalar.activation(out=dst, in_=src, func=ACT.Relu, bias=0.0, scale=sign)
 
-        def shrinks(k):
-            return exists(k) and exists(k + 1) and sum(GROUPS[k + 1]) < sum(GROUPS[k])
+        def fill_z(k, q):
+            z = tiles[k]["z"]
+            t = psum.tile([P, 2, 2, P], F32, tag="z")
+            for pos in range(2):
+                for e in range(2):
+                    nc.tensor.transpose(
+                        t[:, pos, e, :], words(z[:, 2 * q + pos, 2 * e:2 * e + 2, :].rearrange("p s f -> p (s f)")), ident_f[:],
+                    )
+            tiles[k][("zt", q)] = t
 
-        def shares(k):
-            f = dims(k)[1]
-            if short(k):
-                pieces = 4.0
-            elif shrinks(k):
-                pieces = 2.0 * V_PIECES
-            elif shrinks(k - 1):
-                pieces = 0.0
-            else:
-                pieces = V_PIECES
-            left = int(pieces * f)
-            for_scalar, for_vector = [], []
-            for un, g in ((1, 0), (1, 1), (0, 0), (0, 1)):
-                take = min(f, left)
-                left -= take
-                if take < f:
-                    for_scalar.append((un, g, 0, f - take))
-                if take > 0:
-                    for_vector.append((un, g, f - take, f))
-            return list(reversed(for_scalar)), list(reversed(for_vector))
+        def copy_z(k, q):
+            un = 0 if 2 * q < GROUPS[k][0] else 1
+            n0, n1 = unit_tiles(k, un)
+            if ("gz", un) not in tiles[k]:
+                tiles[k][("gz", un)] = be.tile([P, 4 * P * (n1 - n0)], BF16, tag="gz", bufs=3, align_bytes=64, name="gz")
+            first = (2 * q - n0) * 4 * P
+            nc.scalar.copy(
+                out=words(tiles[k][("gz", un)][:, first:first + 8 * P]).rearrange("p (n b e) -> p n b e", n=2, e=2),
+                in_=tiles[k][("zt", q)][:].rearrange("p n e b -> p n b e"),
+            )
 
-        def quantise_multiply(k, un):
-            f = GROUPS[k][un] * P
-            bcodes = be.tile([P, 2, f], U32, tag="bcodes", bufs=4, align_bytes=64)
-            bscales = be.tile([P, 2, f], U8, tag="bscales", bufs=4, align_bytes=64)
+        def halves(k, un):
+            n0, n1 = unit_tiles(k, un)
+            gr = be.tile([P, 2, 4 * P * (n1 - n0)], BF16, tag="gr", align_bytes=64)
+            for g in range(2):
+                nc.vector.tensor_scalar(
+                    out=gr[:, g, :], in0=tiles[k][("gz", un)][:], scalar1=(-4.0, 4.0)[g], scalar2=0.0, op0=ALU.mult, op1=ALU.max,
+                )
+            tiles[k][("gr", un)] = gr
+
+        def quantise(k, un):
+            n0, n1 = unit_tiles(k, un)
+            f = P * (n1 - n0)
+            bcodes = be.tile([P, 2, f], U32, tag="bcodes", align_bytes=64)
+            bscales = be.tile([P, 2, f], U8, tag="bscales", align_bytes=64)
             nc.vector.quantize_mx(
                 out=bcodes[:].rearrange("p g w -> p (g w)").bitcast(FP8X4),
                 scales=bscales[:].rearrange("p g w -> p (g w)"),
                 in_=tiles[k][("gr", un)][:].rearrange("p g w -> p (g w)"),
             )
+            tiles[k][("q", un)] = (bcodes, bscales)
+
+        def multiply(k, un):
+            n0, n1 = unit_tiles(k, un)
+            bcodes, bscales = tiles[k][("q", un)]
             mxs = []
             for h in range(2):
-                mx = psum.tile([P, f], F32, tag="mx", bufs=4)
+                mx = psum.tile([P, P * (n1 - n0)], F32, tag="mx", bufs=2)
                 for g in range(2):
                     nc.tensor.matmul_mx(
                         out=mx[:],
@@ -310,38 +337,41 @@ def tile_bsplinebasis_v2_t_kernel(tc, x, spline_coeffs, residual_weight, residua
                 mxs.append(mx)
             tiles[k][("mx", un)] = mxs
 
-        def scale_add_residual(k, un):
-            nt = GROUPS[k][un]
-            n0 = GSTART[k] + sum(GROUPS[k][:un])
+        def scale_add(k, un):
+            n0, n1 = unit_tiles(k, un)
             t1s = []
             for h in range(2):
-                t1 = be.tile([P, nt * P], F32, tag="t1_%d" % h, bufs=3)
+                t1 = be.tile([P, P * (n1 - n0)], F32, tag="t1_%d" % h)
                 nc.scalar.activation(
                     out=t1[:], in_=tiles[k][("mx", un)][h][:], func=ACT.Identity, bias=bias[:, h:h + 1], scale=scale[:, h:h + 1],
                 )
                 t1s.append(t1)
+            tiles[k][("t1", un)] = t1s
+
+        def add_residual(k, un):
+            n0, n1 = unit_tiles(k, un)
+            t1s = tiles[k][("t1", un)]
             ots = []
-            for first in range(0, nt, 2):
-                count = min(2, nt - first)
-                ot = psum.tile([P, count, O], F32, tag="ot", bufs=3)
-                for pos in range(count):
+            for first in range(n0, n1, 2):
+                ot = psum.tile([P, 2, O], F32, tag="ot", bufs=2)
+                for pos in range(2):
                     n = first + pos
+                    nc.tensor.matmul(out=ot[:, pos, :], lhsT=xT[:, GSTART[k] + n, :], rhs=rwT[:], start=True, stop=False)
                     for h in range(2):
-                        dst = ot[:, pos, h * P:(h + 1) * P]
-                        nc.tensor.matmul(out=dst, lhsT=xT[:, n0 + n, :], rhs=rwT[:, h, :], start=True, stop=False)
                         nc.tensor.matmul(
-                            out=dst, lhsT=t1s[h][:, n * P:(n + 1) * P], rhs=ident_f[:], is_transpose=True, start=False, stop=True,
+                            out=ot[:, pos, h * P:(h + 1) * P], lhsT=t1s[h][:, (n - n0) * P:(n - n0 + 1) * P], rhs=ident_f[:],
+                            is_transpose=True, start=False, stop=(h == 1),
                         )
-                ots.append((first, count, ot))
+                ots.append(ot)
             tiles[k][("ot", un)] = ots
 
         def store(k, un):
-            nt = GROUPS[k][un]
-            n0 = GSTART[k] + sum(GROUPS[k][:un])
-            osb = be.tile([P, nt, O], F32, tag="osb", bufs=3)
-            for first, count, ot in tiles[k][("ot", un)]:
-                nc.scalar.copy(out=osb[:, first:first + count, :], in_=ot[:])
-            nc.sync.dma_start(out=out_v[:, n0:n0 + nt, :], in_=osb[:])
+            n0, n1 = unit_tiles(k, un)
+            osb = be.tile([P, n1 - n0, O], F32, tag="osb", bufs=3)
+            ots = tiles[k][("ot", un)]
+            for i in range(len(ots)):
+                nc.scalar.copy(out=osb[:, 2 * i:2 * i + 2, :], in_=ots[i][:])
+            nc.sync.dma_start(out=out_v[:, GSTART[k] + n0:GSTART[k] + n1, :], in_=osb[:])
 
 
         def whole(k, *steps):
@@ -349,85 +379,92 @@ def tile_bsplinebasis_v2_t_kernel(tc, x, spline_coeffs, residual_weight, residua
                 for step in steps:
                     step(k)
 
-        def unit(k, un, step):
-            if un < units(k):
-                step(k, un)
+        def cls(k, y, step):
+            if exists(k):
+                step(k, y)
 
-        def alternating(k, *steps):
-            for step in steps:
-                for un in range(units(k)):
+        def unit(k, un, *steps):
+            if exists(k) and un < len(GROUPS[k]):
+                for step in steps:
                     step(k, un)
 
-        def due(k, un, step):
-            if exists(k - 2) and not short(k - 2):
-                unit(k - 2, un, step)
-            if short(k - 1):
-                unit(k - 1, un, step)
+        def pair(k, q, step):
+            if exists(k) and q < tiles_of(k) // 2:
+                step(k, q)
 
-        def due_units(k):
-            found = []
-            if exists(k - 2) and not short(k - 2):
-                found.extend([(k - 2, un) for un in range(units(k - 2))])
-            if short(k - 1):
-                found.extend([(k - 1, un) for un in range(units(k - 1))])
-            return found
+        def unit_pair(k, un, i, step):
+            if exists(k) and un < len(GROUPS[k]) and 2 * i < GROUPS[k][un]:
+                step(k, sum(GROUPS[k][:un]) // 2 + i)
 
-        def scalar_regroups(k, un):
-            if exists(k):
-                for piece in shares(k)[0]:
-                    if piece[0] == un:
-                        regroup(k, *piece, on_vector=False)
-
-        def vector_regroups(k):
-            if exists(k):
-                for piece in shares(k)[1]:
-                    regroup(k, *piece, on_vector=True)
-
-        for k in range(-3, NG + 3):
-            if k < 0:
-                permute(k + 3)
-            whole(k + 3, transpose_x)
-            whole(k, knot_masks)
-            if not short(k - 1):
-                vector_regroups(k - 1)
-            last_rounds = k >= NG - 1
-            if last_rounds:
-                leaving = due_units(k)
-                for i in range(len(leaving)):
-                    scale_add_residual(*leaving[i])
-                    if i >= 2:
-                        store(*leaving[i - 2])
-                for kk_un in leaving[-2:]:
-                    store(*kk_un)
-            else:
-                due(k, 0, scale_add_residual)
-                scalar_regroups(k - 1, 0)
-                scalar_regroups(k - 1, 1)
-                due(k, 0, store)
-                due(k, 1, scale_add_residual)
-            whole(k, ring_piece, near_masks, inner_cubic)
+        permute(0)
+        permute(1)
+        clamp(0)
+        clamp(1)
+        for k in range(-2, NG + 2):
+            pair(k, 0, inner)
+            pair(k, 2, fill_inner)
+            pair(k, 0, ring)
+            pair(k, 1, fill_ring)
+            unit(k - 1, 0, halves)
+            cls(k + 1, 1, square)
+            unit_pair(k - 1, 1, 0, copy_z)
+            unit_pair(k - 1, 1, 1, fill_z)
+            pair(k, 1, inner)
+            pair(k, 3, fill_inner)
             if k == 1:
                 weights_finish()
-            if not short(k - 1):
-                unit(k - 1, 0, quantise_multiply)
-            whole(k, inner_piece)
-            alternating(k + 1, fold_1, fold_2, fold_3)
-            whole(k + 2, clamp)
-            whole(k, inner_negated)
-            if not short(k - 1):
-                unit(k - 1, 1, quantise_multiply)
-            whole(k + 3, keep_xT)
-            whole(k + 1, other_distance)
-            if not last_rounds:
-                due(k, 1, store)
-            whole(k + 1, squares)
-            alternating(k, ring_elsewhere, signed)
-            if short(k):
-                vector_regroups(k)
-                alternating(k, quantise_multiply)
+            unit(k - 1, 0, quantise, multiply)
+            pair(k, 1, ring)
+            pair(k, 2, fill_ring)
+            unit_pair(k - 1, 1, 1, copy_z)
+            whole(k + 2, transpose_u)
+            cls(k + 1, 0, square)
+            pair(k, 2, inner)
+            unit(k - 1, 1, halves)
+            pair(k, 2, ring)
+            pair(k, 3, fill_ring)
+            unit(k - 1, 0, scale_add)
+            unit(k, 0, inner_negated)
+            pair(k, 3, inner)
+            pair(k, 3, ring)
+            unit(k - 1, 1, quantise)
+            unit(k - 1, 0, add_residual)
+            unit(k - 1, 1, multiply)
+            whole(k + 2, fold_1)
+            cls(k + 1, 1, cube)
+            unit(k, 0, ring_elsewhere)
+            unit(k - 1, 0, store)
+            whole(k + 1, transpose_x)
+            unit(k, 1, inner_negated)
+            unit(k - 1, 1, scale_add)
+            unit(k, 0, signed)
+            unit_pair(k, 0, 0, fill_z)
+            unit(k - 1, 1, add_residual)
+            whole(k + 2, fold_2)
+            whole(k + 1, keep_xT)
+            unit(k, 1, ring_elsewhere)
+            cls(k + 1, 0, cube)
+            unit_pair(k, 0, 0, copy_z)
+            pair(k + 1, 0, fill_inner)
+            unit_pair(k, 0, 1, fill_z)
+            pair(k + 1, 1, fill_inner)
+            pair(k + 1, 0, fill_ring)
+            whole(k + 2, fold_3)
+            unit_pair(k, 0, 1, copy_z)
+            whole(k + 1, masks, near_masks)
+            unit(k, 1, signed)
+            unit_pair(k, 1, 0, fill_z)
+            unit(k - 1, 1, store)
+            if k == -2:
+                weights_permute()
+                permute(2)
+                permute(3)
+                clamp(2)
             if k == -1:
                 weights_transpose()
-                for later in range(3, NG):
+                for later in range(4, NG):
                     permute(later)
+                for later in range(3, NG):
+                    clamp(later)
             if k == 0:
                 weights_leave_psum()

@@ -15,7 +15,7 @@ ACT = mybir.ActivationFunctionType
 P = 128
 B, I, O, NBAS = 8192, 128, 256, 8
 NT = B // P
-GROUPS = [[2], [2, 2]] + [[4, 4]] * 6 + [[2, 2], [2, 2], [2]]
+GROUPS = [[2, 2]] + [[4, 4]] * 7 + [[2, 2]]
 NG = len(GROUPS)
 GSTART = [sum(sum(grp) for grp in GROUPS[:k]) for k in range(NG)]
 J_OF_SLOT = (3, 0, 1, 2)
@@ -94,9 +94,14 @@ def tile_bsplinebasis_v2_t_kernel(tc, x, spline_coeffs, residual_weight, residua
                 )
 
         def weights_transpose():
+            rwp = setup.tile([P, 2, I], BF16)
+            nc.vector.tensor_copy(
+                out=rwp[:].rearrange("p h (c a m l) -> p (h c) a m l", c=2, a=4, m=4, l=4),
+                in_=rw_sb[:].rearrange("p h (c m a l) -> p (h c) a m l", c=2, m=4, a=4, l=4),
+            )
             tpr = psum.tile([P, 3, P], BF16, tag="ot", bufs=2)
             for h in range(2):
-                nc.tensor.transpose(tpr[:, h, :], rw_sb[:, h, :], ident_b[:])
+                nc.tensor.transpose(tpr[:, h, :], rwp[:, h, :], ident_b[:])
             nc.tensor.transpose(tpr[:, 2, :], b_sb[:], ident_b[:])
             wt["tpr"] = tpr
             for h in range(2):
@@ -147,33 +152,29 @@ def tile_bsplinebasis_v2_t_kernel(tc, x, spline_coeffs, residual_weight, residua
                 in_=x_sb[:, n0:n0 + nt, :].rearrange("p n (c m a l) -> p (n c) a m l", c=2, m=4, a=4, l=4),
             )
 
-        def clamp(k):
-            nt, n0 = tiles_of(k), GSTART[k]
-            u = up[:, n0:n0 + nt, :].rearrange("p n i -> p (n i)")
-            nc.vector.tensor_scalar(out=u, in0=u, scalar1=-1.0, scalar2=1.0, op0=ALU.max, op1=ALU.min)
-
-        def transpose_u(k):
-            nt, n0 = tiles_of(k), GSTART[k]
-            tpu = psum.tile([P, nt, P], BF16, tag="z")
-            for n in range(nt):
-                nc.tensor.transpose(tpu[:, n, :], up[:, n0 + n, :], ident_b[:])
-            tiles[k]["tpu"] = tpu
-
         def transpose_x(k):
             nt, n0 = tiles_of(k), GSTART[k]
-            tpx = psum.tile([P, nt, P], BF16, tag="ot", bufs=2)
+            tpx = psum.tile([P, nt, P], BF16, tag="z", bufs=2)
             for n in range(nt):
-                nc.tensor.transpose(tpx[:, n, :], x_sb[:, n0 + n, :], ident_b[:])
+                nc.tensor.transpose(tpx[:, n, :], up[:, n0 + n, :], ident_b[:])
             tiles[k]["tpx"] = tpx
 
         def keep_xT(k):
             nt, n0 = tiles_of(k), GSTART[k]
             nc.scalar.copy(out=xT[:, n0:n0 + nt, :], in_=tiles[k]["tpx"][:])
 
+        def clamp(k):
+            nt, n0 = tiles_of(k), GSTART[k]
+            u = ew.tile([P, nt * P], BF16, tag="u", name="u")
+            nc.vector.tensor_scalar(
+                out=u[:], in0=xT[:, n0:n0 + nt, :].rearrange("p n w -> p (n w)"), scalar1=-1.0, scalar2=1.0, op0=ALU.max, op1=ALU.min,
+            )
+            tiles[k]["u"] = u
+
         def fold_1(k):
             nt = tiles_of(k)
             dh = ew.tile([P, nt * P], F32, tag="dh")
-            nc.scalar.activation(out=dh[:], in_=tiles[k]["tpu"][:].rearrange("p n w -> p (n w)"), func=ACT.Abs, bias=0.5, scale=2.5)
+            nc.scalar.activation(out=dh[:], in_=tiles[k]["u"][:], func=ACT.Abs, bias=0.5, scale=2.5)
             tiles[k]["dh"] = dh
 
         def fold_2(k):
@@ -203,7 +204,7 @@ def tile_bsplinebasis_v2_t_kernel(tc, x, spline_coeffs, residual_weight, residua
 
         def fill_inner(k, q):
             sq, cub = tiles[k]["sq"], tiles[k]["cub"]
-            t = psum.tile([P, 2, 2, P], F32, tag="t", bufs=2)
+            t = psum.tile([P, 2, 2, P], F32, tag="t", bufs=1)
             for pos in range(2):
                 cols = slice((2 * q + pos) * P, (2 * q + pos + 1) * P)
                 for y in range(2):
@@ -221,14 +222,14 @@ def tile_bsplinebasis_v2_t_kernel(tc, x, spline_coeffs, residual_weight, residua
             tiles[k][("c", q)] = t
 
 
-        def masks(k):
+        def mask(k, i):
             nt, n0 = tiles_of(k), GSTART[k]
-            gam = ew.tile([P, nt, 4, P], BF16, tag="gam")
-            for s in (SLOT_OF_J[0], SLOT_OF_J[2], SLOT_OF_J[1], SLOT_OF_J[3]):
-                nc.vector.tensor_scalar(
-                    out=gam[:, :, s, :], in0=up[:, n0:n0 + nt, :], scalar1=0.4 * (J_OF_SLOT[s] + 1) - 1.0, scalar2=0.5, op0=ALU.is_gt, op1=ALU.subtract,
-                )
-            tiles[k]["gam"] = gam
+            if i == 0:
+                tiles[k]["gam"] = ew.tile([P, nt, 4, P], BF16, tag="gam", name="gam")
+            s = (SLOT_OF_J[0], SLOT_OF_J[2], SLOT_OF_J[1], SLOT_OF_J[3])[i]
+            nc.vector.tensor_scalar(
+                out=tiles[k]["gam"][:, :, s, :], in0=up[:, n0:n0 + nt, :], scalar1=0.4 * (J_OF_SLOT[s] + 1) - 1.0, scalar2=0.5, op0=ALU.is_gt, op1=ALU.subtract,
+            )
 
         def near_masks(k):
             nt = tiles_of(k)
@@ -249,6 +250,18 @@ def tile_bsplinebasis_v2_t_kernel(tc, x, spline_coeffs, residual_weight, residua
                 out=tiles[k]["v"][:, ns, 0:2, :].rearrange("p n y f -> p n (y f)"), in0=tiles[k][("t", q)][:].rearrange("p n y f -> p n (y f)"),
                 scalar=4.0 / 3.0, in1=tiles[k]["beta"][:, ns].rearrange("p n y f -> p n (y f)"), op0=ALU.subtract, op1=ALU.mult,
             )
+
+        def inner_raw(k, q):
+            ns = slice(2 * q, 2 * q + 2)
+            nc.scalar.activation(
+                out=tiles[k]["v"][:, ns, 0:2, :].rearrange("p n y f -> p n (y f)"), in_=tiles[k][("t", q)][:].rearrange("p n y f -> p n (y f)"),
+                func=ACT.Identity, bias=-4.0 / 3.0, scale=1.0,
+            )
+
+        def inner_masked(k, q):
+            ns = slice(2 * q, 2 * q + 2)
+            v = tiles[k]["v"][:, ns, 0:2, :].rearrange("p n y f -> p n (y f)")
+            nc.vector.tensor_tensor(out=v, in0=v, in1=tiles[k]["beta"][:, ns].rearrange("p n y f -> p n (y f)"), op=ALU.mult)
 
         def ring(k, q):
             ns = slice(2 * q, 2 * q + 2)
@@ -278,7 +291,7 @@ def tile_bsplinebasis_v2_t_kernel(tc, x, spline_coeffs, residual_weight, residua
 
         def fill_z(k, q):
             z = tiles[k]["z"]
-            t = psum.tile([P, 2, 2, P], F32, tag="z")
+            t = psum.tile([P, 2, 2, P], F32, tag="z", bufs=2)
             for pos in range(2):
                 for e in range(2):
                     nc.tensor.transpose(
@@ -299,79 +312,64 @@ def tile_bsplinebasis_v2_t_kernel(tc, x, spline_coeffs, residual_weight, residua
 
         def halves(k, un):
             n0, n1 = unit_tiles(k, un)
-            gr = be.tile([P, 2, 4 * P * (n1 - n0)], BF16, tag="gr", align_bytes=64)
+            np = (n1 - n0) // 2
+            gr = be.tile([P, np, 2, 8 * P], BF16, tag="gr", align_bytes=64)
             for g in range(2):
                 nc.vector.tensor_scalar(
-                    out=gr[:, g, :], in0=tiles[k][("gz", un)][:], scalar1=(-4.0, 4.0)[g], scalar2=0.0, op0=ALU.mult, op1=ALU.max,
+                    out=gr[:, :, g, :], in0=tiles[k][("gz", un)][:].rearrange("p (q w) -> p q w", q=np),
+                    scalar1=(-4.0, 4.0)[g], scalar2=0.0, op0=ALU.mult, op1=ALU.max,
                 )
-            tiles[k][("gr", un)] = gr
+            for i in range(np):
+                tiles[k][("gr", n0 // 2 + i)] = gr[:, i]
 
-        def quantise(k, un):
-            n0, n1 = unit_tiles(k, un)
-            f = P * (n1 - n0)
-            bcodes = be.tile([P, 2, f], U32, tag="bcodes", align_bytes=64)
-            bscales = be.tile([P, 2, f], U8, tag="bscales", align_bytes=64)
+        def quantise(k, q):
+            f = 2 * P
+            bcodes = be.tile([P, 2, f], U32, tag="bcodes", bufs=3, align_bytes=64)
+            bscales = be.tile([P, 2, f], U8, tag="bscales", bufs=3, align_bytes=64)
             nc.vector.quantize_mx(
                 out=bcodes[:].rearrange("p g w -> p (g w)").bitcast(FP8X4),
                 scales=bscales[:].rearrange("p g w -> p (g w)"),
-                in_=tiles[k][("gr", un)][:].rearrange("p g w -> p (g w)"),
+                in_=tiles[k][("gr", q)].rearrange("p g w -> p (g w)"),
             )
-            tiles[k][("q", un)] = (bcodes, bscales)
+            tiles[k][("q", q)] = (bcodes, bscales)
 
-        def multiply(k, un):
-            n0, n1 = unit_tiles(k, un)
-            bcodes, bscales = tiles[k][("q", un)]
-            mxs = []
-            for h in range(2):
-                mx = psum.tile([P, P * (n1 - n0)], F32, tag="mx", bufs=2)
-                for g in range(2):
-                    nc.tensor.matmul_mx(
-                        out=mx[:],
-                        lhsT=ccodes[:, g, h * P:(h + 1) * P].bitcast(FP8X4),
-                        lhsT_scale=cscales[:, g, h * P:(h + 1) * P],
-                        rhs=bcodes[:, g, :].bitcast(FP8X4),
-                        rhs_scale=bscales[:, g, :],
-                        start=(g == 0),
-                        stop=(g == 1),
-                    )
-                mxs.append(mx)
-            tiles[k][("mx", un)] = mxs
-
-        def scale_add(k, un):
-            n0, n1 = unit_tiles(k, un)
-            t1s = []
-            for h in range(2):
-                t1 = be.tile([P, P * (n1 - n0)], F32, tag="t1_%d" % h)
-                nc.scalar.activation(
-                    out=t1[:], in_=tiles[k][("mx", un)][h][:], func=ACT.Identity, bias=bias[:, h:h + 1], scale=scale[:, h:h + 1],
+        def multiply(k, q, h):
+            bcodes, bscales = tiles[k][("q", q)]
+            if h == 0:
+                tiles[k][("mx", q)] = psum.tile([P, 2, 2 * P], F32, tag="mx", bufs=2, name="mx")
+            for g in range(2):
+                nc.tensor.matmul_mx(
+                    out=tiles[k][("mx", q)][:, h, :],
+                    lhsT=ccodes[:, g, h * P:(h + 1) * P].bitcast(FP8X4),
+                    lhsT_scale=cscales[:, g, h * P:(h + 1) * P],
+                    rhs=bcodes[:, g, :].bitcast(FP8X4),
+                    rhs_scale=bscales[:, g, :],
+                    start=(g == 0),
+                    stop=(g == 1),
                 )
-                t1s.append(t1)
-            tiles[k][("t1", un)] = t1s
 
-        def add_residual(k, un):
-            n0, n1 = unit_tiles(k, un)
-            t1s = tiles[k][("t1", un)]
-            ots = []
-            for first in range(n0, n1, 2):
-                ot = psum.tile([P, 2, O], F32, tag="ot", bufs=2)
-                for pos in range(2):
-                    n = first + pos
-                    nc.tensor.matmul(out=ot[:, pos, :], lhsT=xT[:, GSTART[k] + n, :], rhs=rwT[:], start=True, stop=False)
-                    for h in range(2):
-                        nc.tensor.matmul(
-                            out=ot[:, pos, h * P:(h + 1) * P], lhsT=t1s[h][:, (n - n0) * P:(n - n0 + 1) * P], rhs=ident_f[:],
-                            is_transpose=True, start=False, stop=(h == 1),
-                        )
-                ots.append(ot)
-            tiles[k][("ot", un)] = ots
+        def scale_add(k, q, h):
+            if h == 0:
+                tiles[k][("t1", q)] = be.tile([P, 2, 2 * P], F32, tag="t1", bufs=3, name="t1")
+            nc.scalar.activation(
+                out=tiles[k][("t1", q)][:, h, :], in_=tiles[k][("mx", q)][:, h, :], func=ACT.Identity, bias=bias[:, h:h + 1], scale=scale[:, h:h + 1],
+            )
 
-        def store(k, un):
-            n0, n1 = unit_tiles(k, un)
-            osb = be.tile([P, n1 - n0, O], F32, tag="osb", bufs=3)
-            ots = tiles[k][("ot", un)]
-            for i in range(len(ots)):
-                nc.scalar.copy(out=osb[:, 2 * i:2 * i + 2, :], in_=ots[i][:])
-            nc.sync.dma_start(out=out_v[:, GSTART[k] + n0:GSTART[k] + n1, :], in_=osb[:])
+        def add_residual(k, q, pos):
+            t1 = tiles[k][("t1", q)]
+            if pos == 0:
+                tiles[k][("ot", q)] = psum.tile([P, 2, O], F32, tag="ot", bufs=2, name="ot")
+            ot = tiles[k][("ot", q)]
+            nc.tensor.matmul(out=ot[:, pos, :], lhsT=xT[:, GSTART[k] + 2 * q + pos, :], rhs=rwT[:], start=True, stop=False)
+            cols = slice(pos * P, (pos + 1) * P)
+            nc.tensor.matmul(out=ot[:, pos, 0:P], lhsT=t1[:, 0, cols], rhs=ident_f[:], is_transpose=True, start=False, stop=False)
+            nc.tensor.matmul(out=ot[:, pos, P:O], lhsT=t1[:, 1, cols], rhs=ident_f[:], is_transpose=True, start=False, stop=True)
+
+        def store(k, q):
+            osb = be.tile([P, 2, O], F32, tag="osb", bufs=4)
+            nc.scalar.copy(out=osb[:], in_=tiles[k][("ot", q)][:])
+            n0 = GSTART[k] + 2 * q
+            nc.sync.dma_start(out=out_v[:, n0:n0 + 2, :], in_=osb[:])
 
 
         def whole(k, *steps):
@@ -379,7 +377,7 @@ def tile_bsplinebasis_v2_t_kernel(tc, x, spline_coeffs, residual_weight, residua
                 for step in steps:
                     step(k)
 
-        def cls(k, y, step):
+        def part(k, y, step):
             if exists(k):
                 step(k, y)
 
@@ -387,6 +385,10 @@ def tile_bsplinebasis_v2_t_kernel(tc, x, spline_coeffs, residual_weight, residua
             if exists(k) and un < len(GROUPS[k]):
                 for step in steps:
                     step(k, un)
+
+        def half(k, q, i, step):
+            if exists(k) and q < tiles_of(k) // 2:
+                step(k, q, i)
 
         def pair(k, q, step):
             if exists(k) and q < tiles_of(k) // 2:
@@ -396,75 +398,103 @@ def tile_bsplinebasis_v2_t_kernel(tc, x, spline_coeffs, residual_weight, residua
             if exists(k) and un < len(GROUPS[k]) and 2 * i < GROUPS[k][un]:
                 step(k, sum(GROUPS[k][:un]) // 2 + i)
 
-        permute(0)
-        permute(1)
-        clamp(0)
-        clamp(1)
-        for k in range(-2, NG + 2):
+        for k in range(-3, NG + 3):
+            if k == -3:
+                permute(0)
+                permute(1)
             pair(k, 0, inner)
-            pair(k, 2, fill_inner)
+            pair(k, 1, fill_inner)
             pair(k, 0, ring)
             pair(k, 1, fill_ring)
             unit(k - 1, 0, halves)
-            cls(k + 1, 1, square)
+            half(k - 2, 3, 0, add_residual)
+            part(k + 1, 0, mask)
+            part(k + 1, 1, mask)
+            part(k + 1, 1, square)
             unit_pair(k - 1, 1, 0, copy_z)
-            unit_pair(k - 1, 1, 1, fill_z)
-            pair(k, 1, inner)
-            pair(k, 3, fill_inner)
             if k == 1:
                 weights_finish()
-            unit(k - 1, 0, quantise, multiply)
+            pair(k - 1, 0, quantise)
+            half(k - 1, 0, 0, multiply)
+            pair(k, 1, inner)
+            pair(k, 2, fill_inner)
             pair(k, 1, ring)
             pair(k, 2, fill_ring)
             unit_pair(k - 1, 1, 1, copy_z)
-            whole(k + 2, transpose_u)
-            cls(k + 1, 0, square)
+            half(k - 1, 0, 1, multiply)
+            half(k - 2, 3, 1, add_residual)
+            part(k + 1, 2, mask)
+            part(k + 1, 3, mask)
+            half(k - 1, 0, 0, scale_add)
+            part(k + 1, 0, square)
+            part(k + 1, 1, cube)
+            half(k - 1, 0, 1, scale_add)
             pair(k, 2, inner)
-            unit(k - 1, 1, halves)
+            pair(k, 3, fill_inner)
             pair(k, 2, ring)
             pair(k, 3, fill_ring)
-            unit(k - 1, 0, scale_add)
+            pair(k - 2, 3, store)
             unit(k, 0, inner_negated)
-            pair(k, 3, inner)
+            if exists(k - 1) and tiles_of(k - 1) == 4:
+                halves(k - 1, 1)
+            pair(k - 1, 1, quantise)
+            half(k - 1, 1, 0, multiply)
+            half(k - 1, 0, 0, add_residual)
+            if exists(k - 1) and tiles_of(k - 1) == 8:
+                halves(k - 1, 1)
             pair(k, 3, ring)
-            unit(k - 1, 1, quantise)
-            unit(k - 1, 0, add_residual)
-            unit(k - 1, 1, multiply)
+            half(k - 1, 1, 1, multiply)
+            half(k - 1, 0, 1, add_residual)
+            pair(k, 3, inner)
+            half(k - 1, 1, 0, scale_add)
             whole(k + 2, fold_1)
-            cls(k + 1, 1, cube)
+            half(k - 1, 1, 1, scale_add)
+            pair(k - 1, 0, store)
             unit(k, 0, ring_elsewhere)
-            unit(k - 1, 0, store)
-            whole(k + 1, transpose_x)
-            unit(k, 1, inner_negated)
-            unit(k - 1, 1, scale_add)
-            unit(k, 0, signed)
-            unit_pair(k, 0, 0, fill_z)
-            unit(k - 1, 1, add_residual)
+            pair(k - 1, 2, quantise)
+            half(k - 1, 2, 0, multiply)
+            half(k - 1, 1, 0, add_residual)
             whole(k + 2, fold_2)
-            whole(k + 1, keep_xT)
-            unit(k, 1, ring_elsewhere)
-            cls(k + 1, 0, cube)
-            unit_pair(k, 0, 0, copy_z)
-            pair(k + 1, 0, fill_inner)
+            whole(k + 3, transpose_x)
+            unit(k, 1, inner_negated)
+            unit(k, 0, signed)
+            half(k - 1, 2, 0, scale_add)
+            whole(k + 3, keep_xT)
+            half(k - 1, 2, 1, multiply)
+            half(k - 1, 1, 1, add_residual)
+            unit_pair(k, 0, 0, fill_z)
             unit_pair(k, 0, 1, fill_z)
-            pair(k + 1, 1, fill_inner)
+            part(k + 1, 0, cube)
+            pair(k + 1, 0, fill_inner)
             pair(k + 1, 0, fill_ring)
+            unit_pair(k, 0, 0, copy_z)
+            half(k - 1, 2, 1, scale_add)
             whole(k + 2, fold_3)
+            pair(k - 1, 1, store)
+            unit(k, 1, ring_elsewhere)
+            pair(k - 1, 3, quantise)
+            half(k - 1, 3, 0, multiply)
+            half(k - 1, 2, 0, add_residual)
             unit_pair(k, 0, 1, copy_z)
-            whole(k + 1, masks, near_masks)
+            whole(k + 1, near_masks)
+            half(k - 1, 3, 0, scale_add)
+            half(k - 1, 3, 1, multiply)
+            half(k - 1, 2, 1, add_residual)
+            half(k - 1, 3, 1, scale_add)
+            whole(k + 3, clamp)
             unit(k, 1, signed)
             unit_pair(k, 1, 0, fill_z)
-            unit(k - 1, 1, store)
-            if k == -2:
-                weights_permute()
+            unit_pair(k, 1, 1, fill_z)
+            pair(k - 1, 2, store)
+            if k == -3:
                 permute(2)
+                weights_permute()
+            if k == -2:
                 permute(3)
-                clamp(2)
+                permute(4)
             if k == -1:
                 weights_transpose()
-                for later in range(4, NG):
+                for later in range(5, NG):
                     permute(later)
-                for later in range(3, NG):
-                    clamp(later)
             if k == 0:
                 weights_leave_psum()

@@ -15,7 +15,7 @@ ACT = mybir.ActivationFunctionType
 P = 128
 B, I, O, NBAS = 8192, 128, 256, 8
 NT = B // P
-GROUPS = [[2, 2]] + [[4, 4]] * 7 + [[2, 2]]
+GROUPS = [[2], [2, 2]] + [[4, 4]] * 7 + [[2]]
 NG = len(GROUPS)
 GSTART = [sum(sum(grp) for grp in GROUPS[:k]) for k in range(NG)]
 J_OF_SLOT = (3, 0, 1, 2)
@@ -36,7 +36,6 @@ def tile_bsplinebasis_v2_t_kernel(tc, x, spline_coeffs, residual_weight, residua
         ctx.enter_context(tc.manual_schedule())
 
         x_sb = const.tile([P, NT, I], BF16)
-        up = const.tile([P, NT, I], BF16)
         xT = const.tile([P, NT, P], BF16)
         x_v = x.rearrange("(p n) i -> p n i", n=NT)
         out_v = out.rearrange("(p n) o -> p n o", n=NT)
@@ -56,6 +55,13 @@ def tile_bsplinebasis_v2_t_kernel(tc, x, spline_coeffs, residual_weight, residua
         make_identity(nc, ident_b[:])
         ident_f = const.tile([P, P], F32)
         make_identity(nc, ident_f[:])
+
+        ident_p = const.tile([P, P], F32)
+        nc.gpsimd.tensor_copy(
+            out=ident_p[:].rearrange("p (a q l) -> p a q l", a=4, q=8), in_=ident_f[:].rearrange("p (q a l) -> p a q l", q=8, a=4),
+        )
+
+        perm = ident_p[:].rearrange("p (a i) -> p a i", a=4)
 
         c_sb = setup.tile([P, 2, I * NBAS], BF16)
         nc.sync.dma_start(out=c_sb[:], in_=spline_coeffs.rearrange("(h p) i j -> p h (i j)", p=P))
@@ -84,8 +90,8 @@ def tile_bsplinebasis_v2_t_kernel(tc, x, spline_coeffs, residual_weight, residua
 
         def weights_permute():
             nc.vector.tensor_copy(
-                out=cpm[:].rearrange("p h (c a m l) j -> p (h c) a m (l j)", c=2, a=4, m=4, l=4),
-                in_=c_sb[:].rearrange("p h (c m a z) -> p (h c) a m z", c=2, m=4, a=4, z=4 * NBAS),
+                out=cpm[:].rearrange("p h (a q l) j -> p h a q (l j)", a=4, q=8, l=4),
+                in_=c_sb[:].rearrange("p h (q a z) -> p h a q z", q=8, a=4, z=4 * NBAS),
             )
             for s in range(4):
                 nc.vector.tensor_copy(
@@ -94,14 +100,9 @@ def tile_bsplinebasis_v2_t_kernel(tc, x, spline_coeffs, residual_weight, residua
                 )
 
         def weights_transpose():
-            rwp = setup.tile([P, 2, I], BF16)
-            nc.vector.tensor_copy(
-                out=rwp[:].rearrange("p h (c a m l) -> p (h c) a m l", c=2, a=4, m=4, l=4),
-                in_=rw_sb[:].rearrange("p h (c m a l) -> p (h c) a m l", c=2, m=4, a=4, l=4),
-            )
             tpr = psum.tile([P, 3, P], BF16, tag="ot", bufs=2)
             for h in range(2):
-                nc.tensor.transpose(tpr[:, h, :], rwp[:, h, :], ident_b[:])
+                nc.tensor.transpose(tpr[:, h, :], rw_sb[:, h, :], ident_b[:])
             nc.tensor.transpose(tpr[:, 2, :], b_sb[:], ident_b[:])
             wt["tpr"] = tpr
             for h in range(2):
@@ -145,18 +146,11 @@ def tile_bsplinebasis_v2_t_kernel(tc, x, spline_coeffs, residual_weight, residua
             return first, first + GROUPS[k][un]
 
 
-        def permute(k):
-            nt, n0 = tiles_of(k), GSTART[k]
-            nc.vector.tensor_copy(
-                out=up[:, n0:n0 + nt, :].rearrange("p n (c a m l) -> p (n c) a m l", c=2, a=4, m=4, l=4),
-                in_=x_sb[:, n0:n0 + nt, :].rearrange("p n (c m a l) -> p (n c) a m l", c=2, m=4, a=4, l=4),
-            )
-
         def transpose_x(k):
             nt, n0 = tiles_of(k), GSTART[k]
             tpx = psum.tile([P, nt, P], BF16, tag="z", bufs=2)
             for n in range(nt):
-                nc.tensor.transpose(tpx[:, n, :], up[:, n0 + n, :], ident_b[:])
+                nc.tensor.transpose(tpx[:, n, :], x_sb[:, n0 + n, :], ident_b[:])
             tiles[k]["tpx"] = tpx
 
         def keep_xT(k):
@@ -204,89 +198,83 @@ def tile_bsplinebasis_v2_t_kernel(tc, x, spline_coeffs, residual_weight, residua
 
         def fill_inner(k, q):
             sq, cub = tiles[k]["sq"], tiles[k]["cub"]
-            t = psum.tile([P, 2, 2, P], F32, tag="t", bufs=1)
+            t = psum.tile([P, 8, 2, 32], F32, tag="t", bufs=1)
             for pos in range(2):
                 cols = slice((2 * q + pos) * P, (2 * q + pos + 1) * P)
                 for y in range(2):
-                    nc.tensor.matmul(out=t[:, pos, y, :], lhsT=sq[:, y, cols], rhs=ident_f[:], is_transpose=True, start=True, stop=False)
-                    nc.tensor.matmul(out=t[:, pos, y, :], lhsT=cub[:, y, cols], rhs=ident_f[:], is_transpose=True, start=False, stop=True)
+                    dst = t[:, 4 * y:4 * y + 4, pos, :]
+                    nc.tensor.matmul(out=dst, lhsT=sq[:, y, cols], rhs=perm, is_transpose=True, start=True, stop=False)
+                    nc.tensor.matmul(out=dst, lhsT=cub[:, y, cols], rhs=perm, is_transpose=True, start=False, stop=True)
             tiles[k][("t", q)] = t
 
         def fill_ring(k, q):
             cub = tiles[k]["cub"]
-            t = psum.tile([P, 2, 2, P], F32, tag="c")
+            t = psum.tile([P, 8, 2, 32], F32, tag="c")
             for pos in range(2):
                 cols = slice((2 * q + pos) * P, (2 * q + pos + 1) * P)
                 for y in range(2):
-                    nc.tensor.transpose(t[:, pos, y, :], cub[:, y, cols], ident_f[:])
+                    nc.tensor.matmul(out=t[:, 4 * y:4 * y + 4, pos, :], lhsT=cub[:, y, cols], rhs=perm, is_transpose=True, start=True, stop=True)
             tiles[k][("c", q)] = t
 
 
         def mask(k, i):
             nt, n0 = tiles_of(k), GSTART[k]
             if i == 0:
-                tiles[k]["gam"] = ew.tile([P, nt, 4, P], BF16, tag="gam", name="gam")
+                tiles[k]["gam"] = ew.tile([P, 16, nt, 32], BF16, tag="gam", name="gam")
             s = (SLOT_OF_J[0], SLOT_OF_J[2], SLOT_OF_J[1], SLOT_OF_J[3])[i]
             nc.vector.tensor_scalar(
-                out=tiles[k]["gam"][:, :, s, :], in0=up[:, n0:n0 + nt, :], scalar1=0.4 * (J_OF_SLOT[s] + 1) - 1.0, scalar2=0.5, op0=ALU.is_gt, op1=ALU.subtract,
+                out=tiles[k]["gam"][:, 4 * s:4 * s + 4].rearrange("p a n (q l) -> p a (n q) l", l=4),
+                in0=x_sb[:, n0:n0 + nt, :].rearrange("p n (q a l) -> p a (n q) l", a=4, l=4),
+                scalar1=0.4 * (J_OF_SLOT[s] + 1) - 1.0, scalar2=0.5, op0=ALU.is_gt, op1=ALU.subtract,
             )
 
         def near_masks(k):
             nt = tiles_of(k)
             gam = tiles[k]["gam"]
-            beta = ew.tile([P, nt, 2, P], BF16, tag="beta", bufs=1)
+            beta = ew.tile([P, 8, nt, 32], BF16, tag="beta", bufs=1)
             for y in range(2):
+                s0, s1 = SLOT_OF_J[y], SLOT_OF_J[y + 2]
                 nc.vector.tensor_tensor(
-                    out=beta[:, :, y, :], in0=gam[:, :, SLOT_OF_J[y], :], in1=gam[:, :, SLOT_OF_J[y + 2], :], op=ALU.mult,
+                    out=beta[:, 4 * y:4 * y + 4].rearrange("p a n i -> p (a n i)"), in0=gam[:, 4 * s0:4 * s0 + 4].rearrange("p a n i -> p (a n i)"),
+                    in1=gam[:, 4 * s1:4 * s1 + 4].rearrange("p a n i -> p (a n i)"), op=ALU.mult,
                 )
             tiles[k]["beta"] = beta
-            tiles[k]["v"] = ew.tile([P, nt, 4, P], BF16, tag="v", name="v")
-            tiles[k]["z"] = ew.tile([P, nt, 4, P], BF16, tag="z", name="z")
-            tiles[k]["ring"] = ew.tile([P, nt, 2, P], BF16, tag="ring", name="ring")
+            tiles[k]["v"] = ew.tile([P, 16, nt, 32], BF16, tag="v", name="v")
+            tiles[k]["z"] = ew.tile([P, nt, 16, 32], BF16, tag="z", name="z")
+            tiles[k]["ring"] = ew.tile([P, 8, nt, 32], BF16, tag="ring", name="ring")
 
         def inner(k, q):
             ns = slice(2 * q, 2 * q + 2)
             nc.vector.scalar_tensor_tensor(
-                out=tiles[k]["v"][:, ns, 0:2, :].rearrange("p n y f -> p n (y f)"), in0=tiles[k][("t", q)][:].rearrange("p n y f -> p n (y f)"),
-                scalar=4.0 / 3.0, in1=tiles[k]["beta"][:, ns].rearrange("p n y f -> p n (y f)"), op0=ALU.subtract, op1=ALU.mult,
+                out=tiles[k]["v"][:, 0:8, ns, :].rearrange("p b n i -> p b (n i)"), in0=tiles[k][("t", q)][:].rearrange("p b n i -> p b (n i)"),
+                scalar=4.0 / 3.0, in1=tiles[k]["beta"][:, :, ns, :].rearrange("p b n i -> p b (n i)"), op0=ALU.subtract, op1=ALU.mult,
             )
-
-        def inner_raw(k, q):
-            ns = slice(2 * q, 2 * q + 2)
-            nc.scalar.activation(
-                out=tiles[k]["v"][:, ns, 0:2, :].rearrange("p n y f -> p n (y f)"), in_=tiles[k][("t", q)][:].rearrange("p n y f -> p n (y f)"),
-                func=ACT.Identity, bias=-4.0 / 3.0, scale=1.0,
-            )
-
-        def inner_masked(k, q):
-            ns = slice(2 * q, 2 * q + 2)
-            v = tiles[k]["v"][:, ns, 0:2, :].rearrange("p n y f -> p n (y f)")
-            nc.vector.tensor_tensor(out=v, in0=v, in1=tiles[k]["beta"][:, ns].rearrange("p n y f -> p n (y f)"), op=ALU.mult)
 
         def ring(k, q):
             ns = slice(2 * q, 2 * q + 2)
             nc.scalar.activation(
-                out=tiles[k]["ring"][:, ns].rearrange("p n y f -> p (n y f)"), in_=tiles[k][("c", q)][:].rearrange("p n y f -> p (n y f)"),
-                func=ACT.Copy, bias=0.0, scale=-1.0 / 12.0,
+                out=tiles[k]["ring"][:, :, ns, :].rearrange("p b n i -> p b (n i)"), in_=tiles[k][("c", q)][:].rearrange("p b n i -> p b (n i)"), func=ACT.Copy, bias=0.0, scale=-1.0 / 12.0,
             )
 
         def inner_negated(k, un):
             n0, n1 = unit_tiles(k, un)
             v = tiles[k]["v"]
             nc.vector.tensor_scalar(
-                out=v[:, n0:n1, 2:4, :].rearrange("p n y f -> p n (y f)"), in0=v[:, n0:n1, 0:2, :].rearrange("p n y f -> p n (y f)"),
+                out=v[:, 8:16, n0:n1, :].rearrange("p b n i -> p b (n i)"), in0=v[:, 0:8, n0:n1, :].rearrange("p b n i -> p b (n i)"),
                 scalar1=-1.0, scalar2=None, op0=ALU.mult,
             )
 
         def ring_elsewhere(k, un):
             n0, n1 = unit_tiles(k, un)
-            v4 = tiles[k]["v"][:, n0:n1].rearrange("p n (e y) f -> p n e (y f)", e=2)
-            r4 = tiles[k]["ring"][:, n0:n1].rearrange("p n y f -> p n (y f)").unsqueeze(2).to_broadcast([P, n1 - n0, 2, 2 * P])
+            v4 = tiles[k]["v"][:, :, n0:n1, :].rearrange("p (e b) n i -> p e b (n i)", e=2)
+            r4 = tiles[k]["ring"][:, :, n0:n1, :].rearrange("p b n i -> p b (n i)").unsqueeze(1).to_broadcast([P, 2, 8, 32 * (n1 - n0)])
             nc.vector.tensor_tensor(out=v4, in0=v4, in1=r4, op=ALU.max)
 
         def signed(k, un):
             n0, n1 = unit_tiles(k, un)
-            nc.vector.tensor_tensor(out=tiles[k]["z"][:, n0:n1], in0=tiles[k]["v"][:, n0:n1], in1=tiles[k]["gam"][:, n0:n1], op=ALU.mult)
+            nc.vector.tensor_tensor(
+                out=tiles[k]["z"][:, n0:n1].rearrange("p n b i -> p b n i"), in0=tiles[k]["v"][:, :, n0:n1, :], in1=tiles[k]["gam"][:, :, n0:n1, :], op=ALU.mult,
+            )
 
 
         def fill_z(k, q):
@@ -295,7 +283,7 @@ def tile_bsplinebasis_v2_t_kernel(tc, x, spline_coeffs, residual_weight, residua
             for pos in range(2):
                 for e in range(2):
                     nc.tensor.transpose(
-                        t[:, pos, e, :], words(z[:, 2 * q + pos, 2 * e:2 * e + 2, :].rearrange("p s f -> p (s f)")), ident_f[:],
+                        t[:, pos, e, :], words(z[:, 2 * q + pos, 8 * e:8 * e + 8, :].rearrange("p b i -> p (b i)")), ident_f[:],
                     )
             tiles[k][("zt", q)] = t
 
@@ -322,6 +310,17 @@ def tile_bsplinebasis_v2_t_kernel(tc, x, spline_coeffs, residual_weight, residua
             for i in range(np):
                 tiles[k][("gr", n0 // 2 + i)] = gr[:, i]
 
+        def halves_at_once(k, q):
+            gr = be.tile([P, 2, 8 * P], BF16, tag="gr", align_bytes=64)
+            zt = tiles[k][("zt", q)][:].rearrange("p n e b -> p (n e b)").bitcast(BF16).rearrange("p (n e b d) -> p n b e d", n=2, e=2, d=2)
+            for g in range(2):
+                for pos in range(2):
+                    nc.vector.tensor_scalar(
+                        out=gr[:, g, pos * 4 * P:(pos + 1) * 4 * P].rearrange("p (b e d) -> p b e d", e=2, d=2), in0=zt[:, pos],
+                        scalar1=(-4.0, 4.0)[g], scalar2=0.0, op0=ALU.mult, op1=ALU.max,
+                    )
+            tiles[k][("gr", q)] = gr
+
         def quantise(k, q):
             f = 2 * P
             bcodes = be.tile([P, 2, f], U32, tag="bcodes", bufs=3, align_bytes=64)
@@ -329,7 +328,7 @@ def tile_bsplinebasis_v2_t_kernel(tc, x, spline_coeffs, residual_weight, residua
             nc.vector.quantize_mx(
                 out=bcodes[:].rearrange("p g w -> p (g w)").bitcast(FP8X4),
                 scales=bscales[:].rearrange("p g w -> p (g w)"),
-                in_=tiles[k][("gr", q)].rearrange("p g w -> p (g w)"),
+                in_=tiles[k][("gr", q)][:].rearrange("p g w -> p (g w)"),
             )
             tiles[k][("q", q)] = (bcodes, bscales)
 
@@ -351,9 +350,11 @@ def tile_bsplinebasis_v2_t_kernel(tc, x, spline_coeffs, residual_weight, residua
         def scale_add(k, q, h):
             if h == 0:
                 tiles[k][("t1", q)] = be.tile([P, 2, 2 * P], F32, tag="t1", bufs=3, name="t1")
-            nc.scalar.activation(
-                out=tiles[k][("t1", q)][:, h, :], in_=tiles[k][("mx", q)][:, h, :], func=ACT.Identity, bias=bias[:, h:h + 1], scale=scale[:, h:h + 1],
-            )
+            dst, src = tiles[k][("t1", q)][:, h, :], tiles[k][("mx", q)][:, h, :]
+            if k == NG - 1 and h == 1:
+                nc.vector.tensor_scalar(out=dst, in0=src, scalar1=scale[:, h:h + 1], scalar2=bias[:, h:h + 1], op0=ALU.mult, op1=ALU.add)
+            else:
+                nc.scalar.activation(out=dst, in_=src, func=ACT.Identity, bias=bias[:, h:h + 1], scale=scale[:, h:h + 1])
 
         def add_residual(k, q, pos):
             t1 = tiles[k][("t1", q)]
@@ -367,7 +368,11 @@ def tile_bsplinebasis_v2_t_kernel(tc, x, spline_coeffs, residual_weight, residua
 
         def store(k, q):
             osb = be.tile([P, 2, O], F32, tag="osb", bufs=4)
-            nc.scalar.copy(out=osb[:], in_=tiles[k][("ot", q)][:])
+            if k == NG - 1:
+                nc.scalar.copy(out=osb[:, 0, :], in_=tiles[k][("ot", q)][:, 0, :])
+                nc.vector.tensor_copy(out=osb[:, 1, :], in_=tiles[k][("ot", q)][:, 1, :])
+            else:
+                nc.scalar.copy(out=osb[:], in_=tiles[k][("ot", q)][:])
             n0 = GSTART[k] + 2 * q
             nc.sync.dma_start(out=out_v[:, n0:n0 + 2, :], in_=osb[:])
 
@@ -398,36 +403,44 @@ def tile_bsplinebasis_v2_t_kernel(tc, x, spline_coeffs, residual_weight, residua
             if exists(k) and un < len(GROUPS[k]) and 2 * i < GROUPS[k][un]:
                 step(k, sum(GROUPS[k][:un]) // 2 + i)
 
+        def copy_out(k, q):
+            if k < NG - 1:
+                copy_z(k, q)
+
+        def halves_later(k, un):
+            if k < NG - 1:
+                halves(k, un)
+            else:
+                for q in range(sum(GROUPS[k][:un]) // 2, sum(GROUPS[k][:un + 1]) // 2):
+                    halves_at_once(k, q)
+
         for k in range(-3, NG + 3):
-            if k == -3:
-                permute(0)
-                permute(1)
             pair(k, 0, inner)
             pair(k, 1, fill_inner)
             pair(k, 0, ring)
             pair(k, 1, fill_ring)
-            unit(k - 1, 0, halves)
-            half(k - 2, 3, 0, add_residual)
+            unit(k - 1, 0, halves_later)
             part(k + 1, 0, mask)
             part(k + 1, 1, mask)
             part(k + 1, 1, square)
-            unit_pair(k - 1, 1, 0, copy_z)
+            unit_pair(k - 1, 1, 0, copy_out)
             if k == 1:
                 weights_finish()
             pair(k - 1, 0, quantise)
             half(k - 1, 0, 0, multiply)
+            half(k - 1, 0, 1, multiply)
             pair(k, 1, inner)
             pair(k, 2, fill_inner)
             pair(k, 1, ring)
             pair(k, 2, fill_ring)
-            unit_pair(k - 1, 1, 1, copy_z)
-            half(k - 1, 0, 1, multiply)
+            unit_pair(k - 1, 1, 1, copy_out)
+            half(k - 2, 3, 0, add_residual)
             half(k - 2, 3, 1, add_residual)
             part(k + 1, 2, mask)
             part(k + 1, 3, mask)
-            half(k - 1, 0, 0, scale_add)
             part(k + 1, 0, square)
             part(k + 1, 1, cube)
+            half(k - 1, 0, 0, scale_add)
             half(k - 1, 0, 1, scale_add)
             pair(k, 2, inner)
             pair(k, 3, fill_inner)
@@ -436,50 +449,50 @@ def tile_bsplinebasis_v2_t_kernel(tc, x, spline_coeffs, residual_weight, residua
             pair(k - 2, 3, store)
             unit(k, 0, inner_negated)
             if exists(k - 1) and tiles_of(k - 1) == 4:
-                halves(k - 1, 1)
+                halves_later(k - 1, 1)
             pair(k - 1, 1, quantise)
             half(k - 1, 1, 0, multiply)
-            half(k - 1, 0, 0, add_residual)
-            if exists(k - 1) and tiles_of(k - 1) == 8:
-                halves(k - 1, 1)
-            pair(k, 3, ring)
             half(k - 1, 1, 1, multiply)
+            if exists(k - 1) and tiles_of(k - 1) == 8:
+                halves_later(k - 1, 1)
+            pair(k, 3, ring)
+            half(k - 1, 0, 0, add_residual)
             half(k - 1, 0, 1, add_residual)
             pair(k, 3, inner)
-            half(k - 1, 1, 0, scale_add)
             whole(k + 2, fold_1)
+            half(k - 1, 1, 0, scale_add)
             half(k - 1, 1, 1, scale_add)
             pair(k - 1, 0, store)
             unit(k, 0, ring_elsewhere)
             pair(k - 1, 2, quantise)
             half(k - 1, 2, 0, multiply)
-            half(k - 1, 1, 0, add_residual)
+            half(k - 1, 2, 1, multiply)
             whole(k + 2, fold_2)
             whole(k + 3, transpose_x)
             unit(k, 1, inner_negated)
             unit(k, 0, signed)
-            half(k - 1, 2, 0, scale_add)
             whole(k + 3, keep_xT)
-            half(k - 1, 2, 1, multiply)
+            half(k - 1, 1, 0, add_residual)
             half(k - 1, 1, 1, add_residual)
             unit_pair(k, 0, 0, fill_z)
             unit_pair(k, 0, 1, fill_z)
             part(k + 1, 0, cube)
             pair(k + 1, 0, fill_inner)
             pair(k + 1, 0, fill_ring)
-            unit_pair(k, 0, 0, copy_z)
+            unit_pair(k, 0, 0, copy_out)
+            half(k - 1, 2, 0, scale_add)
             half(k - 1, 2, 1, scale_add)
             whole(k + 2, fold_3)
             pair(k - 1, 1, store)
             unit(k, 1, ring_elsewhere)
             pair(k - 1, 3, quantise)
             half(k - 1, 3, 0, multiply)
-            half(k - 1, 2, 0, add_residual)
-            unit_pair(k, 0, 1, copy_z)
-            whole(k + 1, near_masks)
-            half(k - 1, 3, 0, scale_add)
             half(k - 1, 3, 1, multiply)
+            unit_pair(k, 0, 1, copy_out)
+            whole(k + 1, near_masks)
+            half(k - 1, 2, 0, add_residual)
             half(k - 1, 2, 1, add_residual)
+            half(k - 1, 3, 0, scale_add)
             half(k - 1, 3, 1, scale_add)
             whole(k + 3, clamp)
             unit(k, 1, signed)
@@ -487,14 +500,8 @@ def tile_bsplinebasis_v2_t_kernel(tc, x, spline_coeffs, residual_weight, residua
             unit_pair(k, 1, 1, fill_z)
             pair(k - 1, 2, store)
             if k == -3:
-                permute(2)
                 weights_permute()
-            if k == -2:
-                permute(3)
-                permute(4)
             if k == -1:
                 weights_transpose()
-                for later in range(5, NG):
-                    permute(later)
             if k == 0:
                 weights_leave_psum()

@@ -403,6 +403,10 @@ def tile_bsplinebasis_v2_t_kernel(tc, x, spline_coeffs, residual_weight, residua
             if exists(k) and un < len(GROUPS[k]) and 2 * i < GROUPS[k][un]:
                 step(k, sum(GROUPS[k][:un]) // 2 + i)
 
+        def later_mask(k, i):
+            if k > 1:
+                part(k, i, mask)
+
         def copy_out(k, q):
             if k < NG - 1:
                 copy_z(k, q)
@@ -414,91 +418,85 @@ def tile_bsplinebasis_v2_t_kernel(tc, x, spline_coeffs, residual_weight, residua
                 for q in range(sum(GROUPS[k][:un]) // 2, sum(GROUPS[k][:un + 1]) // 2):
                     halves_at_once(k, q)
 
+        def both(k, q, step):
+            half(k, q, 0, step)
+            half(k, q, 1, step)
+
+        for g in range(2):
+            for i in range(4):
+                mask(g, i)
+        near_masks(0)
         for k in range(-3, NG + 3):
             pair(k, 0, inner)
-            pair(k, 1, fill_inner)
             pair(k, 0, ring)
+            pair(k, 1, fill_inner)
             pair(k, 1, fill_ring)
-            unit(k - 1, 0, halves_later)
-            part(k + 1, 0, mask)
-            part(k + 1, 1, mask)
             part(k + 1, 1, square)
+            unit(k - 1, 0, halves_later)
+            later_mask(k + 1, 0)
+            later_mask(k + 1, 1)
             unit_pair(k - 1, 1, 0, copy_out)
+            unit_pair(k - 1, 1, 1, copy_out)
             if k == 1:
                 weights_finish()
             pair(k - 1, 0, quantise)
-            half(k - 1, 0, 0, multiply)
-            half(k - 1, 0, 1, multiply)
+            both(k - 2, 3, add_residual)
+            both(k - 1, 0, multiply)
             pair(k, 1, inner)
-            pair(k, 2, fill_inner)
             pair(k, 1, ring)
+            pair(k, 2, fill_inner)
             pair(k, 2, fill_ring)
-            unit_pair(k - 1, 1, 1, copy_out)
-            half(k - 2, 3, 0, add_residual)
-            half(k - 2, 3, 1, add_residual)
-            part(k + 1, 2, mask)
-            part(k + 1, 3, mask)
+            later_mask(k + 1, 2)
+            later_mask(k + 1, 3)
+            both(k - 1, 0, scale_add)
             part(k + 1, 0, square)
-            part(k + 1, 1, cube)
-            half(k - 1, 0, 0, scale_add)
-            half(k - 1, 0, 1, scale_add)
-            pair(k, 2, inner)
-            pair(k, 3, fill_inner)
-            pair(k, 2, ring)
-            pair(k, 3, fill_ring)
-            pair(k - 2, 3, store)
             unit(k, 0, inner_negated)
-            if exists(k - 1) and tiles_of(k - 1) == 4:
-                halves_later(k - 1, 1)
-            pair(k - 1, 1, quantise)
-            half(k - 1, 1, 0, multiply)
-            half(k - 1, 1, 1, multiply)
-            if exists(k - 1) and tiles_of(k - 1) == 8:
-                halves_later(k - 1, 1)
-            pair(k, 3, ring)
-            half(k - 1, 0, 0, add_residual)
-            half(k - 1, 0, 1, add_residual)
-            pair(k, 3, inner)
+            part(k + 1, 1, cube)
+            unit(k - 1, 1, halves_later)
+            pair(k, 2, inner)
+            pair(k, 2, ring)
+            pair(k, 3, fill_inner)
+            pair(k, 3, fill_ring)
             whole(k + 2, fold_1)
-            half(k - 1, 1, 0, scale_add)
-            half(k - 1, 1, 1, scale_add)
-            pair(k - 1, 0, store)
-            unit(k, 0, ring_elsewhere)
+            pair(k - 1, 1, quantise)
+            both(k - 1, 1, multiply)
             pair(k - 1, 2, quantise)
-            half(k - 1, 2, 0, multiply)
-            half(k - 1, 2, 1, multiply)
-            whole(k + 2, fold_2)
+            pair(k - 2, 3, store)
+            unit(k, 0, ring_elsewhere)
             whole(k + 3, transpose_x)
-            unit(k, 1, inner_negated)
-            unit(k, 0, signed)
+            both(k - 1, 2, multiply)
+            pair(k, 3, inner)
+            pair(k, 3, ring)
+            both(k - 1, 1, scale_add)
+            both(k - 1, 0, add_residual)
             whole(k + 3, keep_xT)
-            half(k - 1, 1, 0, add_residual)
-            half(k - 1, 1, 1, add_residual)
+            unit(k, 0, signed)
+            whole(k + 2, fold_2)
+            pair(k - 1, 0, store)
+            both(k - 1, 2, scale_add)
             unit_pair(k, 0, 0, fill_z)
-            unit_pair(k, 0, 1, fill_z)
+            both(k - 1, 1, add_residual)
+            unit(k, 1, inner_negated)
             part(k + 1, 0, cube)
+            unit_pair(k, 0, 0, copy_out)
             pair(k + 1, 0, fill_inner)
             pair(k + 1, 0, fill_ring)
-            unit_pair(k, 0, 0, copy_out)
-            half(k - 1, 2, 0, scale_add)
-            half(k - 1, 2, 1, scale_add)
-            whole(k + 2, fold_3)
+            unit_pair(k, 0, 1, fill_z)
             pair(k - 1, 1, store)
             unit(k, 1, ring_elsewhere)
             pair(k - 1, 3, quantise)
-            half(k - 1, 3, 0, multiply)
-            half(k - 1, 3, 1, multiply)
+            both(k - 1, 3, multiply)
             unit_pair(k, 0, 1, copy_out)
-            whole(k + 1, near_masks)
-            half(k - 1, 2, 0, add_residual)
-            half(k - 1, 2, 1, add_residual)
-            half(k - 1, 3, 0, scale_add)
-            half(k - 1, 3, 1, scale_add)
-            whole(k + 3, clamp)
+            whole(k + 2, fold_3)
+            if k + 1 > 0:
+                whole(k + 1, near_masks)
+            both(k - 1, 3, scale_add)
+            both(k - 1, 2, add_residual)
             unit(k, 1, signed)
+            pair(k - 1, 2, store)
             unit_pair(k, 1, 0, fill_z)
             unit_pair(k, 1, 1, fill_z)
-            pair(k - 1, 2, store)
+            whole(k + 3, clamp)
             if k == -3:
                 weights_permute()
             if k == -1:

@@ -20,6 +20,7 @@ NG = len(GROUPS)
 GSTART = [sum(sum(grp) for grp in GROUPS[:k]) for k in range(NG)]
 J_OF_SLOT = (3, 0, 1, 2)
 SLOT_OF_J = (1, 2, 3, 0)
+KEEP_ON_VECTOR = -1
 FLOPS = 2 * B * I * NBAS * O + 2 * B * I * O
 assert sum(sum(grp) for grp in GROUPS) == NT
 
@@ -118,7 +119,7 @@ def tile_bsplinebasis_v2_t_kernel(tc, x, spline_coeffs, residual_weight, residua
             nc.scalar.copy(out=rwT[:].rearrange("p (h o) -> p h o", h=2), in_=wt["tpr"][:, 0:2, :])
             nc.scalar.copy(out=bias[:], in_=wt["tpr"][:, 2, 0:2])
             for h in range(2):
-                nc.scalar.copy(
+                nc.vector.tensor_copy(
                     out=words(cgr[:, :, h * 4 * P:(h + 1) * 4 * P]).rearrange("p g (o e) -> p g o e", e=2),
                     in_=wt[h][:].rearrange("p g e o -> p g o e"),
                 )
@@ -155,7 +156,10 @@ def tile_bsplinebasis_v2_t_kernel(tc, x, spline_coeffs, residual_weight, residua
 
         def keep_xT(k):
             nt, n0 = tiles_of(k), GSTART[k]
-            nc.scalar.copy(out=xT[:, n0:n0 + nt, :], in_=tiles[k]["tpx"][:])
+            if k <= KEEP_ON_VECTOR:
+                nc.vector.tensor_copy(out=xT[:, n0:n0 + nt, :], in_=tiles[k]["tpx"][:])
+            else:
+                nc.scalar.copy(out=xT[:, n0:n0 + nt, :], in_=tiles[k]["tpx"][:])
 
         def clamp(k):
             nt, n0 = tiles_of(k), GSTART[k]
@@ -220,7 +224,7 @@ def tile_bsplinebasis_v2_t_kernel(tc, x, spline_coeffs, residual_weight, residua
         def mask(k, i):
             nt, n0 = tiles_of(k), GSTART[k]
             if i == 0:
-                tiles[k]["gam"] = ew.tile([P, 16, nt, 32], BF16, tag="gam", name="gam")
+                tiles[k]["gam"] = ew.tile([P, 16, nt, 32], BF16, tag="gam", bufs=3, name="gam")
             s = (SLOT_OF_J[0], SLOT_OF_J[2], SLOT_OF_J[1], SLOT_OF_J[3])[i]
             nc.vector.tensor_scalar(
                 out=tiles[k]["gam"][:, 4 * s:4 * s + 4].rearrange("p a n (q l) -> p a (n q) l", l=4),
@@ -231,7 +235,7 @@ def tile_bsplinebasis_v2_t_kernel(tc, x, spline_coeffs, residual_weight, residua
         def near_masks(k):
             nt = tiles_of(k)
             gam = tiles[k]["gam"]
-            beta = ew.tile([P, 8, nt, 32], BF16, tag="beta", bufs=1)
+            beta = ew.tile([P, 8, nt, 32], BF16, tag="beta")
             for y in range(2):
                 s0, s1 = SLOT_OF_J[y], SLOT_OF_J[y + 2]
                 nc.vector.tensor_tensor(
@@ -249,6 +253,17 @@ def tile_bsplinebasis_v2_t_kernel(tc, x, spline_coeffs, residual_weight, residua
                 out=tiles[k]["v"][:, 0:8, ns, :].rearrange("p b n i -> p b (n i)"), in0=tiles[k][("t", q)][:].rearrange("p b n i -> p b (n i)"),
                 scalar=4.0 / 3.0, in1=tiles[k]["beta"][:, :, ns, :].rearrange("p b n i -> p b (n i)"), op0=ALU.subtract, op1=ALU.mult,
             )
+
+        def inner_raw(k, q):
+            ns = slice(2 * q, 2 * q + 2)
+            nc.scalar.activation(
+                out=tiles[k]["v"][:, 0:8, ns, :].rearrange("p b n i -> p b (n i)"), in_=tiles[k][("t", q)][:].rearrange("p b n i -> p b (n i)"), func=ACT.Identity, bias=-4.0 / 3.0, scale=1.0,
+            )
+
+        def inner_masked(k, un):
+            n0, n1 = unit_tiles(k, un)
+            v = tiles[k]["v"][:, 0:8, n0:n1, :].rearrange("p b n i -> p b (n i)")
+            nc.vector.tensor_tensor(out=v, in0=v, in1=tiles[k]["beta"][:, :, n0:n1, :].rearrange("p b n i -> p b (n i)"), op=ALU.mult)
 
         def ring(k, q):
             ns = slice(2 * q, 2 * q + 2)
@@ -404,7 +419,7 @@ def tile_bsplinebasis_v2_t_kernel(tc, x, spline_coeffs, residual_weight, residua
                 step(k, sum(GROUPS[k][:un]) // 2 + i)
 
         def later_mask(k, i):
-            if k > 1:
+            if k > 2:
                 part(k, i, mask)
 
         def copy_out(k, q):
@@ -440,32 +455,34 @@ def tile_bsplinebasis_v2_t_kernel(tc, x, spline_coeffs, residual_weight, residua
             if k == 1:
                 weights_finish()
             pair(k - 1, 0, quantise)
-            both(k - 2, 3, add_residual)
             both(k - 1, 0, multiply)
             pair(k, 1, inner)
             pair(k, 1, ring)
             pair(k, 2, fill_inner)
             pair(k, 2, fill_ring)
+            both(k - 2, 3, add_residual)
             later_mask(k + 1, 2)
             later_mask(k + 1, 3)
-            both(k - 1, 0, scale_add)
             part(k + 1, 0, square)
+            both(k - 1, 0, scale_add)
             unit(k, 0, inner_negated)
+            if k == 0:
+                near_masks(1)
             part(k + 1, 1, cube)
             unit(k - 1, 1, halves_later)
-            pair(k, 2, inner)
+            pair(k, 2, inner_raw)
             pair(k, 2, ring)
             pair(k, 3, fill_inner)
             pair(k, 3, fill_ring)
             whole(k + 2, fold_1)
             pair(k - 1, 1, quantise)
             both(k - 1, 1, multiply)
+            unit(k, 0, ring_elsewhere)
             pair(k - 1, 2, quantise)
             pair(k - 2, 3, store)
-            unit(k, 0, ring_elsewhere)
             whole(k + 3, transpose_x)
             both(k - 1, 2, multiply)
-            pair(k, 3, inner)
+            pair(k, 3, inner_raw)
             pair(k, 3, ring)
             both(k - 1, 1, scale_add)
             both(k - 1, 0, add_residual)
@@ -476,19 +493,21 @@ def tile_bsplinebasis_v2_t_kernel(tc, x, spline_coeffs, residual_weight, residua
             both(k - 1, 2, scale_add)
             unit_pair(k, 0, 0, fill_z)
             both(k - 1, 1, add_residual)
-            unit(k, 1, inner_negated)
+            if exists(k) and tiles_of(k) == 8:
+                inner_masked(k, 1)
             part(k + 1, 0, cube)
+            unit(k, 1, inner_negated)
             unit_pair(k, 0, 0, copy_out)
             pair(k + 1, 0, fill_inner)
             pair(k + 1, 0, fill_ring)
             unit_pair(k, 0, 1, fill_z)
             pair(k - 1, 1, store)
-            unit(k, 1, ring_elsewhere)
             pair(k - 1, 3, quantise)
+            unit(k, 1, ring_elsewhere)
             both(k - 1, 3, multiply)
             unit_pair(k, 0, 1, copy_out)
             whole(k + 2, fold_3)
-            if k + 1 > 0:
+            if k + 1 > 1:
                 whole(k + 1, near_masks)
             both(k - 1, 3, scale_add)
             both(k - 1, 2, add_residual)
@@ -496,6 +515,9 @@ def tile_bsplinebasis_v2_t_kernel(tc, x, spline_coeffs, residual_weight, residua
             pair(k - 1, 2, store)
             unit_pair(k, 1, 0, fill_z)
             unit_pair(k, 1, 1, fill_z)
+            if k == -1:
+                for i in range(4):
+                    mask(2, i)
             whole(k + 3, clamp)
             if k == -3:
                 weights_permute()

@@ -440,7 +440,6 @@ def tile_bsplinebasis_v2_t_kernel(tc, x, spline_coeffs, residual_weight, residua
         for g in range(2):
             for i in range(4):
                 mask(g, i)
-        near_masks(0)
         for k in range(-3, NG + 3):
             pair(k, 0, inner)
             pair(k, 0, ring)
@@ -454,7 +453,11 @@ def tile_bsplinebasis_v2_t_kernel(tc, x, spline_coeffs, residual_weight, residua
             unit_pair(k - 1, 1, 1, copy_out)
             if k == 1:
                 weights_finish()
+            if k == NG - 1:
+                inner_negated(k, 0)
             pair(k - 1, 0, quantise)
+            if k == NG - 1:
+                ring_elsewhere(k, 0)
             both(k - 1, 0, multiply)
             pair(k, 1, inner)
             pair(k, 1, ring)
@@ -465,7 +468,8 @@ def tile_bsplinebasis_v2_t_kernel(tc, x, spline_coeffs, residual_weight, residua
             later_mask(k + 1, 3)
             part(k + 1, 0, square)
             both(k - 1, 0, scale_add)
-            unit(k, 0, inner_negated)
+            if k != NG - 1:
+                unit(k, 0, inner_negated)
             if k == 0:
                 near_masks(1)
             part(k + 1, 1, cube)
@@ -475,9 +479,13 @@ def tile_bsplinebasis_v2_t_kernel(tc, x, spline_coeffs, residual_weight, residua
             pair(k, 3, fill_inner)
             pair(k, 3, fill_ring)
             whole(k + 2, fold_1)
+            if k == NG - 1:
+                signed(k, 0)
+                fill_z(k, 0)
             pair(k - 1, 1, quantise)
             both(k - 1, 1, multiply)
-            unit(k, 0, ring_elsewhere)
+            if k != NG - 1:
+                unit(k, 0, ring_elsewhere)
             pair(k - 1, 2, quantise)
             pair(k - 2, 3, store)
             whole(k + 3, transpose_x)
@@ -487,20 +495,22 @@ def tile_bsplinebasis_v2_t_kernel(tc, x, spline_coeffs, residual_weight, residua
             both(k - 1, 1, scale_add)
             both(k - 1, 0, add_residual)
             whole(k + 3, keep_xT)
-            unit(k, 0, signed)
+            if k != NG - 1:
+                unit(k, 0, signed)
             whole(k + 2, fold_2)
             pair(k - 1, 0, store)
             both(k - 1, 2, scale_add)
-            unit_pair(k, 0, 0, fill_z)
+            if k != NG - 1:
+                unit_pair(k, 0, 0, fill_z)
             both(k - 1, 1, add_residual)
             if exists(k) and tiles_of(k) == 8:
                 inner_masked(k, 1)
             part(k + 1, 0, cube)
             unit(k, 1, inner_negated)
             unit_pair(k, 0, 0, copy_out)
+            unit_pair(k, 0, 1, fill_z)
             pair(k + 1, 0, fill_inner)
             pair(k + 1, 0, fill_ring)
-            unit_pair(k, 0, 1, fill_z)
             pair(k - 1, 1, store)
             pair(k - 1, 3, quantise)
             unit(k, 1, ring_elsewhere)
@@ -519,6 +529,8 @@ def tile_bsplinebasis_v2_t_kernel(tc, x, spline_coeffs, residual_weight, residua
                 for i in range(4):
                     mask(2, i)
             whole(k + 3, clamp)
+            if k == -3:
+                near_masks(0)
             if k == -3:
                 weights_permute()
             if k == -1:

@@ -58,10 +58,6 @@ def tile_bsplinebasis_v2_t_kernel(tc, x, spline_coeffs, residual_weight, residua
         make_identity(nc, ident_f[:])
 
         ident_p = const.tile([P, P], F32)
-        nc.gpsimd.tensor_copy(
-            out=ident_p[:].rearrange("p (a q l) -> p a q l", a=4, q=8), in_=ident_f[:].rearrange("p (q a l) -> p a q l", q=8, a=4),
-        )
-
         perm = ident_p[:].rearrange("p (a i) -> p a i", a=4)
 
         c_sb = setup.tile([P, 2, I * NBAS], BF16)
@@ -532,6 +528,9 @@ def tile_bsplinebasis_v2_t_kernel(tc, x, spline_coeffs, residual_weight, residua
             if k == -3:
                 near_masks(0)
             if k == -3:
+                nc.vector.tensor_copy(
+                    out=ident_p[:].rearrange("p (a q l) -> p a q l", a=4, q=8), in_=ident_f[:].rearrange("p (q a l) -> p a q l", q=8, a=4),
+                )
                 weights_permute()
             if k == -1:
                 weights_transpose()

import math
from contextlib import ExitStack

import concourse.mybir as mybir
from concourse.masks import make_identity

F32 = mybir.dt.float32
BF16 = mybir.dt.bfloat16
U32 = mybir.dt.uint32
U8 = mybir.dt.uint8
FP8X4 = mybir.dt.float8_e4m3fn_x4
ALU = mybir.AluOpType
ACT = mybir.ActivationFunctionType

P = 128
B, I, O, NBAS = 8192, 128, 256, 8
NT = B // P
GROUPS = [[2], [2, 2]] + [[4, 4]] * 7 + [[2]]
NG = len(GROUPS)
GSTART = [sum(sum(grp) for grp in GROUPS[:k]) for k in range(NG)]
J_OF_SLOT = (3, 0, 1, 2)
SLOT_OF_J = (1, 2, 3, 0)
KEEP_ON_VECTOR = -1
FLOPS = 2 * B * I * NBAS * O + 2 * B * I * O
assert sum(sum(grp) for grp in GROUPS) == NT


def tile_bsplinebasis_v2_t_kernel(tc, x, spline_coeffs, residual_weight, residual_bias, scale_base, out):
    nc = tc.nc
    root2 = math.sqrt(2.0)
    with ExitStack() as ctx:
        const = ctx.enter_context(tc.tile_pool(name="const", bufs=1))
        setup = ctx.enter_context(tc.tile_pool(name="setup", bufs=1))
        ew = ctx.enter_context(tc.tile_pool(name="ew", bufs=2))
        be = ctx.enter_context(tc.tile_pool(name="be", bufs=2))
        psum = ctx.enter_context(tc.psum_pool(name="psum", bufs=1))
        ctx.enter_context(tc.manual_schedule())

        x_sb = const.tile([P, NT, I], BF16)
        xT = const.tile([P, NT, P], BF16)
        x_v = x.rearrange("(p n) i -> p n i", n=NT)
        out_v = out.rearrange("(p n) o -> p n o", n=NT)
        warm = const.tile([P, 1], F32)
        nc.vector.memset(warm[:], 0.0)
        nc.scalar.activation(out=warm[:], in_=warm[:], func=ACT.Abs, bias=0.0, scale=1.0)

        def load_x(k):
            n0 = GSTART[k]
            n1 = n0 + sum(GROUPS[k])
            nc.sync.dma_start(out=x_sb[:, n0:n1, :], in_=x_v[:, n0:n1, :])

        load_x(0)
        load_x(1)

        ident_b = const.tile([P, P], BF16)
        make_identity(nc, ident_b[:])
        ident_f = const.tile([P, P], F32)
        make_identity(nc, ident_f[:])

        ident_p = const.tile([P, P], F32)
        perm = ident_p[:].rearrange("p (a i) -> p a i", a=4)

        c_sb = setup.tile([P, 2, I * NBAS], BF16)
        nc.sync.dma_start(out=c_sb[:], in_=spline_coeffs.rearrange("(h p) i j -> p h (i j)", p=P))
        rw_sb = setup.tile([P, 2, I], BF16)
        nc.sync.dma_start(out=rw_sb[:], in_=residual_weight.rearrange("(h p) i -> p h i", p=P))
        sb_sb = setup.tile([P, 2, I], BF16)
        nc.sync.dma_start(out=sb_sb[:], in_=scale_base.rearrange("(h p) i -> p h i", p=P))
        b_sb = setup.tile([P, P], BF16)
        nc.vector.memset(b_sb[:], 0.0)
        nc.sync.dma_start(out=b_sb[0:2, :], in_=residual_bias.rearrange("(h p) -> h p", p=P))
        for k in range(2, NG):
            load_x(k)

        cpm = setup.tile([P, 2, I, NBAS], BF16)
        cz = setup.tile([P, 2, 2, 4, I], BF16)
        cgr = setup.tile([P, 2, 4 * O], BF16, align_bytes=64)
        ccodes = const.tile([P, 2, O], U32, align_bytes=64)
        cscales = const.tile([P, 2, O], U8, align_bytes=64)
        rwT = const.tile([P, 2 * P], BF16)
        bias = const.tile([P, 2], F32)
        scale = const.tile([P, 2], F32)
        wt = dict()

        def words(ap):
            return ap.bitcast(F32)

        def weights_permute():
            nc.vector.tensor_copy(
                out=cpm[:].rearrange("p h (a q l) j -> p h a q (l j)", a=4, q=8, l=4),
                in_=c_sb[:].rearrange("p h (q a z) -> p h a q z", q=8, a=4, z=4 * NBAS),
            )
            for s in range(4):
                nc.vector.tensor_copy(
                    out=cz[:, :, :, s, :],
                    in_=cpm[:].rearrange("p h r (g j) -> p h g j r", g=2)[:, :, :, J_OF_SLOT[s], :],
                )

        def weights_transpose():
            tpr = psum.tile([P, 3, P], BF16, tag="ot", bufs=2)
            for h in range(2):
                nc.tensor.transpose(tpr[:, h, :], rw_sb[:, h, :], ident_b[:])
            nc.tensor.transpose(tpr[:, 2, :], b_sb[:], ident_b[:])
            wt["tpr"] = tpr
            for h in range(2):
                tpc = psum.tile([P, 2, 2, P], F32, tag="mx", bufs=2)
                for g in range(2):
                    for e in range(2):
                        nc.tensor.transpose(
                            tpc[:, g, e, :], words(cz[:, h, g, 2 * e:2 * e + 2, :].rearrange("p s r -> p (s r)")), ident_f[:],
                        )
                wt[h] = tpc

        def weights_leave_psum():
            nc.scalar.copy(out=rwT[:].rearrange("p (h o) -> p h o", h=2), in_=wt["tpr"][:, 0:2, :])
            nc.scalar.copy(out=bias[:], in_=wt["tpr"][:, 2, 0:2])
            for h in range(2):
                nc.vector.tensor_copy(
                    out=words(cgr[:, :, h * 4 * P:(h + 1) * 4 * P]).rearrange("p g (o e) -> p g o e", e=2),
                    in_=wt[h][:].rearrange("p g e o -> p g o e"),
                )

        def weights_finish():
            ssum = setup.tile([P, 2], F32)
            nc.vector.tensor_reduce(out=ssum[:], in_=sb_sb[:], axis=mybir.AxisListType.X, op=ALU.add)
            nc.vector.quantize_mx(
                out=ccodes[:].rearrange("p g o -> p (g o)").bitcast(FP8X4),
                scales=cscales[:].rearrange("p g o -> p (g o)"),
                in_=cgr[:].rearrange("p g w -> p (g w)"),
            )
            nc.vector.tensor_scalar(out=scale[:], in0=ssum[:], scalar1=1.0 / I, scalar2=None, op0=ALU.mult)

        tiles = [dict() for k in range(NG)]

        def exists(k):
            return 0 <= k < NG

        def tiles_of(k):
            return sum(GROUPS[k])

        def unit_tiles(k, un):
            first = sum(GROUPS[k][:un])
            return first, first + GROUPS[k][un]


        def transpose_x(k):
            nt, n0 = tiles_of(k), GSTART[k]
            tpx = psum.tile([P, nt, P], BF16, tag="z", bufs=2)
            for n in range(nt):
                nc.tensor.transpose(tpx[:, n, :], x_sb[:, n0 + n, :], ident_b[:])
            tiles[k]["tpx"] = tpx

        def keep_xT(k):
            nt, n0 = tiles_of(k), GSTART[k]
            if k <= KEEP_ON_VECTOR:
                nc.vector.tensor_copy(out=xT[:, n0:n0 + nt, :], in_=tiles[k]["tpx"][:])
            else:
                nc.scalar.copy(out=xT[:, n0:n0 + nt, :], in_=tiles[k]["tpx"][:])

        def clamp(k):
            nt, n0 = tiles_of(k), GSTART[k]
            u = ew.tile([P, nt * P], BF16, tag="u", name="u")
            nc.vector.tensor_scalar(
                out=u[:], in0=xT[:, n0:n0 + nt, :].rearrange("p n w -> p (n w)"), scalar1=-1.0, scalar2=1.0, op0=ALU.max, op1=ALU.min,
            )
            tiles[k]["u"] = u

        def fold_1(k):
            nt = tiles_of(k)
            dh = ew.tile([P, nt * P], F32, tag="dh")
            nc.scalar.activation(out=dh[:], in_=tiles[k]["u"][:], func=ACT.Abs, bias=0.5, scale=2.5)
            tiles[k]["dh"] = dh

        def fold_2(k):
            dh = tiles[k]["dh"]
            nc.scalar.activation(out=dh[:], in_=dh[:], func=ACT.Abs, bias=-2.0, scale=1.0)

        def fold_3(k):
            dh = tiles[k]["dh"]
            nc.scalar.activation(out=dh[:], in_=dh[:], func=ACT.Abs, bias=-0.5, scale=0.5)

        def square(k, y):
            nt = tiles_of(k)
            if "sq" not in tiles[k]:
                tiles[k]["sq"] = ew.tile([P, 2, nt * P], F32, tag="sq", name="sq")
                tiles[k]["cub"] = ew.tile([P, 2, nt * P], F32, tag="cub", name="cub")
            nc.scalar.activation(
                out=tiles[k]["sq"][:, y, :], in_=tiles[k]["dh"][:], func=ACT.Square,
                bias=(root2, 0.0)[y], scale=(-2.0 * root2, 2.0 * root2)[y],
            )

        def cube(k, y):
            dh, sq, cub = tiles[k]["dh"], tiles[k]["sq"], tiles[k]["cub"]
            nc.vector.scalar_tensor_tensor(
                out=cub[:, y, :], in0=(dh[:], sq[:, 1, :])[y], scalar=(0.5, -1.0)[y], in1=(sq[:, 0, :], dh[:])[y],
                op0=(ALU.subtract, ALU.mult)[y], op1=ALU.mult,
            )

        def fill_inner(k, q):
            sq, cub = tiles[k]["sq"], tiles[k]["cub"]
            t = psum.tile([P, 8, 2, 32], F32, tag="t", bufs=1)
            for pos in range(2):
                cols = slice((2 * q + pos) * P, (2 * q + pos + 1) * P)
                for y in range(2):
                    dst = t[:, 4 * y:4 * y + 4, pos, :]
                    nc.tensor.matmul(out=dst, lhsT=sq[:, y, cols], rhs=perm, is_transpose=True, start=True, stop=False)
                    nc.tensor.matmul(out=dst, lhsT=cub[:, y, cols], rhs=perm, is_transpose=True, start=False, stop=True)
            tiles[k][("t", q)] = t

        def fill_ring(k, q):
            cub = tiles[k]["cub"]
            t = psum.tile([P, 8, 2, 32], F32, tag="c")
            for pos in range(2):
                cols = slice((2 * q + pos) * P, (2 * q + pos + 1) * P)
                for y in range(2):
                    nc.tensor.matmul(out=t[:, 4 * y:4 * y + 4, pos, :], lhsT=cub[:, y, cols], rhs=perm, is_transpose=True, start=True, stop=True)
            tiles[k][("c", q)] = t


        def mask(k, i):
            nt, n0 = tiles_of(k), GSTART[k]
            if i == 0:
                tiles[k]["gam"] = ew.tile([P, 16, nt, 32], BF16, tag="gam", bufs=3, name="gam")
            s = (SLOT_OF_J[0], SLOT_OF_J[2], SLOT_OF_J[1], SLOT_OF_J[3])[i]
            nc.vector.tensor_scalar(
                out=tiles[k]["gam"][:, 4 * s:4 * s + 4].rearrange("p a n (q l) -> p a (n q) l", l=4),
                in0=x_sb[:, n0:n0 + nt, :].rearrange("p n (q a l) -> p a (n q) l", a=4, l=4),
                scalar1=0.4 * (J_OF_SLOT[s] + 1) - 1.0, scalar2=0.5, op0=ALU.is_gt, op1=ALU.subtract,
            )

        def near_masks(k):
            nt = tiles_of(k)
            gam = tiles[k]["gam"]
            beta = ew.tile([P, 8, nt, 32], BF16, tag="beta")
            for y in range(2):
                s0, s1 = SLOT_OF_J[y], SLOT_OF_J[y + 2]
                nc.vector.tensor_tensor(
                    out=beta[:, 4 * y:4 * y + 4].rearrange("p a n i -> p (a n i)"), in0=gam[:, 4 * s0:4 * s0 + 4].rearrange("p a n i -> p (a n i)"),
                    in1=gam[:, 4 * s1:4 * s1 + 4].rearrange("p a n i -> p (a n i)"), op=ALU.mult,
                )
            tiles[k]["beta"] = beta
            tiles[k]["v"] = ew.tile([P, 16, nt, 32], BF16, tag="v", name="v")
            tiles[k]["z"] = ew.tile([P, nt, 16, 32], BF16, tag="z", name="z")
            tiles[k]["ring"] = ew.tile([P, 8, nt, 32], BF16, tag="ring", name="ring")

        def inner(k, q):
            ns = slice(2 * q, 2 * q + 2)
            nc.vector.scalar_tensor_tensor(
                out=tiles[k]["v"][:, 0:8, ns, :].rearrange("p b n i -> p b (n i)"), in0=tiles[k][("t", q)][:].rearrange("p b n i -> p b (n i)"),
                scalar=4.0 / 3.0, in1=tiles[k]["beta"][:, :, ns, :].rearrange("p b n i -> p b (n i)"), op0=ALU.subtract, op1=ALU.mult,
            )

        def inner_raw(k, q):
            ns = slice(2 * q, 2 * q + 2)
            nc.scalar.activation(
                out=tiles[k]["v"][:, 0:8, ns, :].rearrange("p b n i -> p b (n i)"), in_=tiles[k][("t", q)][:].rearrange("p b n i -> p b (n i)"), func=ACT.Identity, bias=-4.0 / 3.0, scale=1.0,
            )

        def inner_masked(k, un):
            n0, n1 = unit_tiles(k, un)
            v = tiles[k]["v"][:, 0:8, n0:n1, :].rearrange("p b n i -> p b (n i)")
            nc.vector.tensor_tensor(out=v, in0=v, in1=tiles[k]["beta"][:, :, n0:n1, :].rearrange("p b n i -> p b (n i)"), op=ALU.mult)

        def ring(k, q):
            ns = slice(2 * q, 2 * q + 2)
            nc.scalar.activation(
                out=tiles[k]["ring"][:, :, ns, :].rearrange("p b n i -> p b (n i)"), in_=tiles[k][("c", q)][:].rearrange("p b n i -> p b (n i)"), func=ACT.Copy, bias=0.0, scale=-1.0 / 12.0,
            )

        def inner_negated(k, un):
            n0, n1 = unit_tiles(k, un)
            v = tiles[k]["v"]
            nc.vector.tensor_scalar(
                out=v[:, 8:16, n0:n1, :].rearrange("p b n i -> p b (n i)"), in0=v[:, 0:8, n0:n1, :].rearrange("p b n i -> p b (n i)"),
                scalar1=-1.0, scalar2=None, op0=ALU.mult,
            )

        def ring_elsewhere(k, un):
            n0, n1 = unit_tiles(k, un)
            v4 = tiles[k]["v"][:, :, n0:n1, :].rearrange("p (e b) n i -> p e b (n i)", e=2)
            r4 = tiles[k]["ring"][:, :, n0:n1, :].rearrange("p b n i -> p b (n i)").unsqueeze(1).to_broadcast([P, 2, 8, 32 * (n1 - n0)])
            nc.vector.tensor_tensor(out=v4, in0=v4, in1=r4, op=ALU.max)

        def signed(k, un):
            n0, n1 = unit_tiles(k, un)
            nc.vector.tensor_tensor(
                out=tiles[k]["z"][:, n0:n1].rearrange("p n b i -> p b n i"), in0=tiles[k]["v"][:, :, n0:n1, :], in1=tiles[k]["gam"][:, :, n0:n1, :], op=ALU.mult,
            )


        def fill_z(k, q):
            z = tiles[k]["z"]
            t = psum.tile([P, 2, 2, P], F32, tag="z", bufs=2)
            for pos in range(2):
                for e in range(2):
                    nc.tensor.transpose(
                        t[:, pos, e, :], words(z[:, 2 * q + pos, 8 * e:8 * e + 8, :].rearrange("p b i -> p (b i)")), ident_f[:],
                    )
            tiles[k][("zt", q)] = t

        def copy_z(k, q):
            un = 0 if 2 * q < GROUPS[k][0] else 1
            n0, n1 = unit_tiles(k, un)
            if ("gz", un) not in tiles[k]:
                tiles[k][("gz", un)] = be.tile([P, 4 * P * (n1 - n0)], BF16, tag="gz", bufs=3, align_bytes=64, name="gz")
            first = (2 * q - n0) * 4 * P
            nc.scalar.copy(
                out=words(tiles[k][("gz", un)][:, first:first + 8 * P]).rearrange("p (n b e) -> p n b e", n=2, e=2),
                in_=tiles[k][("zt", q)][:].rearrange("p n e b -> p n b e"),
            )

        def halves(k, un):
            n0, n1 = unit_tiles(k, un)
            np = (n1 - n0) // 2
            gr = be.tile([P, np, 2, 8 * P], BF16, tag="gr", align_bytes=64)
            for g in range(2):
                nc.vector.tensor_scalar(
                    out=gr[:, :, g, :], in0=tiles[k][("gz", un)][:].rearrange("p (q w) -> p q w", q=np),
                    scalar1=(-4.0, 4.0)[g], scalar2=0.0, op0=ALU.mult, op1=ALU.max,
                )
            for i in range(np):
                tiles[k][("gr", n0 // 2 + i)] = gr[:, i]

        def halves_at_once(k, q):
            gr = be.tile([P, 2, 8 * P], BF16, tag="gr", align_bytes=64)
            zt = tiles[k][("zt", q)][:].rearrange("p n e b -> p (n e b)").bitcast(BF16).rearrange("p (n e b d) -> p n b e d", n=2, e=2, d=2)
            for g in range(2):
                for pos in range(2):
                    nc.vector.tensor_scalar(
                        out=gr[:, g, pos * 4 * P:(pos + 1) * 4 * P].rearrange("p (b e d) -> p b e d", e=2, d=2), in0=zt[:, pos],
                        scalar1=(-4.0, 4.0)[g], scalar2=0.0, op0=ALU.mult, op1=ALU.max,
                    )
            tiles[k][("gr", q)] = gr

        def quantise(k, q):
            f = 2 * P
            bcodes = be.tile([P, 2, f], U32, tag="bcodes", bufs=3, align_bytes=64)
            bscales = be.tile([P, 2, f], U8, tag="bscales", bufs=3, align_bytes=64)
            nc.vector.quantize_mx(
                out=bcodes[:].rearrange("p g w -> p (g w)").bitcast(FP8X4),
                scales=bscales[:].rearrange("p g w -> p (g w)"),
                in_=tiles[k][("gr", q)][:].rearrange("p g w -> p (g w)"),
            )
            tiles[k][("q", q)] = (bcodes, bscales)

        def multiply(k, q, h):
            bcodes, bscales = tiles[k][("q", q)]
            if h == 0:
                tiles[k][("mx", q)] = psum.tile([P, 2, 2 * P], F32, tag="mx", bufs=2, name="mx")
            for g in range(2):
                nc.tensor.matmul_mx(
                    out=tiles[k][("mx", q)][:, h, :],
                    lhsT=ccodes[:, g, h * P:(h + 1) * P].bitcast(FP8X4),
                    lhsT_scale=cscales[:, g, h * P:(h + 1) * P],
                    rhs=bcodes[:, g, :].bitcast(FP8X4),
                    rhs_scale=bscales[:, g, :],
                    start=(g == 0),
                    stop=(g == 1),
                )

        def scale_add(k, q, h):
            if h == 0:
                tiles[k][("t1", q)] = be.tile([P, 2, 2 * P], F32, tag="t1", bufs=3, name="t1")
            dst, src = tiles[k][("t1", q)][:, h, :], tiles[k][("mx", q)][:, h, :]
            if k == NG - 1 and h == 1:
                nc.vector.tensor_scalar(out=dst, in0=src, scalar1=scale[:, h:h + 1], scalar2=bias[:, h:h + 1], op0=ALU.mult, op1=ALU.add)
            else:
                nc.scalar.activation(out=dst, in_=src, func=ACT.Identity, bias=bias[:, h:h + 1], scale=scale[:, h:h + 1])

        def add_residual(k, q, pos):
            t1 = tiles[k][("t1", q)]
            if pos == 0:
                tiles[k][("ot", q)] = psum.tile([P, 2, O], F32, tag="ot", bufs=2, name="ot")
            ot = tiles[k][("ot", q)]
            nc.tensor.matmul(out=ot[:, pos, :], lhsT=xT[:, GSTART[k] + 2 * q + pos, :], rhs=rwT[:], start=True, stop=False)
            cols = slice(pos * P, (pos + 1) * P)
            nc.tensor.matmul(out=ot[:, pos, 0:P], lhsT=t1[:, 0, cols], rhs=ident_f[:], is_transpose=True, start=False, stop=False)
            nc.tensor.matmul(out=ot[:, pos, P:O], lhsT=t1[:, 1, cols], rhs=ident_f[:], is_transpose=True, start=False, stop=True)

        def store(k, q):
            osb = be.tile([P, 2, O], F32, tag="osb", bufs=4)
            if k == NG - 1:
                nc.scalar.copy(out=osb[:, 0, :], in_=tiles[k][("ot", q)][:, 0, :])
                nc.vector.tensor_copy(out=osb[:, 1, :], in_=tiles[k][("ot", q)][:, 1, :])
            else:
                nc.scalar.copy(out=osb[:], in_=tiles[k][("ot", q)][:])
            n0 = GSTART[k] + 2 * q
            nc.sync.dma_start(out=out_v[:, n0:n0 + 2, :], in_=osb[:])


        def whole(k, *steps):
            if exists(k):
                for step in steps:
                    step(k)

        def part(k, y, step):
            if exists(k):
                step(k, y)

        def unit(k, un, *steps):
            if exists(k) and un < len(GROUPS[k]):
                for step in steps:
                    step(k, un)

        def half(k, q, i, step):
            if exists(k) and q < tiles_of(k) // 2:
                step(k, q, i)

        def pair(k, q, step):
            if exists(k) and q < tiles_of(k) // 2:
                step(k, q)

        def unit_pair(k, un, i, step):
            if exists(k) and un < len(GROUPS[k]) and 2 * i < GROUPS[k][un]:
                step(k, sum(GROUPS[k][:un]) // 2 + i)

        def later_mask(k, i):
            if k > 2:
                part(k, i, mask)

        def copy_out(k, q):
            if k < NG - 1:
                copy_z(k, q)

        def halves_later(k, un):
            if k < NG - 1:
                halves(k, un)
            else:
                for q in range(sum(GROUPS[k][:un]) // 2, sum(GROUPS[k][:un + 1]) // 2):
                    halves_at_once(k, q)

        def both(k, q, step):
            half(k, q, 0, step)
            half(k, q, 1, step)

        for g in range(2):
            for i in range(4):
                mask(g, i)
        for k in range(-3, NG + 3):
            pair(k, 0, inner)
            pair(k, 0, ring)
            pair(k, 1, fill_inner)
            pair(k, 1, fill_ring)
            part(k + 1, 1, square)
            unit(k - 1, 0, halves_later)
            later_mask(k + 1, 0)
            later_mask(k + 1, 1)
            unit_pair(k - 1, 1, 0, copy_out)
            unit_pair(k - 1, 1, 1, copy_out)
            if k == 1:
                weights_finish()
            if k == NG - 1:
                inner_negated(k, 0)
            pair(k - 1, 0, quantise)
            if k == NG - 1:
                ring_elsewhere(k, 0)
            both(k - 1, 0, multiply)
            pair(k, 1, inner)
            pair(k, 1, ring)
            pair(k, 2, fill_inner)
            pair(k, 2, fill_ring)
            both(k - 2, 3, add_residual)
            later_mask(k + 1, 2)
            later_mask(k + 1, 3)
            part(k + 1, 0, square)
            both(k - 1, 0, scale_add)
            if k != NG - 1:
                unit(k, 0, inner_negated)
            if k == 0:
                near_masks(1)
            part(k + 1, 1, cube)
            unit(k - 1, 1, halves_later)
            pair(k, 2, inner_raw)
            pair(k, 2, ring)
            pair(k, 3, fill_inner)
            pair(k, 3, fill_ring)
            whole(k + 2, fold_1)
            if k == NG - 1:
                signed(k, 0)
                fill_z(k, 0)
            pair(k - 1, 1, quantise)
            both(k - 1, 1, multiply)
            if k != NG - 1:
                unit(k, 0, ring_elsewhere)
            pair(k - 1, 2, quantise)
            pair(k - 2, 3, store)
            whole(k + 3, transpose_x)
            both(k - 1, 2, multiply)
            pair(k, 3, inner_raw)
            pair(k, 3, ring)
            both(k - 1, 1, scale_add)
            both(k - 1, 0, add_residual)
            whole(k + 3, keep_xT)
            if k != NG - 1:
                unit(k, 0, signed)
            whole(k + 2, fold_2)
            pair(k - 1, 0, store)
            both(k - 1, 2, scale_add)
            if k != NG - 1:
                unit_pair(k, 0, 0, fill_z)
            both(k - 1, 1, add_residual)
            if exists(k) and tiles_of(k) == 8:
                inner_masked(k, 1)
            part(k + 1, 0, cube)
            unit(k, 1, inner_negated)
            unit_pair(k, 0, 0, copy_out)
            unit_pair(k, 0, 1, fill_z)
            pair(k + 1, 0, fill_inner)
            pair(k + 1, 0, fill_ring)
            pair(k - 1, 1, store)
            pair(k - 1, 3, quantise)
            unit(k, 1, ring_elsewhere)
            both(k - 1, 3, multiply)
            unit_pair(k, 0, 1, copy_out)
            whole(k + 2, fold_3)
            if k + 1 > 1:
                whole(k + 1, near_masks)
            both(k - 1, 3, scale_add)
            both(k - 1, 2, add_residual)
            unit(k, 1, signed)
            pair(k - 1, 2, store)
            unit_pair(k, 1, 0, fill_z)
            unit_pair(k, 1, 1, fill_z)
            if k == -1:
                for i in range(4):
                    mask(2, i)
            whole(k + 3, clamp)
            if k == -3:
                near_masks(0)
            if k == -3:
                nc.vector.tensor_copy(
                    out=ident_p[:].rearrange("p (a q l) -> p a q l", a=4, q=8), in_=ident_f[:].rearrange("p (q a l) -> p a q l", q=8, a=4),
                )
                weights_permute()
            if k == -1:
                weights_transpose()
            if k == 0:
                weights_leave_psum()
